import numpy as np
import ml_dtypes


def mxq(x, axis, fmt="e4m3"):
    dtype, down = {"e4m3": (ml_dtypes.float8_e4m3fn, 7), "e5m2": (ml_dtypes.float8_e5m2, 14)}[fmt]
    v = np.moveaxis(np.asarray(x, np.float32).astype(ml_dtypes.bfloat16).astype(np.float64), axis, -1)
    blocks = v.reshape(v.shape[:-1] + (-1, 32))
    amax = np.abs(blocks).max(-1, keepdims=True)
    byte = np.maximum(np.where(amax > 0, np.frexp(amax)[1] - 1 + 127, 0) - down, 1)
    scale = np.exp2(byte - 127.0)
    codes = (blocks / scale).astype(np.float32).astype(dtype).astype(np.float64)
    return np.moveaxis((codes * scale).reshape(v.shape), -1, axis)


WIDE = False


def mx_kscale(k):
    if not WIDE:
        return np.ones(k)
    levels = np.array([10, -10, 5, -5, 0])
    a = np.random.permutation(np.resize(levels, k // 512 * 4)).reshape(k // 512, 4)
    idx = np.arange(k)
    return np.exp2(a[idx // 512, idx % 128 // 32])


BF16 = ml_dtypes.bfloat16


def bf(x):
    return np.asarray(x, np.float32).astype(BF16)


def f64(x):
    return np.asarray(x).astype(np.float64)


E2M1 = np.array([0.0, 0.5, 1.0, 1.5, 2.0, 3.0, 4.0, 6.0, -0.0, -0.5, -1.0, -1.5, -2.0, -3.0, -4.0, -6.0])


def pack_weight(w, fmt):
    k, n = w.shape
    w = f64(bf(w)).reshape(k // 32, 32, n)
    amax = np.abs(w).max(1)
    if fmt == "e4m3":
        byte = np.frexp(amax)[1] - 1 + 127 - 7
    else:
        mant, ex = np.frexp(amax / 6.0)
        byte = np.where(mant > 0.5, ex, ex - 1) + 127
    byte = np.clip(np.where(amax > 0, byte, 1), 1, 254)
    scaled = (w * np.exp2(127.0 - byte)[:, None, :]).reshape(k, n).astype(np.float32)
    by_word = np.ascontiguousarray(scaled.reshape(k // 512, 128, 4, n).transpose(0, 1, 3, 2))
    if fmt == "e4m3":
        words = by_word.astype(ml_dtypes.float8_e4m3fn).view(np.uint8)
    else:
        c = by_word.astype(ml_dtypes.float4_e2m1fn).view(np.uint8) & 0xF
        words = c[..., 0::2] | (c[..., 1::2] << 4)
    return np.ascontiguousarray(words), np.ascontiguousarray(byte.astype(np.uint8).reshape(k // 512, 16, n))


def unpack_weight(words, scales, fmt):
    g, p, n, _ = words.shape
    if fmt == "e4m3":
        vals = np.ascontiguousarray(words).view(ml_dtypes.float8_e4m3fn).astype(np.float64)
    else:
        nib = np.empty((g, p, n, 4), np.uint8)
        nib[..., 0::2] = words & 0xF
        nib[..., 1::2] = words >> 4
        vals = E2M1[nib]
    vals = vals * np.repeat(np.exp2(scales.astype(np.float64) - 127.0), 8, axis=1)[..., None]
    return vals.transpose(0, 1, 3, 2).reshape(g * 512, n)


B, DIM, HID, LS = 4096, 128, 512, 3
DL = DIM * LS
O1 = DL
O2 = O1 + DL
O3 = O2 + DL
O4 = O3 + DIM
O5 = O4 + DIM
P = O5 + DIM


def elu(v):
    return np.where(v > 0.0, v, np.exp(np.minimum(v, 0.0)) - 1.0)


def sigmoid(v):
    return 1.0 / (1.0 + np.exp(-v))


def col_scale():
    return np.concatenate([np.full(DL, 0.5), np.full(DL, 1.0), np.full(DL, 2.5 / np.sqrt(LS)),
                           np.full(DIM, 0.5), np.full(DIM, 8.0), np.full(DIM, 2.5)])


def setup_inputs():
    t = mx_kscale(HID)
    cs = col_scale()
    x = bf(np.random.standard_normal((B, DIM)))
    cond = bf(np.random.standard_normal((B, DIM)))
    W1 = bf(np.random.standard_normal((DIM, HID)) / np.sqrt(DIM) * t)
    b1 = bf(np.random.standard_normal(HID) * 0.5 * t)
    W2_words, W2_scales = pack_weight(np.random.standard_normal((HID, P)) * 1.2 / np.sqrt(HID) * cs / t[:, None], "e4m3")
    b2 = bf(np.random.standard_normal(P) * 0.5 * cs)
    return {"x": x,
            "cond": cond,
            "W1": W1,
            "b1": b1,
            "W2_words": W2_words,
            "W2_scales": W2_scales,
            "b2": b2}


def reference(x, cond, W1, b1, W2_words, W2_scales, b2):
    x = f64(x)
    h = np.maximum(f64(cond) @ f64(W1) + f64(b1), 0.0)
    p = (mxq(h, 1, "e4m3") @ unpack_weight(W2_words, W2_scales, "e4m3")) + f64(b2)
    n = x.shape[0]
    mat1 = p[:, :O1].reshape(n, DIM, LS)
    bias1 = p[:, O1:O2].reshape(n, DIM, LS)
    mat2 = p[:, O2:O3].reshape(n, DIM, LS)
    bias2 = p[:, O3:O4]
    eps = p[:, O4:O5] / 10.0
    alpha = p[:, O5:] / 10.0
    z = x[:, :, None] * mat1 + bias1
    num = np.sum(elu(z) * mat2, axis=-1)
    den = np.sum(np.maximum(-mat1 * mat2, 0.0), axis=-1) + 1.0
    return np.exp(alpha) * (x + 0.8 * sigmoid(eps) * num / den) + bias2

@@ -1,0 +1,271 @@
+import math
+from contextlib import ExitStack
+
+import concourse.mybir as mybir
+from concourse.masks import make_identity
+
+F32 = mybir.dt.float32
+BF16 = mybir.dt.bfloat16
+I32 = mybir.dt.int32
+U32 = mybir.dt.uint32
+U8 = mybir.dt.uint8
+FP8X4 = mybir.dt.float8_e4m3fn_x4
+ACT = mybir.ActivationFunctionType
+ALU = mybir.AluOpType
+AXIS = mybir.AxisListType
+
+P = 128
+PACK = 4
+BATCH, DIM, HID, LS = 4096, 128, 512, 3
+P_COLS = 3 * DIM * LS + 3 * DIM
+COL_TILES = P_COLS // P
+C_TILES = DIM * LS // P
+MAT1, BIAS1, MAT2 = 0, C_TILES, 2 * C_TILES
+BIAS2, EPS, ALPHA = 3 * C_TILES, 3 * C_TILES + 1, 3 * C_TILES + 2
+SUBTILES = BATCH // P
+SUBS = 4
+BLOCK = SUBS * P
+BLOCKS = SUBTILES // SUBS
+GROUP_BLOCKS = 4
+GROUPS = BLOCKS // GROUP_BLOCKS
+GROUP = GROUP_BLOCKS * BLOCK
+
+FLOPS = 2 * BATCH * DIM * HID + 2 * BATCH * HID * P_COLS
+
+
+def tile_cn_pa_t_kernel(tc, x, cond, W1, b1, W2_words, W2_scales, b2, out):
+    nc = tc.nc
+    with ExitStack() as ctx:
+        const = ctx.enter_context(tc.tile_pool(name="const", bufs=1))
+        prep = ctx.enter_context(tc.tile_pool(name="prep", bufs=2))
+        work = ctx.enter_context(tc.tile_pool(name="work", bufs=3))
+        block_pool = ctx.enter_context(tc.tile_pool(name="block", bufs=2))
+        held = ctx.enter_context(tc.tile_pool(name="held", bufs=GROUP_BLOCKS + 2))
+        psum_mm = ctx.enter_context(tc.psum_pool(name="psum_mm", bufs=4))
+        psum_tr = ctx.enter_context(tc.psum_pool(name="psum_tr", bufs=2))
+        psum_tp = ctx.enter_context(tc.psum_pool(name="psum_tp", bufs=2))
+
+        cond_view = cond.rearrange("(p i) d -> p i d", i=SUBTILES)
+        x_view = x.rearrange("(p i) d -> p i d", i=SUBTILES)
+        out_view = out.rearrange("(p i) d -> p i d", i=SUBTILES)
+
+        ident_bf = const.tile([P, P], BF16)
+        make_identity(nc, ident_bf[:])
+        ident_f32 = const.tile([P, P], F32)
+        make_identity(nc, ident_f32[:])
+
+        cond_all = const.tile([P, SUBTILES, DIM], BF16)
+        x_all = const.tile([P, SUBTILES, DIM], BF16)
+
+        def load_block(blk):
+            subs = slice(blk * SUBS, (blk + 1) * SUBS)
+            nc.sync.dma_start(out=cond_all[:, subs, :], in_=cond_view[:, subs, :])
+            nc.sync.dma_start(out=x_all[:, subs, :], in_=x_view[:, subs, :])
+
+        load_block(0)
+
+        w1_rows = const.tile([P, HID], BF16)
+        nc.sync.dma_start(out=w1_rows[:], in_=W1)
+        w1_by_t = const.tile([P, PACK, P], BF16)
+        nc.vector.tensor_copy(out=w1_by_t[:], in_=w1_rows[:].rearrange("d (p t) -> d t p", t=PACK))
+        b1_bf = const.tile([P, PACK], BF16)
+        nc.sync.dma_start(out=b1_bf[:], in_=b1.rearrange("(p t) -> p t", t=PACK))
+        b1_col = const.tile([P, PACK], F32)
+        nc.vector.tensor_copy(out=b1_col[:], in_=b1_bf[:])
+
+        b2_rows = const.tile([P, P], BF16)
+        nc.vector.memset(b2_rows[:], 0.0)
+        nc.sync.dma_start(out=b2_rows[0:COL_TILES, :], in_=b2.rearrange("(r q) -> r q", q=P))
+        b2_ps = psum_tp.tile([P, P], BF16, tag="tp")
+        nc.tensor.transpose(b2_ps[:], b2_rows[:], ident_bf[:])
+        b2_col = const.tile([P, COL_TILES], F32)
+        nc.vector.tensor_copy(out=b2_col[:], in_=b2_ps[:, 0:COL_TILES])
+        half_eps_bias = const.tile([P, 1], F32)
+        nc.vector.tensor_scalar_mul(out=half_eps_bias[:], in0=b2_col[:, EPS : EPS + 1], scalar1=0.05)
+        alpha_bias = const.tile([P, 1], F32)
+        nc.vector.tensor_scalar_mul(out=alpha_bias[:], in0=b2_col[:, ALPHA : ALPHA + 1], scalar1=0.1)
+        one_col = const.tile([P, 1], F32)
+        nc.vector.memset(one_col[:], 1.0)
+        ln_04_col = const.tile([P, 1], F32)
+        nc.vector.tensor_scalar_mul(out=ln_04_col[:], in0=one_col[:], scalar1=math.log(0.4))
+
+        w2_scales = const.tile([P, P_COLS], U8, align_bytes=64)
+        nc.vector.memset(w2_scales[:].bitcast(I32), 0)
+        for quad in range(4):
+            nc.sync.dma_start(
+                out=w2_scales[32 * quad : 32 * quad + 4, :].bitcast(I32),
+                in_=W2_scales[0, 4 * quad : 4 * quad + 4, :].bitcast(I32),
+            )
+        w2_codes = const.tile([P, P_COLS], U32, align_bytes=64)
+        nc.sync.dma_start(
+            out=w2_codes[:].bitcast(I32),
+            in_=W2_words[0].rearrange("p n t -> p (n t)").bitcast(I32),
+        )
+        for blk in range(1, BLOCKS):
+            load_block(blk)
+
+        def transpose_rows(rows_of_sub, dest):
+            turned = psum_tp.tile([P, BLOCK], BF16, tag="tp")
+            for s in range(SUBS):
+                nc.tensor.transpose(turned[:, s * P : (s + 1) * P], rows_of_sub(s), ident_bf[:])
+            nc.scalar.copy(out=dest, in_=turned[:])
+
+        def prepare(blk):
+            first = blk * SUBS
+            cond_t = prep.tile([P, BLOCK], BF16)
+            transpose_rows(lambda s: cond_all[:, first + s, :], cond_t[:])
+
+            x_thrice = prep.tile([P, SUBS, DIM, LS], BF16)
+            nc.gpsimd.tensor_scalar(
+                out=x_thrice[:],
+                in0=x_all[:, first : first + SUBS, :].unsqueeze(3).to_broadcast([P, SUBS, DIM, LS]),
+                scalar1=1.0,
+                scalar2=0.0,
+                op0=ALU.mult,
+                op1=ALU.add,
+            )
+            x_cols = x_thrice[:].rearrange("p s d l -> p s (d l)")
+            x_by_c = prep.tile([P, C_TILES, BLOCK], BF16)
+            for j in range(C_TILES):
+                transpose_rows(lambda s: x_cols[:, s, j * P : (j + 1) * P], x_by_c[:, j, :])
+
+            h_rows = prep.tile([P, PACK, BLOCK], BF16)
+            for t in range(PACK):
+                h_ps = psum_mm.tile([P, BLOCK], F32, tag="mm")
+                nc.tensor.matmul(out=h_ps[:], lhsT=w1_by_t[:, t, :], rhs=cond_t[:], start=True, stop=True)
+                nc.scalar.activation(
+                    out=h_rows[:, t, :], in_=h_ps[:], func=ACT.Relu, bias=b1_col[:, t : t + 1], scale=1.0
+                )
+            h_grouped = prep.tile([P, BLOCK, PACK], BF16, align_bytes=64)
+            nc.vector.tensor_copy(
+                out=h_grouped[:].rearrange("p (c i) t -> p c t i", i=4),
+                in_=h_rows[:].rearrange("p t (c i) -> p c t i", i=4),
+            )
+            h_codes = prep.tile([P, BLOCK], U32, align_bytes=64)
+            h_scales = prep.tile([P, BLOCK], U8, align_bytes=64)
+            nc.vector.quantize_mx(
+                out=h_codes[:].bitcast(FP8X4),
+                scales=h_scales[:],
+                in_=h_grouped[:].rearrange("p b t -> p (b t)"),
+            )
+            return x_by_c, h_codes, h_scales
+
+        def subnet(col_tile, h_codes, h_scales):
+            cols = slice(col_tile * P, (col_tile + 1) * P)
+            p_ps = psum_mm.tile([P, BLOCK], F32, tag="mm")
+            nc.tensor.matmul_mx(
+                out=p_ps[:],
+                lhsT=w2_codes[:, cols].bitcast(FP8X4),
+                lhsT_scale=w2_scales[:, cols],
+                rhs=h_codes[:].bitcast(FP8X4),
+                rhs_scale=h_scales[:],
+                start=True,
+                stop=True,
+            )
+            return p_ps
+
+        def bias_of(col_tile):
+            return b2_col[:, col_tile : col_tile + 1]
+
+        def main(blk, prepared, num_grp, den_grp):
+            x_by_c, h_codes, h_scales = prepared
+            in_group = blk % GROUP_BLOCKS
+            terms = block_pool.tile([P, C_TILES, BLOCK], F32)
+            prods = block_pool.tile([P, C_TILES, BLOCK], F32)
+            for j in range(C_TILES):
+                mat2_ps = subnet(MAT2 + j, h_codes, h_scales)
+                mat2 = work.tile([P, BLOCK], F32)
+                nc.scalar.activation(out=mat2[:], in_=mat2_ps[:], func=ACT.Identity, bias=bias_of(MAT2 + j), scale=1.0)
+                mat1_ps = subnet(MAT1 + j, h_codes, h_scales)
+                xm = work.tile([P, BLOCK], F32)
+                nc.vector.scalar_tensor_tensor(
+                    out=xm[:], in0=mat1_ps[:], scalar=bias_of(MAT1 + j), in1=x_by_c[:, j, :], op0=ALU.add, op1=ALU.mult
+                )
+                nc.vector.scalar_tensor_tensor(
+                    out=prods[:, j, :], in0=mat1_ps[:], scalar=bias_of(MAT1 + j), in1=mat2[:], op0=ALU.add, op1=ALU.mult
+                )
+                bias1_ps = subnet(BIAS1 + j, h_codes, h_scales)
+                z = work.tile([P, BLOCK], F32)
+                nc.vector.scalar_tensor_tensor(
+                    out=z[:], in0=bias1_ps[:], scalar=bias_of(BIAS1 + j), in1=xm[:], op0=ALU.add, op1=ALU.add
+                )
+                ez = work.tile([P, BLOCK], F32)
+                nc.scalar.activation(out=ez[:], in_=z[:], func=ACT.Exp)
+                nc.gpsimd.tensor_scalar(out=ez[:], in0=ez[:], scalar1=-1.0, scalar2=0.0, op0=ALU.add, op1=ALU.min)
+                nc.vector.tensor_tensor(out=z[:], in0=z[:], in1=ez[:], op=ALU.max)
+                nc.gpsimd.tensor_tensor(out=terms[:, j, :], in0=z[:], in1=mat2[:], op=ALU.mult)
+
+            gate = held.tile([P, BLOCK], F32)
+            eps_ps = subnet(EPS, h_codes, h_scales)
+            nc.scalar.activation(out=gate[:], in_=eps_ps[:], func=ACT.Tanh, bias=half_eps_bias[:], scale=0.05)
+            gain = held.tile([P, BLOCK], F32)
+            alpha_ps = subnet(ALPHA, h_codes, h_scales)
+            nc.scalar.activation(out=gain[:], in_=alpha_ps[:], func=ACT.Exp, bias=alpha_bias[:], scale=0.1)
+            shift = held.tile([P, BLOCK], F32)
+            bias2_ps = subnet(BIAS2, h_codes, h_scales)
+            nc.scalar.activation(out=shift[:], in_=bias2_ps[:], func=ACT.Identity, bias=bias_of(BIAS2), scale=1.0)
+
+            relu_rows = block_pool.tile([P, SUBS, DIM * LS], F32)
+            for s in range(SUBS):
+                sub = slice(s * P, (s + 1) * P)
+                terms_t = psum_tr.tile([P, DIM * LS], F32, tag="tr")
+                for j in range(C_TILES):
+                    nc.tensor.transpose(terms_t[:, j * P : (j + 1) * P], terms[:, j, sub], ident_f32[:])
+                nc.vector.tensor_reduce(
+                    out=num_grp[:, in_group * BLOCK + s * P : in_group * BLOCK + (s + 1) * P],
+                    in_=terms_t[:].rearrange("p (d l) -> p d l", l=LS),
+                    axis=AXIS.X,
+                    op=ALU.add,
+                )
+                prods_t = psum_tr.tile([P, DIM * LS], F32, tag="tr")
+                for j in range(C_TILES):
+                    nc.tensor.transpose(prods_t[:, j * P : (j + 1) * P], prods[:, j, sub], ident_f32[:])
+                nc.scalar.activation(out=relu_rows[:, s, :], in_=prods_t[:], func=ACT.Relu, scale=-1.0)
+            by_l = relu_rows[:].rearrange("p s (d l) -> p (s d) l", l=LS)
+            den_cols = den_grp[:, in_group * BLOCK : (in_group + 1) * BLOCK]
+            nc.gpsimd.tensor_tensor(out=den_cols, in0=by_l[:, :, 0], in1=by_l[:, :, 1], op=ALU.add)
+            nc.gpsimd.tensor_tensor(out=den_cols, in0=den_cols, in1=by_l[:, :, 2], op=ALU.add)
+            return gate, gain, shift
+
+        def turn_back(rows):
+            turned = psum_tr.tile([P, BLOCK], F32, tag="tr")
+            for s in range(SUBS):
+                sub = slice(s * P, (s + 1) * P)
+                nc.tensor.transpose(turned[:, sub], rows[:, sub], ident_f32[:])
+            return turned
+
+        def finish_group(grp, num_grp, den_grp, held_tiles):
+            nc.scalar.activation(out=den_grp[:], in_=den_grp[:], func=ACT.Ln, bias=one_col[:], scale=1.0)
+            nc.scalar.activation(out=den_grp[:], in_=den_grp[:], func=ACT.Exp, bias=ln_04_col[:], scale=-1.0)
+            for in_group in range(GROUP_BLOCKS):
+                blk = grp * GROUP_BLOCKS + in_group
+                subs = slice(blk * SUBS, (blk + 1) * SUBS)
+                cols = slice(in_group * BLOCK, (in_group + 1) * BLOCK)
+                gate, gain, shift = held_tiles[in_group]
+                y = work.tile([P, BLOCK], F32)
+                nc.gpsimd.tensor_tensor(out=y[:], in0=num_grp[:, cols], in1=den_grp[:, cols], op=ALU.mult)
+                gate_t = turn_back(gate)
+                nc.vector.scalar_tensor_tensor(out=y[:], in0=gate_t[:], scalar=1.0, in1=y[:], op0=ALU.add, op1=ALU.mult)
+                nc.gpsimd.tensor_tensor(
+                    out=y[:], in0=y[:], in1=x_all[:, subs, :].rearrange("p s d -> p (s d)"), op=ALU.add
+                )
+                gain_t = turn_back(gain)
+                nc.vector.tensor_tensor(out=y[:], in0=gain_t[:], in1=y[:], op=ALU.mult)
+                shift_t = turn_back(shift)
+                result = work.tile([P, SUBS, DIM], F32)
+                nc.vector.tensor_tensor(
+                    out=result[:].rearrange("p s d -> p (s d)"), in0=shift_t[:], in1=y[:], op=ALU.add
+                )
+                nc.sync.dma_start(out=out_view[:, subs, :], in_=result[:])
+
+        prepared = prepare(0)
+        for grp in range(GROUPS):
+            num_grp = block_pool.tile([P, GROUP], F32)
+            den_grp = block_pool.tile([P, GROUP], F32)
+            held_tiles = []
+            for in_group in range(GROUP_BLOCKS):
+                blk = grp * GROUP_BLOCKS + in_group
+                following = prepare(blk + 1) if blk + 1 < BLOCKS else None
+                held_tiles.append(main(blk, prepared, num_grp, den_grp))
+                prepared = following
+            finish_group(grp, num_grp, den_grp, held_tiles)

@@ -26,7 +26,7 @@ SUBTILES = BATCH // P
 SUBS = 4
 BLOCK = SUBS * P
 BLOCKS = SUBTILES // SUBS
-GROUP_BLOCKS = 4
+GROUP_BLOCKS = 2
 GROUPS = BLOCKS // GROUP_BLOCKS
 GROUP = GROUP_BLOCKS * BLOCK
 
@@ -38,12 +38,12 @@ def tile_cn_pa_t_kernel(tc, x, cond, W1, b1, W2_words, W2_scales, b2, out):
     with ExitStack() as ctx:
         const = ctx.enter_context(tc.tile_pool(name="const", bufs=1))
         prep = ctx.enter_context(tc.tile_pool(name="prep", bufs=2))
-        work = ctx.enter_context(tc.tile_pool(name="work", bufs=3))
+        work = ctx.enter_context(tc.tile_pool(name="work", bufs=4))
         block_pool = ctx.enter_context(tc.tile_pool(name="block", bufs=2))
         held = ctx.enter_context(tc.tile_pool(name="held", bufs=GROUP_BLOCKS + 2))
         psum_mm = ctx.enter_context(tc.psum_pool(name="psum_mm", bufs=4))
-        psum_tr = ctx.enter_context(tc.psum_pool(name="psum_tr", bufs=2))
-        psum_tp = ctx.enter_context(tc.psum_pool(name="psum_tp", bufs=2))
+        psum_tr = ctx.enter_context(tc.psum_pool(name="psum_tr", bufs=3))
+        psum_tp = ctx.enter_context(tc.psum_pool(name="psum_tp", bufs=1))
 
         cond_view = cond.rearrange("(p i) d -> p i d", i=SUBTILES)
         x_view = x.rearrange("(p i) d -> p i d", i=SUBTILES)
@@ -116,13 +116,9 @@ def tile_cn_pa_t_kernel(tc, x, cond, W1, b1, W2_words, W2_scales, b2, out):
             transpose_rows(lambda s: cond_all[:, first + s, :], cond_t[:])
 
             x_thrice = prep.tile([P, SUBS, DIM, LS], BF16)
-            nc.gpsimd.tensor_scalar(
+            nc.vector.tensor_copy(
                 out=x_thrice[:],
-                in0=x_all[:, first : first + SUBS, :].unsqueeze(3).to_broadcast([P, SUBS, DIM, LS]),
-                scalar1=1.0,
-                scalar2=0.0,
-                op0=ALU.mult,
-                op1=ALU.add,
+                in_=x_all[:, first : first + SUBS, :].unsqueeze(3).to_broadcast([P, SUBS, DIM, LS]),
             )
             x_cols = x_thrice[:].rearrange("p s d l -> p s (d l)")
             x_by_c = prep.tile([P, C_TILES, BLOCK], BF16)
@@ -191,9 +187,23 @@ def tile_cn_pa_t_kernel(tc, x, cond, W1, b1, W2_words, W2_scales, b2, out):
                 )
                 ez = work.tile([P, BLOCK], F32)
                 nc.scalar.activation(out=ez[:], in_=z[:], func=ACT.Exp)
-                nc.gpsimd.tensor_scalar(out=ez[:], in0=ez[:], scalar1=-1.0, scalar2=0.0, op0=ALU.add, op1=ALU.min)
+                nc.vector.tensor_scalar(out=ez[:], in0=ez[:], scalar1=-1.0, scalar2=0.0, op0=ALU.add, op1=ALU.min)
                 nc.vector.tensor_tensor(out=z[:], in0=z[:], in1=ez[:], op=ALU.max)
                 nc.gpsimd.tensor_tensor(out=terms[:, j, :], in0=z[:], in1=mat2[:], op=ALU.mult)
+
+            relu_rows = block_pool.tile([P, SUBS, DIM * LS], F32)
+            for s in range(SUBS):
+                prods_t = psum_tr.tile([P, DIM * LS], F32, tag="tr")
+                for j in range(C_TILES):
+                    nc.tensor.transpose(prods_t[:, j * P : (j + 1) * P], prods[:, j, s * P : (s + 1) * P], ident_f32[:])
+                nc.scalar.activation(out=relu_rows[:, s, :], in_=prods_t[:], func=ACT.Relu, scale=-1.0)
+            by_l = relu_rows[:].rearrange("p s (d l) -> p (s d) l", l=LS)
+            den_cols = den_grp[:, in_group * BLOCK : (in_group + 1) * BLOCK]
+            nc.gpsimd.tensor_tensor(out=den_cols, in0=by_l[:, :, 0], in1=by_l[:, :, 1], op=ALU.add)
+            nc.gpsimd.tensor_tensor(out=den_cols, in0=den_cols, in1=by_l[:, :, 2], op=ALU.add)
+            if in_group == GROUP_BLOCKS - 1:
+                nc.scalar.activation(out=den_grp[:], in_=den_grp[:], func=ACT.Ln, bias=one_col[:], scale=1.0)
+                nc.scalar.activation(out=den_grp[:], in_=den_grp[:], func=ACT.Exp, bias=ln_04_col[:], scale=-1.0)
 
             gate = held.tile([P, BLOCK], F32)
             eps_ps = subnet(EPS, h_codes, h_scales)
@@ -205,26 +215,16 @@ def tile_cn_pa_t_kernel(tc, x, cond, W1, b1, W2_words, W2_scales, b2, out):
             bias2_ps = subnet(BIAS2, h_codes, h_scales)
             nc.scalar.activation(out=shift[:], in_=bias2_ps[:], func=ACT.Identity, bias=bias_of(BIAS2), scale=1.0)
 
-            relu_rows = block_pool.tile([P, SUBS, DIM * LS], F32)
             for s in range(SUBS):
-                sub = slice(s * P, (s + 1) * P)
                 terms_t = psum_tr.tile([P, DIM * LS], F32, tag="tr")
                 for j in range(C_TILES):
-                    nc.tensor.transpose(terms_t[:, j * P : (j + 1) * P], terms[:, j, sub], ident_f32[:])
+                    nc.tensor.transpose(terms_t[:, j * P : (j + 1) * P], terms[:, j, s * P : (s + 1) * P], ident_f32[:])
                 nc.vector.tensor_reduce(
                     out=num_grp[:, in_group * BLOCK + s * P : in_group * BLOCK + (s + 1) * P],
                     in_=terms_t[:].rearrange("p (d l) -> p d l", l=LS),
                     axis=AXIS.X,
                     op=ALU.add,
                 )
-                prods_t = psum_tr.tile([P, DIM * LS], F32, tag="tr")
-                for j in range(C_TILES):
-                    nc.tensor.transpose(prods_t[:, j * P : (j + 1) * P], prods[:, j, sub], ident_f32[:])
-                nc.scalar.activation(out=relu_rows[:, s, :], in_=prods_t[:], func=ACT.Relu, scale=-1.0)
-            by_l = relu_rows[:].rearrange("p s (d l) -> p (s d) l", l=LS)
-            den_cols = den_grp[:, in_group * BLOCK : (in_group + 1) * BLOCK]
-            nc.gpsimd.tensor_tensor(out=den_cols, in0=by_l[:, :, 0], in1=by_l[:, :, 1], op=ALU.add)
-            nc.gpsimd.tensor_tensor(out=den_cols, in0=den_cols, in1=by_l[:, :, 2], op=ALU.add)
             return gate, gain, shift
 
         def turn_back(rows):
@@ -235,18 +235,17 @@ def tile_cn_pa_t_kernel(tc, x, cond, W1, b1, W2_words, W2_scales, b2, out):
             return turned
 
         def finish_group(grp, num_grp, den_grp, held_tiles):
-            nc.scalar.activation(out=den_grp[:], in_=den_grp[:], func=ACT.Ln, bias=one_col[:], scale=1.0)
-            nc.scalar.activation(out=den_grp[:], in_=den_grp[:], func=ACT.Exp, bias=ln_04_col[:], scale=-1.0)
+            helper = nc.vector if grp == GROUPS - 1 else nc.gpsimd
             for in_group in range(GROUP_BLOCKS):
                 blk = grp * GROUP_BLOCKS + in_group
                 subs = slice(blk * SUBS, (blk + 1) * SUBS)
                 cols = slice(in_group * BLOCK, (in_group + 1) * BLOCK)
                 gate, gain, shift = held_tiles[in_group]
                 y = work.tile([P, BLOCK], F32)
-                nc.gpsimd.tensor_tensor(out=y[:], in0=num_grp[:, cols], in1=den_grp[:, cols], op=ALU.mult)
+                helper.tensor_tensor(out=y[:], in0=num_grp[:, cols], in1=den_grp[:, cols], op=ALU.mult)
                 gate_t = turn_back(gate)
                 nc.vector.scalar_tensor_tensor(out=y[:], in0=gate_t[:], scalar=1.0, in1=y[:], op0=ALU.add, op1=ALU.mult)
-                nc.gpsimd.tensor_tensor(
+                helper.tensor_tensor(
                     out=y[:], in0=y[:], in1=x_all[:, subs, :].rearrange("p s d -> p (s d)"), op=ALU.add
                 )
                 gain_t = turn_back(gain)

@@ -26,7 +26,7 @@ SUBTILES = BATCH // P
 SUBS = 4
 BLOCK = SUBS * P
 BLOCKS = SUBTILES // SUBS
-GROUP_BLOCKS = 2
+GROUP_BLOCKS = 4
 GROUPS = BLOCKS // GROUP_BLOCKS
 GROUP = GROUP_BLOCKS * BLOCK
 
@@ -40,7 +40,7 @@ def tile_cn_pa_t_kernel(tc, x, cond, W1, b1, W2_words, W2_scales, b2, out):
         prep = ctx.enter_context(tc.tile_pool(name="prep", bufs=2))
         work = ctx.enter_context(tc.tile_pool(name="work", bufs=4))
         block_pool = ctx.enter_context(tc.tile_pool(name="block", bufs=2))
-        held = ctx.enter_context(tc.tile_pool(name="held", bufs=GROUP_BLOCKS + 2))
+        held = ctx.enter_context(tc.tile_pool(name="held", bufs=GROUP_BLOCKS + 3))
         psum_mm = ctx.enter_context(tc.psum_pool(name="psum_mm", bufs=4))
         psum_tr = ctx.enter_context(tc.psum_pool(name="psum_tr", bufs=3))
         psum_tp = ctx.enter_context(tc.psum_pool(name="psum_tp", bufs=1))
@@ -115,16 +115,6 @@ def tile_cn_pa_t_kernel(tc, x, cond, W1, b1, W2_words, W2_scales, b2, out):
             cond_t = prep.tile([P, BLOCK], BF16)
             transpose_rows(lambda s: cond_all[:, first + s, :], cond_t[:])
 
-            x_thrice = prep.tile([P, SUBS, DIM, LS], BF16)
-            nc.vector.tensor_copy(
-                out=x_thrice[:],
-                in_=x_all[:, first : first + SUBS, :].unsqueeze(3).to_broadcast([P, SUBS, DIM, LS]),
-            )
-            x_cols = x_thrice[:].rearrange("p s d l -> p s (d l)")
-            x_by_c = prep.tile([P, C_TILES, BLOCK], BF16)
-            for j in range(C_TILES):
-                transpose_rows(lambda s: x_cols[:, s, j * P : (j + 1) * P], x_by_c[:, j, :])
-
             h_rows = prep.tile([P, PACK, BLOCK], BF16)
             for t in range(PACK):
                 h_ps = psum_mm.tile([P, BLOCK], F32, tag="mm")
@@ -144,6 +134,16 @@ def tile_cn_pa_t_kernel(tc, x, cond, W1, b1, W2_words, W2_scales, b2, out):
                 scales=h_scales[:],
                 in_=h_grouped[:].rearrange("p b t -> p (b t)"),
             )
+
+            x_thrice = prep.tile([P, SUBS, DIM, LS], BF16)
+            nc.vector.tensor_copy(
+                out=x_thrice[:],
+                in_=x_all[:, first : first + SUBS, :].unsqueeze(3).to_broadcast([P, SUBS, DIM, LS]),
+            )
+            x_cols = x_thrice[:].rearrange("p s d l -> p s (d l)")
+            x_by_c = prep.tile([P, C_TILES, BLOCK], BF16)
+            for j in range(C_TILES):
+                transpose_rows(lambda s: x_cols[:, s, j * P : (j + 1) * P], x_by_c[:, j, :])
             return x_by_c, h_codes, h_scales
 
         def subnet(col_tile, h_codes, h_scales):
@@ -163,9 +163,8 @@ def tile_cn_pa_t_kernel(tc, x, cond, W1, b1, W2_words, W2_scales, b2, out):
         def bias_of(col_tile):
             return b2_col[:, col_tile : col_tile + 1]
 
-        def main(blk, prepared, num_grp, den_grp):
+        def column_tiles(prepared):
             x_by_c, h_codes, h_scales = prepared
-            in_group = blk % GROUP_BLOCKS
             terms = block_pool.tile([P, C_TILES, BLOCK], F32)
             prods = block_pool.tile([P, C_TILES, BLOCK], F32)
             for j in range(C_TILES):
@@ -191,6 +190,20 @@ def tile_cn_pa_t_kernel(tc, x, cond, W1, b1, W2_words, W2_scales, b2, out):
                 nc.vector.tensor_tensor(out=z[:], in0=z[:], in1=ez[:], op=ALU.max)
                 nc.gpsimd.tensor_tensor(out=terms[:, j, :], in0=z[:], in1=mat2[:], op=ALU.mult)
 
+            gate = held.tile([P, BLOCK], F32)
+            eps_ps = subnet(EPS, h_codes, h_scales)
+            nc.scalar.activation(out=gate[:], in_=eps_ps[:], func=ACT.Tanh, bias=half_eps_bias[:], scale=0.05)
+            gain = held.tile([P, BLOCK], F32)
+            alpha_ps = subnet(ALPHA, h_codes, h_scales)
+            nc.scalar.activation(out=gain[:], in_=alpha_ps[:], func=ACT.Exp, bias=alpha_bias[:], scale=0.1)
+            shift = held.tile([P, BLOCK], F32)
+            bias2_ps = subnet(BIAS2, h_codes, h_scales)
+            nc.scalar.activation(out=shift[:], in_=bias2_ps[:], func=ACT.Identity, bias=bias_of(BIAS2), scale=1.0)
+
+            return terms, prods, gate, gain, shift
+
+        def sums_over_l(blk, terms, prods, num_grp, den_grp):
+            in_group = blk % GROUP_BLOCKS
             relu_rows = block_pool.tile([P, SUBS, DIM * LS], F32)
             for s in range(SUBS):
                 prods_t = psum_tr.tile([P, DIM * LS], F32, tag="tr")
@@ -205,16 +218,6 @@ def tile_cn_pa_t_kernel(tc, x, cond, W1, b1, W2_words, W2_scales, b2, out):
                 nc.scalar.activation(out=den_grp[:], in_=den_grp[:], func=ACT.Ln, bias=one_col[:], scale=1.0)
                 nc.scalar.activation(out=den_grp[:], in_=den_grp[:], func=ACT.Exp, bias=ln_04_col[:], scale=-1.0)
 
-            gate = held.tile([P, BLOCK], F32)
-            eps_ps = subnet(EPS, h_codes, h_scales)
-            nc.scalar.activation(out=gate[:], in_=eps_ps[:], func=ACT.Tanh, bias=half_eps_bias[:], scale=0.05)
-            gain = held.tile([P, BLOCK], F32)
-            alpha_ps = subnet(ALPHA, h_codes, h_scales)
-            nc.scalar.activation(out=gain[:], in_=alpha_ps[:], func=ACT.Exp, bias=alpha_bias[:], scale=0.1)
-            shift = held.tile([P, BLOCK], F32)
-            bias2_ps = subnet(BIAS2, h_codes, h_scales)
-            nc.scalar.activation(out=shift[:], in_=bias2_ps[:], func=ACT.Identity, bias=bias_of(BIAS2), scale=1.0)
-
             for s in range(SUBS):
                 terms_t = psum_tr.tile([P, DIM * LS], F32, tag="tr")
                 for j in range(C_TILES):
@@ -225,7 +228,6 @@ def tile_cn_pa_t_kernel(tc, x, cond, W1, b1, W2_words, W2_scales, b2, out):
                     axis=AXIS.X,
                     op=ALU.add,
                 )
-            return gate, gain, shift
 
         def turn_back(rows):
             turned = psum_tr.tile([P, BLOCK], F32, tag="tr")
@@ -257,14 +259,24 @@ def tile_cn_pa_t_kernel(tc, x, cond, W1, b1, W2_words, W2_scales, b2, out):
                 )
                 nc.sync.dma_start(out=out_view[:, subs, :], in_=result[:])
 
-        prepared = prepare(0)
-        for grp in range(GROUPS):
-            num_grp = block_pool.tile([P, GROUP], F32)
-            den_grp = block_pool.tile([P, GROUP], F32)
-            held_tiles = []
-            for in_group in range(GROUP_BLOCKS):
-                blk = grp * GROUP_BLOCKS + in_group
-                following = prepare(blk + 1) if blk + 1 < BLOCKS else None
-                held_tiles.append(main(blk, prepared, num_grp, den_grp))
-                prepared = following
-            finish_group(grp, num_grp, den_grp, held_tiles)
+        prepared = [prepare(0)]
+        tiles = []
+        groups = []
+        for step in range(BLOCKS + 1):
+            if step < BLOCKS:
+                tiles.append(column_tiles(prepared[step]))
+            if step >= 1:
+                blk = step - 1
+                if blk % GROUP_BLOCKS == 0:
+                    num_grp = block_pool.tile([P, GROUP], F32)
+                    den_grp = block_pool.tile([P, GROUP], F32)
+                    groups.append((num_grp, den_grp))
+                num_grp, den_grp = groups[blk // GROUP_BLOCKS]
+                sums_over_l(blk, tiles[blk][0], tiles[blk][1], num_grp, den_grp)
+                if blk % GROUP_BLOCKS == GROUP_BLOCKS - 1:
+                    first = blk - GROUP_BLOCKS + 1
+                    finish_group(blk // GROUP_BLOCKS, num_grp, den_grp, [t[2:] for t in tiles[first : blk + 1]])
+            if step == 0:
+                prepared.append(prepare(1))
+            if step + 2 < BLOCKS:
+                prepared.append(prepare(step + 2))

@@ -40,7 +40,7 @@ def tile_cn_pa_t_kernel(tc, x, cond, W1, b1, W2_words, W2_scales, b2, out):
         prep = ctx.enter_context(tc.tile_pool(name="prep", bufs=2))
         work = ctx.enter_context(tc.tile_pool(name="work", bufs=4))
         block_pool = ctx.enter_context(tc.tile_pool(name="block", bufs=2))
-        held = ctx.enter_context(tc.tile_pool(name="held", bufs=GROUP_BLOCKS + 3))
+        held = ctx.enter_context(tc.tile_pool(name="held", bufs=3))
         psum_mm = ctx.enter_context(tc.psum_pool(name="psum_mm", bufs=4))
         psum_tr = ctx.enter_context(tc.psum_pool(name="psum_tr", bufs=3))
         psum_tp = ctx.enter_context(tc.psum_pool(name="psum_tp", bufs=1))
@@ -48,6 +48,7 @@ def tile_cn_pa_t_kernel(tc, x, cond, W1, b1, W2_words, W2_scales, b2, out):
         cond_view = cond.rearrange("(p i) d -> p i d", i=SUBTILES)
         x_view = x.rearrange("(p i) d -> p i d", i=SUBTILES)
         out_view = out.rearrange("(p i) d -> p i d", i=SUBTILES)
+        scratch = out.rearrange("(p i) d -> p (i d)", i=SUBTILES)[:, BATCH * DIM // P // 2 :]
 
         ident_bf = const.tile([P, P], BF16)
         make_identity(nc, ident_bf[:])
@@ -101,8 +102,6 @@ def tile_cn_pa_t_kernel(tc, x, cond, W1, b1, W2_words, W2_scales, b2, out):
             out=w2_codes[:].bitcast(I32),
             in_=W2_words[0].rearrange("p n t -> p (n t)").bitcast(I32),
         )
-        for blk in range(1, BLOCKS):
-            load_block(blk)
 
         def transpose_rows(rows_of_sub, dest):
             turned = psum_tp.tile([P, BLOCK], BF16, tag="tp")
@@ -112,6 +111,8 @@ def tile_cn_pa_t_kernel(tc, x, cond, W1, b1, W2_words, W2_scales, b2, out):
 
         def prepare(blk):
             first = blk * SUBS
+            if blk + 1 < BLOCKS:
+                load_block(blk + 1)
             cond_t = prep.tile([P, BLOCK], BF16)
             transpose_rows(lambda s: cond_all[:, first + s, :], cond_t[:])
 
@@ -135,15 +136,23 @@ def tile_cn_pa_t_kernel(tc, x, cond, W1, b1, W2_words, W2_scales, b2, out):
                 in_=h_grouped[:].rearrange("p b t -> p (b t)"),
             )
 
-            x_thrice = prep.tile([P, SUBS, DIM, LS], BF16)
-            nc.vector.tensor_copy(
-                out=x_thrice[:],
-                in_=x_all[:, first : first + SUBS, :].unsqueeze(3).to_broadcast([P, SUBS, DIM, LS]),
-            )
-            x_cols = x_thrice[:].rearrange("p s d l -> p s (d l)")
+            x_t = prep.tile([P, BLOCK], BF16)
+            transpose_rows(lambda s: x_all[:, first + s, :], x_t[:])
+            parked = scratch[:, blk * (BLOCK // 2) : (blk + 1) * (BLOCK // 2)]
+            nc.sync.dma_start(out=parked, in_=x_t[:].bitcast(F32))
             x_by_c = prep.tile([P, C_TILES, BLOCK], BF16)
             for j in range(C_TILES):
-                transpose_rows(lambda s: x_cols[:, s, j * P : (j + 1) * P], x_by_c[:, j, :])
+                head = (-j * P) % LS
+                whole = (P - head) // LS
+                tail = P - head - whole * LS
+                feature = (j * P + head) // LS
+                pieces = [(0, feature - 1, 1, head), (head, feature, whole, LS), (P - tail, feature + whole, 1, tail)]
+                for row, d, features, copies in pieces:
+                    if copies > 0:
+                        nc.sync.dma_start(
+                            out=x_by_c[row : row + features * copies, j, :].bitcast(F32),
+                            in_=parked[d : d + features, :].unsqueeze(1).to_broadcast([features, copies, BLOCK // 2]),
+                        )
             return x_by_c, h_codes, h_scales
 
         def subnet(col_tile, h_codes, h_scales):
@@ -202,33 +211,6 @@ def tile_cn_pa_t_kernel(tc, x, cond, W1, b1, W2_words, W2_scales, b2, out):
 
             return terms, prods, gate, gain, shift
 
-        def sums_over_l(blk, terms, prods, num_grp, den_grp):
-            in_group = blk % GROUP_BLOCKS
-            relu_rows = block_pool.tile([P, SUBS, DIM * LS], F32)
-            for s in range(SUBS):
-                prods_t = psum_tr.tile([P, DIM * LS], F32, tag="tr")
-                for j in range(C_TILES):
-                    nc.tensor.transpose(prods_t[:, j * P : (j + 1) * P], prods[:, j, s * P : (s + 1) * P], ident_f32[:])
-                nc.scalar.activation(out=relu_rows[:, s, :], in_=prods_t[:], func=ACT.Relu, scale=-1.0)
-            by_l = relu_rows[:].rearrange("p s (d l) -> p (s d) l", l=LS)
-            den_cols = den_grp[:, in_group * BLOCK : (in_group + 1) * BLOCK]
-            nc.gpsimd.tensor_tensor(out=den_cols, in0=by_l[:, :, 0], in1=by_l[:, :, 1], op=ALU.add)
-            nc.gpsimd.tensor_tensor(out=den_cols, in0=den_cols, in1=by_l[:, :, 2], op=ALU.add)
-            if in_group == GROUP_BLOCKS - 1:
-                nc.scalar.activation(out=den_grp[:], in_=den_grp[:], func=ACT.Ln, bias=one_col[:], scale=1.0)
-                nc.scalar.activation(out=den_grp[:], in_=den_grp[:], func=ACT.Exp, bias=ln_04_col[:], scale=-1.0)
-
-            for s in range(SUBS):
-                terms_t = psum_tr.tile([P, DIM * LS], F32, tag="tr")
-                for j in range(C_TILES):
-                    nc.tensor.transpose(terms_t[:, j * P : (j + 1) * P], terms[:, j, s * P : (s + 1) * P], ident_f32[:])
-                nc.vector.tensor_reduce(
-                    out=num_grp[:, in_group * BLOCK + s * P : in_group * BLOCK + (s + 1) * P],
-                    in_=terms_t[:].rearrange("p (d l) -> p d l", l=LS),
-                    axis=AXIS.X,
-                    op=ALU.add,
-                )
-
         def turn_back(rows):
             turned = psum_tr.tile([P, BLOCK], F32, tag="tr")
             for s in range(SUBS):
@@ -236,46 +218,72 @@ def tile_cn_pa_t_kernel(tc, x, cond, W1, b1, W2_words, W2_scales, b2, out):
                 nc.tensor.transpose(turned[:, sub], rows[:, sub], ident_f32[:])
             return turned
 
-        def finish_group(grp, num_grp, den_grp, held_tiles):
+        def sums_over_l(blk, column_results, den_grp, scaled_grp, offset_grp):
+            terms, prods, gate, gain, shift = column_results
+            in_group = blk % GROUP_BLOCKS
+            cols = slice(in_group * BLOCK, (in_group + 1) * BLOCK)
+            relu_rows = block_pool.tile([P, SUBS, DIM * LS], F32)
+            for s in range(SUBS):
+                prods_t = psum_tr.tile([P, DIM * LS], F32, tag="tr")
+                for j in range(C_TILES):
+                    nc.tensor.transpose(prods_t[:, j * P : (j + 1) * P], prods[:, j, s * P : (s + 1) * P], ident_f32[:])
+                nc.scalar.activation(out=relu_rows[:, s, :], in_=prods_t[:], func=ACT.Relu, scale=-1.0)
+            by_l = relu_rows[:].rearrange("p s (d l) -> p (s d) l", l=LS)
+            den_cols = den_grp[:, cols]
+            nc.gpsimd.tensor_tensor(out=den_cols, in0=by_l[:, :, 0], in1=by_l[:, :, 1], op=ALU.add)
+            nc.gpsimd.tensor_tensor(out=den_cols, in0=den_cols, in1=by_l[:, :, 2], op=ALU.add)
+            if in_group == GROUP_BLOCKS - 1:
+                nc.scalar.activation(out=den_grp[:], in_=den_grp[:], func=ACT.Ln, bias=one_col[:], scale=1.0)
+                nc.scalar.activation(out=den_grp[:], in_=den_grp[:], func=ACT.Exp, bias=ln_04_col[:], scale=-1.0)
+
+            num = block_pool.tile([P, BLOCK], F32)
+            for s in range(SUBS):
+                terms_t = psum_tr.tile([P, DIM * LS], F32, tag="tr")
+                for j in range(C_TILES):
+                    nc.tensor.transpose(terms_t[:, j * P : (j + 1) * P], terms[:, j, s * P : (s + 1) * P], ident_f32[:])
+                nc.vector.tensor_reduce(
+                    out=num[:, s * P : (s + 1) * P],
+                    in_=terms_t[:].rearrange("p (d l) -> p d l", l=LS),
+                    axis=AXIS.X,
+                    op=ALU.add,
+                )
+            scaled = scaled_grp[:, cols]
+            offset = offset_grp[:, cols]
+            gate_t = turn_back(gate)
+            nc.vector.scalar_tensor_tensor(out=scaled, in0=gate_t[:], scalar=1.0, in1=num[:], op0=ALU.add, op1=ALU.mult)
+            gain_t = turn_back(gain)
+            nc.vector.tensor_tensor(out=scaled, in0=gain_t[:], in1=scaled, op=ALU.mult)
+            x_rows = x_all[:, blk * SUBS : (blk + 1) * SUBS, :].rearrange("p s d -> p (s d)")
+            nc.vector.tensor_tensor(out=offset, in0=gain_t[:], in1=x_rows, op=ALU.mult)
+            shift_t = turn_back(shift)
+            nc.vector.tensor_tensor(out=offset, in0=shift_t[:], in1=offset, op=ALU.add)
+
+        def finish_group(grp, den_grp, scaled_grp, offset_grp):
             helper = nc.vector if grp == GROUPS - 1 else nc.gpsimd
             for in_group in range(GROUP_BLOCKS):
                 blk = grp * GROUP_BLOCKS + in_group
-                subs = slice(blk * SUBS, (blk + 1) * SUBS)
                 cols = slice(in_group * BLOCK, (in_group + 1) * BLOCK)
-                gate, gain, shift = held_tiles[in_group]
-                y = work.tile([P, BLOCK], F32)
-                helper.tensor_tensor(out=y[:], in0=num_grp[:, cols], in1=den_grp[:, cols], op=ALU.mult)
-                gate_t = turn_back(gate)
-                nc.vector.scalar_tensor_tensor(out=y[:], in0=gate_t[:], scalar=1.0, in1=y[:], op0=ALU.add, op1=ALU.mult)
-                helper.tensor_tensor(
-                    out=y[:], in0=y[:], in1=x_all[:, subs, :].rearrange("p s d -> p (s d)"), op=ALU.add
-                )
-                gain_t = turn_back(gain)
-                nc.vector.tensor_tensor(out=y[:], in0=gain_t[:], in1=y[:], op=ALU.mult)
-                shift_t = turn_back(shift)
+                helper.tensor_tensor(out=scaled_grp[:, cols], in0=scaled_grp[:, cols], in1=den_grp[:, cols], op=ALU.mult)
                 result = work.tile([P, SUBS, DIM], F32)
-                nc.vector.tensor_tensor(
-                    out=result[:].rearrange("p s d -> p (s d)"), in0=shift_t[:], in1=y[:], op=ALU.add
+                helper.tensor_tensor(
+                    out=result[:].rearrange("p s d -> p (s d)"), in0=scaled_grp[:, cols], in1=offset_grp[:, cols], op=ALU.add
                 )
-                nc.sync.dma_start(out=out_view[:, subs, :], in_=result[:])
+                nc.sync.dma_start(out=out_view[:, blk * SUBS : (blk + 1) * SUBS, :], in_=result[:])
 
         prepared = [prepare(0)]
         tiles = []
-        groups = []
         for step in range(BLOCKS + 1):
             if step < BLOCKS:
                 tiles.append(column_tiles(prepared[step]))
             if step >= 1:
                 blk = step - 1
                 if blk % GROUP_BLOCKS == 0:
-                    num_grp = block_pool.tile([P, GROUP], F32)
                     den_grp = block_pool.tile([P, GROUP], F32)
-                    groups.append((num_grp, den_grp))
-                num_grp, den_grp = groups[blk // GROUP_BLOCKS]
-                sums_over_l(blk, tiles[blk][0], tiles[blk][1], num_grp, den_grp)
+                    scaled_grp = block_pool.tile([P, GROUP], F32)
+                    offset_grp = block_pool.tile([P, GROUP], F32)
+                sums_over_l(blk, tiles[blk], den_grp, scaled_grp, offset_grp)
                 if blk % GROUP_BLOCKS == GROUP_BLOCKS - 1:
-                    first = blk - GROUP_BLOCKS + 1
-                    finish_group(blk // GROUP_BLOCKS, num_grp, den_grp, [t[2:] for t in tiles[first : blk + 1]])
+                    finish_group(blk // GROUP_BLOCKS, den_grp, scaled_grp, offset_grp)
             if step == 0:
                 prepared.append(prepare(1))
             if step + 2 < BLOCKS:

@@ -12,23 +12,19 @@ U8 = mybir.dt.uint8
 FP8X4 = mybir.dt.float8_e4m3fn_x4
 ACT = mybir.ActivationFunctionType
 ALU = mybir.AluOpType
-AXIS = mybir.AxisListType
 
 P = 128
 PACK = 4
 BATCH, DIM, HID, LS = 4096, 128, 512, 3
-P_COLS = 3 * DIM * LS + 3 * DIM
+DL = DIM * LS
+P_COLS = 3 * DL + 3 * DIM
 COL_TILES = P_COLS // P
-C_TILES = DIM * LS // P
-MAT1, BIAS1, MAT2 = 0, C_TILES, 2 * C_TILES
-BIAS2, EPS, ALPHA = 3 * C_TILES, 3 * C_TILES + 1, 3 * C_TILES + 2
+MAT1, BIAS1, MAT2 = 0, LS, 2 * LS
+BIAS2, EPS, ALPHA = 3 * LS, 3 * LS + 1, 3 * LS + 2
 SUBTILES = BATCH // P
 SUBS = 4
 BLOCK = SUBS * P
 BLOCKS = SUBTILES // SUBS
-GROUP_BLOCKS = 4
-GROUPS = BLOCKS // GROUP_BLOCKS
-GROUP = GROUP_BLOCKS * BLOCK
 
 FLOPS = 2 * BATCH * DIM * HID + 2 * BATCH * HID * P_COLS
 
@@ -36,11 +32,9 @@ FLOPS = 2 * BATCH * DIM * HID + 2 * BATCH * HID * P_COLS
 def tile_cn_pa_t_kernel(tc, x, cond, W1, b1, W2_words, W2_scales, b2, out):
     nc = tc.nc
     with ExitStack() as ctx:
+        ctx.enter_context(tc.manual_schedule(engines={mybir.EngineType.Activation}))
         const = ctx.enter_context(tc.tile_pool(name="const", bufs=1))
-        prep = ctx.enter_context(tc.tile_pool(name="prep", bufs=2))
-        work = ctx.enter_context(tc.tile_pool(name="work", bufs=4))
-        block_pool = ctx.enter_context(tc.tile_pool(name="block", bufs=2))
-        held = ctx.enter_context(tc.tile_pool(name="held", bufs=3))
+        kept = ctx.enter_context(tc.tile_pool(name="kept", bufs=BLOCKS))
         psum_mm = ctx.enter_context(tc.psum_pool(name="psum_mm", bufs=4))
         psum_tr = ctx.enter_context(tc.psum_pool(name="psum_tr", bufs=3))
         psum_tp = ctx.enter_context(tc.psum_pool(name="psum_tp", bufs=1))
@@ -48,120 +42,80 @@ def tile_cn_pa_t_kernel(tc, x, cond, W1, b1, W2_words, W2_scales, b2, out):
         cond_view = cond.rearrange("(p i) d -> p i d", i=SUBTILES)
         x_view = x.rearrange("(p i) d -> p i d", i=SUBTILES)
         out_view = out.rearrange("(p i) d -> p i d", i=SUBTILES)
-        scratch = out.rearrange("(p i) d -> p (i d)", i=SUBTILES)[:, BATCH * DIM // P // 2 :]
 
+        one_col = const.tile([P, 1], F32)
+        nc.vector.memset(one_col[:], 1.0)
+        warm = const.tile([P, 1], F32)
+        nc.scalar.activation(out=warm[:], in_=one_col[:], func=ACT.Ln)
         ident_bf = const.tile([P, P], BF16)
         make_identity(nc, ident_bf[:])
         ident_f32 = const.tile([P, P], F32)
         make_identity(nc, ident_f32[:])
 
-        cond_all = const.tile([P, SUBTILES, DIM], BF16)
-        x_all = const.tile([P, SUBTILES, DIM], BF16)
-
-        def load_block(blk):
-            subs = slice(blk * SUBS, (blk + 1) * SUBS)
-            nc.sync.dma_start(out=cond_all[:, subs, :], in_=cond_view[:, subs, :])
-            nc.sync.dma_start(out=x_all[:, subs, :], in_=x_view[:, subs, :])
-
-        load_block(0)
-
         w1_rows = const.tile([P, HID], BF16)
-        nc.sync.dma_start(out=w1_rows[:], in_=W1)
         w1_by_t = const.tile([P, PACK, P], BF16)
-        nc.vector.tensor_copy(out=w1_by_t[:], in_=w1_rows[:].rearrange("d (p t) -> d t p", t=PACK))
         b1_bf = const.tile([P, PACK], BF16)
-        nc.sync.dma_start(out=b1_bf[:], in_=b1.rearrange("(p t) -> p t", t=PACK))
         b1_col = const.tile([P, PACK], F32)
-        nc.vector.tensor_copy(out=b1_col[:], in_=b1_bf[:])
-
-        b2_rows = const.tile([P, P], BF16)
-        nc.vector.memset(b2_rows[:], 0.0)
-        nc.sync.dma_start(out=b2_rows[0:COL_TILES, :], in_=b2.rearrange("(r q) -> r q", q=P))
-        b2_ps = psum_tp.tile([P, P], BF16, tag="tp")
-        nc.tensor.transpose(b2_ps[:], b2_rows[:], ident_bf[:])
-        b2_col = const.tile([P, COL_TILES], F32)
-        nc.vector.tensor_copy(out=b2_col[:], in_=b2_ps[:, 0:COL_TILES])
-        half_eps_bias = const.tile([P, 1], F32)
-        nc.vector.tensor_scalar_mul(out=half_eps_bias[:], in0=b2_col[:, EPS : EPS + 1], scalar1=0.05)
-        alpha_bias = const.tile([P, 1], F32)
-        nc.vector.tensor_scalar_mul(out=alpha_bias[:], in0=b2_col[:, ALPHA : ALPHA + 1], scalar1=0.1)
-        one_col = const.tile([P, 1], F32)
-        nc.vector.memset(one_col[:], 1.0)
-        ln_04_col = const.tile([P, 1], F32)
-        nc.vector.tensor_scalar_mul(out=ln_04_col[:], in0=one_col[:], scalar1=math.log(0.4))
-
         w2_scales = const.tile([P, P_COLS], U8, align_bytes=64)
-        nc.vector.memset(w2_scales[:].bitcast(I32), 0)
-        for quad in range(4):
-            nc.sync.dma_start(
-                out=w2_scales[32 * quad : 32 * quad + 4, :].bitcast(I32),
-                in_=W2_scales[0, 4 * quad : 4 * quad + 4, :].bitcast(I32),
-            )
         w2_codes = const.tile([P, P_COLS], U32, align_bytes=64)
-        nc.sync.dma_start(
-            out=w2_codes[:].bitcast(I32),
-            in_=W2_words[0].rearrange("p n t -> p (n t)").bitcast(I32),
-        )
+        codes_by_l = const.tile([P, 3 * DL], U32, align_bytes=64)
+        scales_by_l = const.tile([P, 3 * DL], U8, align_bytes=64)
+        b2_col = const.tile([P, COL_TILES], F32)
+        b2_dl = const.tile([P, 3, PACK], BF16)
+        b2_rows = const.tile([P, P], BF16)
+        bias1_plus_1 = const.tile([P, LS], F32)
+        half_eps_bias = const.tile([P, 1], F32)
+        alpha_bias = const.tile([P, 1], F32)
+        minus_one_col = const.tile([P, 1], F32)
+        ln_04_col = const.tile([P, 1], F32)
+        ln_den = const.tile([P, BATCH], F32)
 
-        def transpose_rows(rows_of_sub, dest):
-            turned = psum_tp.tile([P, BLOCK], BF16, tag="tp")
-            for s in range(SUBS):
-                nc.tensor.transpose(turned[:, s * P : (s + 1) * P], rows_of_sub(s), ident_bf[:])
-            nc.scalar.copy(out=dest, in_=turned[:])
-
-        def prepare(blk):
-            first = blk * SUBS
-            if blk + 1 < BLOCKS:
-                load_block(blk + 1)
-            cond_t = prep.tile([P, BLOCK], BF16)
-            transpose_rows(lambda s: cond_all[:, first + s, :], cond_t[:])
-
-            h_rows = prep.tile([P, PACK, BLOCK], BF16)
-            for t in range(PACK):
-                h_ps = psum_mm.tile([P, BLOCK], F32, tag="mm")
-                nc.tensor.matmul(out=h_ps[:], lhsT=w1_by_t[:, t, :], rhs=cond_t[:], start=True, stop=True)
-                nc.scalar.activation(
-                    out=h_rows[:, t, :], in_=h_ps[:], func=ACT.Relu, bias=b1_col[:, t : t + 1], scale=1.0
+        def load_weights():
+            nc.sync.dma_start(out=w1_rows[:], in_=W1)
+            nc.vector.tensor_copy(out=w1_by_t[:], in_=w1_rows[:].rearrange("d (p t) -> d t p", t=PACK))
+            nc.sync.dma_start(out=b1_bf[:], in_=b1.rearrange("(p t) -> p t", t=PACK))
+            nc.vector.tensor_copy(out=b1_col[:], in_=b1_bf[:])
+            nc.vector.memset(w2_scales[:].bitcast(I32), 0)
+            for quad in range(4):
+                nc.sync.dma_start(
+                    out=w2_scales[32 * quad : 32 * quad + 4, :].bitcast(I32),
+                    in_=W2_scales[0, 4 * quad : 4 * quad + 4, :].bitcast(I32),
                 )
-            h_grouped = prep.tile([P, BLOCK, PACK], BF16, align_bytes=64)
-            nc.vector.tensor_copy(
-                out=h_grouped[:].rearrange("p (c i) t -> p c t i", i=4),
-                in_=h_rows[:].rearrange("p t (c i) -> p c t i", i=4),
+            nc.sync.dma_start(
+                out=w2_codes[:].bitcast(I32),
+                in_=W2_words[0].rearrange("p n t -> p (n t)").bitcast(I32),
             )
-            h_codes = prep.tile([P, BLOCK], U32, align_bytes=64)
-            h_scales = prep.tile([P, BLOCK], U8, align_bytes=64)
-            nc.vector.quantize_mx(
-                out=h_codes[:].bitcast(FP8X4),
-                scales=h_scales[:],
-                in_=h_grouped[:].rearrange("p b t -> p (b t)"),
-            )
-
-            x_t = prep.tile([P, BLOCK], BF16)
-            transpose_rows(lambda s: x_all[:, first + s, :], x_t[:])
-            parked = scratch[:, blk * (BLOCK // 2) : (blk + 1) * (BLOCK // 2)]
-            nc.sync.dma_start(out=parked, in_=x_t[:].bitcast(F32))
-            x_by_c = prep.tile([P, C_TILES, BLOCK], BF16)
-            for j in range(C_TILES):
-                head = (-j * P) % LS
-                whole = (P - head) // LS
-                tail = P - head - whole * LS
-                feature = (j * P + head) // LS
-                pieces = [(0, feature - 1, 1, head), (head, feature, whole, LS), (P - tail, feature + whole, 1, tail)]
-                for row, d, features, copies in pieces:
-                    if copies > 0:
-                        nc.sync.dma_start(
-                            out=x_by_c[row : row + features * copies, j, :].bitcast(F32),
-                            in_=parked[d : d + features, :].unsqueeze(1).to_broadcast([features, copies, BLOCK // 2]),
-                        )
-            return x_by_c, h_codes, h_scales
+            for section in (2, 0, 1):
+                cols = slice(section * DL, (section + 1) * DL)
+                nc.vector.tensor_copy(
+                    out=codes_by_l[:, cols].bitcast(I32).rearrange("p (l d) -> p l d", l=LS),
+                    in_=w2_codes[:, cols].bitcast(I32).rearrange("p (d l) -> p l d", l=LS),
+                )
+                nc.vector.tensor_copy(
+                    out=scales_by_l[:, cols].rearrange("p (l d) -> p l d", l=LS),
+                    in_=w2_scales[:, cols].rearrange("p (d l) -> p l d", l=LS),
+                )
+            nc.sync.dma_start(out=b2_dl[:, :, 0:LS], in_=b2[0 : 3 * DL].rearrange("(s d l) -> d s l", s=3, l=LS))
+            nc.vector.tensor_copy(out=b2_col[:, 0 : 3 * LS].rearrange("p (s l) -> p s l", l=LS), in_=b2_dl[:, :, 0:LS])
+            nc.vector.memset(b2_rows[:], 0.0)
+            nc.sync.dma_start(out=b2_rows[0:COL_TILES, :], in_=b2.rearrange("(r q) -> r q", q=P))
+            b2_ps = psum_tr.tile([P, P], BF16, tag="tr")
+            nc.tensor.transpose(b2_ps[:], b2_rows[:], ident_bf[:])
+            nc.vector.tensor_copy(out=b2_col[:, BIAS2:COL_TILES], in_=b2_ps[:, BIAS2:COL_TILES])
+            nc.vector.tensor_scalar_add(out=bias1_plus_1[:], in0=b2_col[:, BIAS1 : BIAS1 + LS], scalar1=1.0)
+            nc.vector.tensor_scalar_mul(out=half_eps_bias[:], in0=b2_col[:, EPS : EPS + 1], scalar1=0.05)
+            nc.vector.tensor_scalar_mul(out=alpha_bias[:], in0=b2_col[:, ALPHA : ALPHA + 1], scalar1=0.1)
+            nc.vector.memset(minus_one_col[:], -1.0)
+            nc.vector.tensor_scalar_mul(out=ln_04_col[:], in0=one_col[:], scalar1=math.log(0.4))
 
         def subnet(col_tile, h_codes, h_scales):
             cols = slice(col_tile * P, (col_tile + 1) * P)
+            codes, scales = (codes_by_l, scales_by_l) if col_tile < BIAS2 else (w2_codes, w2_scales)
             p_ps = psum_mm.tile([P, BLOCK], F32, tag="mm")
             nc.tensor.matmul_mx(
                 out=p_ps[:],
-                lhsT=w2_codes[:, cols].bitcast(FP8X4),
-                lhsT_scale=w2_scales[:, cols],
+                lhsT=codes[:, cols].bitcast(FP8X4),
+                lhsT_scale=scales[:, cols],
                 rhs=h_codes[:].bitcast(FP8X4),
                 rhs_scale=h_scales[:],
                 start=True,
@@ -172,119 +126,174 @@ def tile_cn_pa_t_kernel(tc, x, cond, W1, b1, W2_words, W2_scales, b2, out):
         def bias_of(col_tile):
             return b2_col[:, col_tile : col_tile + 1]
 
-        def column_tiles(prepared):
-            x_by_c, h_codes, h_scales = prepared
-            terms = block_pool.tile([P, C_TILES, BLOCK], F32)
-            prods = block_pool.tile([P, C_TILES, BLOCK], F32)
-            for j in range(C_TILES):
-                mat2_ps = subnet(MAT2 + j, h_codes, h_scales)
-                mat2 = work.tile([P, BLOCK], F32)
-                nc.scalar.activation(out=mat2[:], in_=mat2_ps[:], func=ACT.Identity, bias=bias_of(MAT2 + j), scale=1.0)
-                mat1_ps = subnet(MAT1 + j, h_codes, h_scales)
-                xm = work.tile([P, BLOCK], F32)
-                nc.vector.scalar_tensor_tensor(
-                    out=xm[:], in0=mat1_ps[:], scalar=bias_of(MAT1 + j), in1=x_by_c[:, j, :], op0=ALU.add, op1=ALU.mult
-                )
-                nc.vector.scalar_tensor_tensor(
-                    out=prods[:, j, :], in0=mat1_ps[:], scalar=bias_of(MAT1 + j), in1=mat2[:], op0=ALU.add, op1=ALU.mult
-                )
-                bias1_ps = subnet(BIAS1 + j, h_codes, h_scales)
-                z = work.tile([P, BLOCK], F32)
-                nc.vector.scalar_tensor_tensor(
-                    out=z[:], in0=bias1_ps[:], scalar=bias_of(BIAS1 + j), in1=xm[:], op0=ALU.add, op1=ALU.add
-                )
-                ez = work.tile([P, BLOCK], F32)
-                nc.scalar.activation(out=ez[:], in_=z[:], func=ACT.Exp)
-                nc.vector.tensor_scalar(out=ez[:], in0=ez[:], scalar1=-1.0, scalar2=0.0, op0=ALU.add, op1=ALU.min)
-                nc.vector.tensor_tensor(out=z[:], in0=z[:], in1=ez[:], op=ALU.max)
-                nc.gpsimd.tensor_tensor(out=terms[:, j, :], in0=z[:], in1=mat2[:], op=ALU.mult)
-
-            gate = held.tile([P, BLOCK], F32)
-            eps_ps = subnet(EPS, h_codes, h_scales)
-            nc.scalar.activation(out=gate[:], in_=eps_ps[:], func=ACT.Tanh, bias=half_eps_bias[:], scale=0.05)
-            gain = held.tile([P, BLOCK], F32)
-            alpha_ps = subnet(ALPHA, h_codes, h_scales)
-            nc.scalar.activation(out=gain[:], in_=alpha_ps[:], func=ACT.Exp, bias=alpha_bias[:], scale=0.1)
-            shift = held.tile([P, BLOCK], F32)
-            bias2_ps = subnet(BIAS2, h_codes, h_scales)
-            nc.scalar.activation(out=shift[:], in_=bias2_ps[:], func=ACT.Identity, bias=bias_of(BIAS2), scale=1.0)
-
-            return terms, prods, gate, gain, shift
-
-        def turn_back(rows):
+        def turned_sum(addends):
             turned = psum_tr.tile([P, BLOCK], F32, tag="tr")
             for s in range(SUBS):
                 sub = slice(s * P, (s + 1) * P)
-                nc.tensor.transpose(turned[:, sub], rows[:, sub], ident_f32[:])
+                for n, rows in enumerate(addends):
+                    nc.tensor.matmul(
+                        out=turned[:, sub],
+                        lhsT=rows[:, sub],
+                        rhs=ident_f32[:],
+                        start=(n == 0),
+                        stop=(n == len(addends) - 1),
+                        is_transpose=True,
+                    )
             return turned
 
-        def sums_over_l(blk, column_results, den_grp, scaled_grp, offset_grp):
-            terms, prods, gate, gain, shift = column_results
-            in_group = blk % GROUP_BLOCKS
-            cols = slice(in_group * BLOCK, (in_group + 1) * BLOCK)
-            relu_rows = block_pool.tile([P, SUBS, DIM * LS], F32)
-            for s in range(SUBS):
-                prods_t = psum_tr.tile([P, DIM * LS], F32, tag="tr")
-                for j in range(C_TILES):
-                    nc.tensor.transpose(prods_t[:, j * P : (j + 1) * P], prods[:, j, s * P : (s + 1) * P], ident_f32[:])
-                nc.scalar.activation(out=relu_rows[:, s, :], in_=prods_t[:], func=ACT.Relu, scale=-1.0)
-            by_l = relu_rows[:].rearrange("p s (d l) -> p (s d) l", l=LS)
-            den_cols = den_grp[:, cols]
-            nc.gpsimd.tensor_tensor(out=den_cols, in0=by_l[:, :, 0], in1=by_l[:, :, 1], op=ALU.add)
-            nc.gpsimd.tensor_tensor(out=den_cols, in0=den_cols, in1=by_l[:, :, 2], op=ALU.add)
-            if in_group == GROUP_BLOCKS - 1:
-                nc.scalar.activation(out=den_grp[:], in_=den_grp[:], func=ACT.Ln, bias=one_col[:], scale=1.0)
-                nc.scalar.activation(out=den_grp[:], in_=den_grp[:], func=ACT.Exp, bias=ln_04_col[:], scale=-1.0)
+        def block_cols(blk):
+            return slice(blk * BLOCK, (blk + 1) * BLOCK)
 
-            num = block_pool.tile([P, BLOCK], F32)
-            for s in range(SUBS):
-                terms_t = psum_tr.tile([P, DIM * LS], F32, tag="tr")
-                for j in range(C_TILES):
-                    nc.tensor.transpose(terms_t[:, j * P : (j + 1) * P], terms[:, j, s * P : (s + 1) * P], ident_f32[:])
-                nc.vector.tensor_reduce(
-                    out=num[:, s * P : (s + 1) * P],
-                    in_=terms_t[:].rearrange("p (d l) -> p d l", l=LS),
-                    axis=AXIS.X,
-                    op=ALU.add,
+        with ExitStack() as phase:
+            loads = phase.enter_context(tc.tile_pool(name="loads", bufs=4))
+            prep = phase.enter_context(tc.tile_pool(name="prep", bufs=2))
+            work = phase.enter_context(tc.tile_pool(name="work", bufs=2))
+
+            def load_block(blk):
+                subs = slice(blk * SUBS, (blk + 1) * SUBS)
+                cond_rows = loads.tile([P, SUBS, DIM], BF16)
+                nc.sync.dma_start(out=cond_rows[:], in_=cond_view[:, subs, :])
+                x_rows = loads.tile([P, SUBS, DIM], BF16)
+                nc.sync.dma_start(out=x_rows[:], in_=x_view[:, subs, :])
+                return cond_rows, x_rows
+
+            def transpose_rows(rows, dest):
+                turned = psum_tp.tile([P, BLOCK], BF16, tag="tp")
+                for s in range(SUBS):
+                    nc.tensor.transpose(turned[:, s * P : (s + 1) * P], rows[:, s, :], ident_bf[:])
+                nc.scalar.copy(out=dest, in_=turned[:])
+
+            def prepare(loaded):
+                cond_rows, x_rows = loaded
+                cond_t = prep.tile([P, BLOCK], BF16)
+                transpose_rows(cond_rows, cond_t[:])
+                h_rows = prep.tile([P, PACK, BLOCK], BF16)
+                for t in range(PACK):
+                    h_ps = psum_mm.tile([P, BLOCK], F32, tag="mm")
+                    nc.tensor.matmul(out=h_ps[:], lhsT=w1_by_t[:, t, :], rhs=cond_t[:], start=True, stop=True)
+                    nc.scalar.activation(
+                        out=h_rows[:, t, :], in_=h_ps[:], func=ACT.Relu, bias=b1_col[:, t : t + 1], scale=1.0
+                    )
+                h_grouped = prep.tile([P, BLOCK, PACK], BF16, align_bytes=64)
+                nc.vector.tensor_copy(
+                    out=h_grouped[:].rearrange("p (c i) t -> p c t i", i=4),
+                    in_=h_rows[:].rearrange("p t (c i) -> p c t i", i=4),
                 )
-            scaled = scaled_grp[:, cols]
-            offset = offset_grp[:, cols]
-            gate_t = turn_back(gate)
-            nc.vector.scalar_tensor_tensor(out=scaled, in0=gate_t[:], scalar=1.0, in1=num[:], op0=ALU.add, op1=ALU.mult)
-            gain_t = turn_back(gain)
-            nc.vector.tensor_tensor(out=scaled, in0=gain_t[:], in1=scaled, op=ALU.mult)
-            x_rows = x_all[:, blk * SUBS : (blk + 1) * SUBS, :].rearrange("p s d -> p (s d)")
-            nc.vector.tensor_tensor(out=offset, in0=gain_t[:], in1=x_rows, op=ALU.mult)
-            shift_t = turn_back(shift)
-            nc.vector.tensor_tensor(out=offset, in0=shift_t[:], in1=offset, op=ALU.add)
-
-        def finish_group(grp, den_grp, scaled_grp, offset_grp):
-            helper = nc.vector if grp == GROUPS - 1 else nc.gpsimd
-            for in_group in range(GROUP_BLOCKS):
-                blk = grp * GROUP_BLOCKS + in_group
-                cols = slice(in_group * BLOCK, (in_group + 1) * BLOCK)
-                helper.tensor_tensor(out=scaled_grp[:, cols], in0=scaled_grp[:, cols], in1=den_grp[:, cols], op=ALU.mult)
-                result = work.tile([P, SUBS, DIM], F32)
-                helper.tensor_tensor(
-                    out=result[:].rearrange("p s d -> p (s d)"), in0=scaled_grp[:, cols], in1=offset_grp[:, cols], op=ALU.add
+                h_codes = kept.tile([P, BLOCK], U32, align_bytes=64)
+                h_scales = kept.tile([P, BLOCK], U8, align_bytes=64)
+                nc.vector.quantize_mx(
+                    out=h_codes[:].bitcast(FP8X4),
+                    scales=h_scales[:],
+                    in_=h_grouped[:].rearrange("p b t -> p (b t)"),
                 )
-                nc.sync.dma_start(out=out_view[:, blk * SUBS : (blk + 1) * SUBS, :], in_=result[:])
+                x_t = kept.tile([P, BLOCK], BF16)
+                transpose_rows(x_rows, x_t[:])
+                return x_t, h_codes, h_scales
 
-        prepared = [prepare(0)]
-        tiles = []
+            def products(prepared):
+                x_t, h_codes, h_scales = prepared
+                mat2 = kept.tile([P, LS, BLOCK], F32)
+                z1 = kept.tile([P, LS, BLOCK], F32)
+                relus = work.tile([P, LS, BLOCK], F32)
+                for l in range(LS):
+                    mat2_ps = subnet(MAT2 + l, h_codes, h_scales)
+                    nc.scalar.activation(
+                        out=mat2[:, l, :], in_=mat2_ps[:], func=ACT.Identity, bias=bias_of(MAT2 + l), scale=1.0
+                    )
+                    mat1_ps = subnet(MAT1 + l, h_codes, h_scales)
+                    nc.vector.scalar_tensor_tensor(
+                        out=z1[:, l, :], in0=mat1_ps[:], scalar=bias_of(MAT1 + l), in1=x_t[:], op0=ALU.add, op1=ALU.mult
+                    )
+                    nc.vector.scalar_tensor_tensor(
+                        out=relus[:, l, :], in0=mat1_ps[:], scalar=bias_of(MAT1 + l), in1=mat2[:, l, :], op0=ALU.add, op1=ALU.mult
+                    )
+                nc.gpsimd.tensor_scalar(
+                    out=relus[:], in0=relus[:], scalar1=-1.0, scalar2=0.0, op0=ALU.mult, op1=ALU.max
+                )
+                return mat2, z1, relus
+
+            def log_denominator(blk, relus):
+                den_t = turned_sum([relus[:, l, :] for l in range(LS)])
+                nc.scalar.activation(out=ln_den[:, block_cols(blk)], in_=den_t[:], func=ACT.Ln, bias=one_col[:], scale=1.0)
+
+            loaded = [load_block(0)]
+            load_weights()
+            loaded.append(load_block(1))
+            loaded.append(load_block(2))
+            prepared = [prepare(loaded[0]), prepare(loaded[1])]
+            made = []
+            for step in range(BLOCKS):
+                if step + 3 < BLOCKS:
+                    loaded.append(load_block(step + 3))
+                made.append(products(prepared[step]))
+                if step + 2 < BLOCKS:
+                    prepared.append(prepare(loaded[step + 2]))
+                if step >= 1:
+                    log_denominator(step - 1, made[step - 1][2])
+            log_denominator(BLOCKS - 1, made[BLOCKS - 1][2])
+
+        wide = ctx.enter_context(tc.tile_pool(name="wide", bufs=3))
+        side = ctx.enter_context(tc.tile_pool(name="side", bufs=2))
+        fin = ctx.enter_context(tc.tile_pool(name="fin", bufs=2))
+
+        def arguments(blk):
+            x_t, h_codes, h_scales = prepared[blk]
+            z1 = made[blk][1]
+            for l in range(LS):
+                bias1_ps = subnet(BIAS1 + l, h_codes, h_scales)
+                nc.vector.scalar_tensor_tensor(
+                    out=z1[:, l, :], in0=bias1_ps[:], scalar=bias1_plus_1[:, l : l + 1], in1=z1[:, l, :], op0=ALU.add, op1=ALU.add
+                )
+
+        def side_sections(blk):
+            x_t, h_codes, h_scales = prepared[blk]
+            gate = side.tile([P, BLOCK], F32)
+            eps_ps = subnet(EPS, h_codes, h_scales)
+            nc.scalar.activation(out=gate[:], in_=eps_ps[:], func=ACT.Tanh, bias=half_eps_bias[:], scale=0.05)
+            gain = side.tile([P, BLOCK], F32)
+            alpha_ps = subnet(ALPHA, h_codes, h_scales)
+            nc.scalar.activation(out=gain[:], in_=alpha_ps[:], func=ACT.Exp, bias=alpha_bias[:], scale=0.1)
+            shift = side.tile([P, BLOCK], F32)
+            bias2_ps = subnet(BIAS2, h_codes, h_scales)
+            nc.scalar.activation(out=shift[:], in_=bias2_ps[:], func=ACT.Identity, bias=bias_of(BIAS2), scale=1.0)
+            nc.scalar.activation(
+                out=ln_den[:, block_cols(blk)], in_=ln_den[:, block_cols(blk)], func=ACT.Exp, bias=ln_04_col[:], scale=-1.0
+            )
+            gated_gain = side.tile([P, BLOCK], F32)
+            nc.vector.scalar_tensor_tensor(
+                out=gated_gain[:], in0=gate[:], scalar=1.0, in1=gain[:], op0=ALU.add, op1=ALU.mult
+            )
+            gain_x = side.tile([P, BLOCK], F32)
+            nc.gpsimd.tensor_tensor(out=gain_x[:], in0=gain[:], in1=x_t[:], op=ALU.mult)
+            return gated_gain, shift, gain_x
+
+        def elu_terms(blk):
+            mat2, z1, relus = made[blk]
+            terms = wide.tile([P, LS, BLOCK], F32)
+            nc.scalar.activation(out=terms[:], in_=z1[:], func=ACT.Exp, bias=minus_one_col[:], scale=1.0)
+            nc.vector.scalar_tensor_tensor(out=terms[:], in0=z1[:], scalar=1.0, in1=terms[:], op0=ALU.max, op1=ALU.min)
+            nc.vector.scalar_tensor_tensor(out=terms[:], in0=terms[:], scalar=-1.0, in1=mat2[:], op0=ALU.add, op1=ALU.mult)
+            return terms
+
+        def finish(blk, terms, sides):
+            gated_gain, shift, gain_x = sides
+            factor = fin.tile([P, BLOCK], F32)
+            gated_t = turned_sum([gated_gain[:]])
+            nc.vector.tensor_tensor(out=factor[:], in0=gated_t[:], in1=ln_den[:, block_cols(blk)], op=ALU.mult)
+            num_t = turned_sum([terms[:, l, :] for l in range(LS)])
+            nc.vector.tensor_tensor(out=factor[:], in0=num_t[:], in1=factor[:], op=ALU.mult)
+            offset_t = turned_sum([shift[:], gain_x[:]])
+            result = fin.tile([P, SUBS, DIM], F32)
+            nc.vector.tensor_tensor(
+                out=result[:].rearrange("p s d -> p (s d)"), in0=offset_t[:], in1=factor[:], op=ALU.add
+            )
+            nc.sync.dma_start(out=out_view[:, blk * SUBS : (blk + 1) * SUBS, :], in_=result[:])
+
+        done = []
         for step in range(BLOCKS + 1):
             if step < BLOCKS:
-                tiles.append(column_tiles(prepared[step]))
+                arguments(step)
+                sides = side_sections(step)
+                done.append((elu_terms(step), sides))
             if step >= 1:
-                blk = step - 1
-                if blk % GROUP_BLOCKS == 0:
-                    den_grp = block_pool.tile([P, GROUP], F32)
-                    scaled_grp = block_pool.tile([P, GROUP], F32)
-                    offset_grp = block_pool.tile([P, GROUP], F32)
-                sums_over_l(blk, tiles[blk], den_grp, scaled_grp, offset_grp)
-                if blk % GROUP_BLOCKS == GROUP_BLOCKS - 1:
-                    finish_group(blk // GROUP_BLOCKS, den_grp, scaled_grp, offset_grp)
-            if step == 0:
-                prepared.append(prepare(1))
-            if step + 2 < BLOCKS:
-                prepared.append(prepare(step + 2))
+                finish(step - 1, done[step - 1][0], done[step - 1][1])

@@ -147,7 +147,7 @@ def tile_cn_pa_t_kernel(tc, x, cond, W1, b1, W2_words, W2_scales, b2, out):
         with ExitStack() as phase:
             loads = phase.enter_context(tc.tile_pool(name="loads", bufs=4))
             prep = phase.enter_context(tc.tile_pool(name="prep", bufs=2))
-            work = phase.enter_context(tc.tile_pool(name="work", bufs=2))
+            work = phase.enter_context(tc.tile_pool(name="work", bufs=3))
 
             def load_block(blk):
                 subs = slice(blk * SUBS, (blk + 1) * SUBS)
@@ -207,10 +207,15 @@ def tile_cn_pa_t_kernel(tc, x, cond, W1, b1, W2_words, W2_scales, b2, out):
                     nc.vector.scalar_tensor_tensor(
                         out=relus[:, l, :], in0=mat1_ps[:], scalar=bias_of(MAT1 + l), in1=mat2[:, l, :], op0=ALU.add, op1=ALU.mult
                     )
-                nc.gpsimd.tensor_scalar(
-                    out=relus[:], in0=relus[:], scalar1=-1.0, scalar2=0.0, op0=ALU.mult, op1=ALU.max
-                )
+                for l in range(LS):
+                    bias1_ps = subnet(BIAS1 + l, h_codes, h_scales)
+                    nc.vector.scalar_tensor_tensor(
+                        out=z1[:, l, :], in0=bias1_ps[:], scalar=bias1_plus_1[:, l : l + 1], in1=z1[:, l, :], op0=ALU.add, op1=ALU.add
+                    )
                 return mat2, z1, relus
+
+            def clamp(relus):
+                nc.scalar.activation(out=relus[:], in_=relus[:], func=ACT.Relu, scale=-1.0)
 
             def log_denominator(blk, relus):
                 den_t = turned_sum([relus[:, l, :] for l in range(LS)])
@@ -226,24 +231,19 @@ def tile_cn_pa_t_kernel(tc, x, cond, W1, b1, W2_words, W2_scales, b2, out):
                 if step + 3 < BLOCKS:
                     loaded.append(load_block(step + 3))
                 made.append(products(prepared[step]))
+                if step >= 1:
+                    clamp(made[step - 1][2])
                 if step + 2 < BLOCKS:
                     prepared.append(prepare(loaded[step + 2]))
-                if step >= 1:
-                    log_denominator(step - 1, made[step - 1][2])
+                if step >= 2:
+                    log_denominator(step - 2, made[step - 2][2])
+            clamp(made[BLOCKS - 1][2])
+            log_denominator(BLOCKS - 2, made[BLOCKS - 2][2])
             log_denominator(BLOCKS - 1, made[BLOCKS - 1][2])
 
         wide = ctx.enter_context(tc.tile_pool(name="wide", bufs=3))
         side = ctx.enter_context(tc.tile_pool(name="side", bufs=2))
         fin = ctx.enter_context(tc.tile_pool(name="fin", bufs=2))
-
-        def arguments(blk):
-            x_t, h_codes, h_scales = prepared[blk]
-            z1 = made[blk][1]
-            for l in range(LS):
-                bias1_ps = subnet(BIAS1 + l, h_codes, h_scales)
-                nc.vector.scalar_tensor_tensor(
-                    out=z1[:, l, :], in0=bias1_ps[:], scalar=bias1_plus_1[:, l : l + 1], in1=z1[:, l, :], op0=ALU.add, op1=ALU.add
-                )
 
         def side_sections(blk):
             x_t, h_codes, h_scales = prepared[blk]
@@ -292,7 +292,6 @@ def tile_cn_pa_t_kernel(tc, x, cond, W1, b1, W2_words, W2_scales, b2, out):
         done = []
         for step in range(BLOCKS + 1):
             if step < BLOCKS:
-                arguments(step)
                 sides = side_sections(step)
                 done.append((elu_terms(step), sides))
             if step >= 1:

@@ -32,12 +32,10 @@ FLOPS = 2 * BATCH * DIM * HID + 2 * BATCH * HID * P_COLS
 def tile_cn_pa_t_kernel(tc, x, cond, W1, b1, W2_words, W2_scales, b2, out):
     nc = tc.nc
     with ExitStack() as ctx:
-        ctx.enter_context(tc.manual_schedule(engines={mybir.EngineType.Activation}))
+        ctx.enter_context(tc.manual_schedule(engines={mybir.EngineType.Activation, mybir.EngineType.DVE}))
         const = ctx.enter_context(tc.tile_pool(name="const", bufs=1))
         kept = ctx.enter_context(tc.tile_pool(name="kept", bufs=BLOCKS))
-        psum_mm = ctx.enter_context(tc.psum_pool(name="psum_mm", bufs=4))
-        psum_tr = ctx.enter_context(tc.psum_pool(name="psum_tr", bufs=3))
-        psum_tp = ctx.enter_context(tc.psum_pool(name="psum_tp", bufs=1))
+        banks = {}
 
         cond_view = cond.rearrange("(p i) d -> p i d", i=SUBTILES)
         x_view = x.rearrange("(p i) d -> p i d", i=SUBTILES)
@@ -71,11 +69,13 @@ def tile_cn_pa_t_kernel(tc, x, cond, W1, b1, W2_words, W2_scales, b2, out):
         ln_den = const.tile([P, BATCH], F32)
 
         def load_weights():
-            nc.sync.dma_start(out=w1_rows[:], in_=W1)
-            nc.vector.tensor_copy(out=w1_by_t[:], in_=w1_rows[:].rearrange("d (p t) -> d t p", t=PACK))
-            nc.sync.dma_start(out=b1_bf[:], in_=b1.rearrange("(p t) -> p t", t=PACK))
-            nc.vector.tensor_copy(out=b1_col[:], in_=b1_bf[:])
             nc.vector.memset(w2_scales[:].bitcast(I32), 0)
+            nc.vector.memset(b2_rows[:], 0.0)
+            nc.vector.memset(minus_one_col[:], -1.0)
+            nc.sync.dma_start(out=w1_rows[:], in_=W1)
+            nc.sync.dma_start(out=b1_bf[:], in_=b1.rearrange("(p t) -> p t", t=PACK))
+            nc.sync.dma_start(out=b2_dl[:, :, 0:LS], in_=b2[0 : 3 * DL].rearrange("(s d l) -> d s l", s=3, l=LS))
+            nc.sync.dma_start(out=b2_rows[0:COL_TILES, :], in_=b2.rearrange("(r q) -> r q", q=P))
             for quad in range(4):
                 nc.sync.dma_start(
                     out=w2_scales[32 * quad : 32 * quad + 4, :].bitcast(I32),
@@ -85,33 +85,34 @@ def tile_cn_pa_t_kernel(tc, x, cond, W1, b1, W2_words, W2_scales, b2, out):
                 out=w2_codes[:].bitcast(I32),
                 in_=W2_words[0].rearrange("p n t -> p (n t)").bitcast(I32),
             )
-            for section in (2, 0, 1):
-                cols = slice(section * DL, (section + 1) * DL)
-                nc.vector.tensor_copy(
-                    out=codes_by_l[:, cols].bitcast(I32).rearrange("p (l d) -> p l d", l=LS),
-                    in_=w2_codes[:, cols].bitcast(I32).rearrange("p (d l) -> p l d", l=LS),
-                )
-                nc.vector.tensor_copy(
-                    out=scales_by_l[:, cols].rearrange("p (l d) -> p l d", l=LS),
-                    in_=w2_scales[:, cols].rearrange("p (d l) -> p l d", l=LS),
-                )
-            nc.sync.dma_start(out=b2_dl[:, :, 0:LS], in_=b2[0 : 3 * DL].rearrange("(s d l) -> d s l", s=3, l=LS))
+            nc.vector.tensor_copy(out=w1_by_t[:], in_=w1_rows[:].rearrange("d (p t) -> d t p", t=PACK))
+            nc.vector.tensor_copy(out=b1_col[:], in_=b1_bf[:])
+
+        def bias_columns():
             nc.vector.tensor_copy(out=b2_col[:, 0 : 3 * LS].rearrange("p (s l) -> p s l", l=LS), in_=b2_dl[:, :, 0:LS])
-            nc.vector.memset(b2_rows[:], 0.0)
-            nc.sync.dma_start(out=b2_rows[0:COL_TILES, :], in_=b2.rearrange("(r q) -> r q", q=P))
-            b2_ps = psum_tr.tile([P, P], BF16, tag="tr")
+            b2_ps = banks["tr"].tile([P, P], BF16, tag="tr")
             nc.tensor.transpose(b2_ps[:], b2_rows[:], ident_bf[:])
             nc.vector.tensor_copy(out=b2_col[:, BIAS2:COL_TILES], in_=b2_ps[:, BIAS2:COL_TILES])
             nc.vector.tensor_scalar_add(out=bias1_plus_1[:], in0=b2_col[:, BIAS1 : BIAS1 + LS], scalar1=1.0)
             nc.vector.tensor_scalar_mul(out=half_eps_bias[:], in0=b2_col[:, EPS : EPS + 1], scalar1=0.05)
             nc.vector.tensor_scalar_mul(out=alpha_bias[:], in0=b2_col[:, ALPHA : ALPHA + 1], scalar1=0.1)
-            nc.vector.memset(minus_one_col[:], -1.0)
             nc.vector.tensor_scalar_mul(out=ln_04_col[:], in0=one_col[:], scalar1=math.log(0.4))
+
+        def sort_by_l(section):
+            cols = slice(section * DL, (section + 1) * DL)
+            nc.vector.tensor_copy(
+                out=codes_by_l[:, cols].bitcast(I32).rearrange("p (l d) -> p l d", l=LS),
+                in_=w2_codes[:, cols].bitcast(I32).rearrange("p (d l) -> p l d", l=LS),
+            )
+            nc.vector.tensor_copy(
+                out=scales_by_l[:, cols].rearrange("p (l d) -> p l d", l=LS),
+                in_=w2_scales[:, cols].rearrange("p (d l) -> p l d", l=LS),
+            )
 
         def subnet(col_tile, h_codes, h_scales):
             cols = slice(col_tile * P, (col_tile + 1) * P)
             codes, scales = (codes_by_l, scales_by_l) if col_tile < BIAS2 else (w2_codes, w2_scales)
-            p_ps = psum_mm.tile([P, BLOCK], F32, tag="mm")
+            p_ps = banks["mm"].tile([P, BLOCK], F32, tag="mm")
             nc.tensor.matmul_mx(
                 out=p_ps[:],
                 lhsT=codes[:, cols].bitcast(FP8X4),
@@ -127,7 +128,7 @@ def tile_cn_pa_t_kernel(tc, x, cond, W1, b1, W2_words, W2_scales, b2, out):
             return b2_col[:, col_tile : col_tile + 1]
 
         def turned_sum(addends):
-            turned = psum_tr.tile([P, BLOCK], F32, tag="tr")
+            turned = banks["tr"].tile([P, BLOCK], F32, tag="tr")
             for s in range(SUBS):
                 sub = slice(s * P, (s + 1) * P)
                 for n, rows in enumerate(addends):
@@ -144,18 +145,23 @@ def tile_cn_pa_t_kernel(tc, x, cond, W1, b1, W2_words, W2_scales, b2, out):
         def block_cols(blk):
             return slice(blk * BLOCK, (blk + 1) * BLOCK)
 
+        x_ts, codes_of, scales_of, mat2s, z1s = {}, {}, {}, {}, {}
+
         with ExitStack() as phase:
-            loads = phase.enter_context(tc.tile_pool(name="loads", bufs=4))
+            loads = phase.enter_context(tc.tile_pool(name="loads", bufs=BLOCKS))
             prep = phase.enter_context(tc.tile_pool(name="prep", bufs=2))
             work = phase.enter_context(tc.tile_pool(name="work", bufs=3))
+            banks["mm"] = phase.enter_context(tc.psum_pool(name="mm1", bufs=6))
+            banks["tr"] = phase.enter_context(tc.psum_pool(name="tr1", bufs=1))
+            psum_tp = phase.enter_context(tc.psum_pool(name="tp1", bufs=1))
+            cond_rows, x_rows, cond_ts, h_rows, h_groups, relus = {}, {}, {}, {}, {}, {}
 
             def load_block(blk):
                 subs = slice(blk * SUBS, (blk + 1) * SUBS)
-                cond_rows = loads.tile([P, SUBS, DIM], BF16)
-                nc.sync.dma_start(out=cond_rows[:], in_=cond_view[:, subs, :])
-                x_rows = loads.tile([P, SUBS, DIM], BF16)
-                nc.sync.dma_start(out=x_rows[:], in_=x_view[:, subs, :])
-                return cond_rows, x_rows
+                cond_rows[blk] = loads.tile([P, SUBS, DIM], BF16, name="cond_rows")
+                nc.sync.dma_start(out=cond_rows[blk][:], in_=cond_view[:, subs, :])
+                x_rows[blk] = loads.tile([P, SUBS, DIM], BF16, name="x_rows")
+                nc.sync.dma_start(out=x_rows[blk][:], in_=x_view[:, subs, :])
 
             def transpose_rows(rows, dest):
                 turned = psum_tp.tile([P, BLOCK], BF16, tag="tp")
@@ -163,136 +169,199 @@ def tile_cn_pa_t_kernel(tc, x, cond, W1, b1, W2_words, W2_scales, b2, out):
                     nc.tensor.transpose(turned[:, s * P : (s + 1) * P], rows[:, s, :], ident_bf[:])
                 nc.scalar.copy(out=dest, in_=turned[:])
 
-            def prepare(loaded):
-                cond_rows, x_rows = loaded
-                cond_t = prep.tile([P, BLOCK], BF16)
-                transpose_rows(cond_rows, cond_t[:])
-                h_rows = prep.tile([P, PACK, BLOCK], BF16)
-                for t in range(PACK):
-                    h_ps = psum_mm.tile([P, BLOCK], F32, tag="mm")
-                    nc.tensor.matmul(out=h_ps[:], lhsT=w1_by_t[:, t, :], rhs=cond_t[:], start=True, stop=True)
-                    nc.scalar.activation(
-                        out=h_rows[:, t, :], in_=h_ps[:], func=ACT.Relu, bias=b1_col[:, t : t + 1], scale=1.0
+            def turn_inputs(blk):
+                if blk < BLOCKS:
+                    cond_ts[blk] = prep.tile([P, BLOCK], BF16, name="cond_t")
+                    transpose_rows(cond_rows[blk], cond_ts[blk][:])
+                    x_ts[blk] = kept.tile([P, BLOCK], BF16, name="x_t")
+                    transpose_rows(x_rows[blk], x_ts[blk][:])
+
+            def hidden(blk):
+                if blk < BLOCKS:
+                    h_rows[blk] = prep.tile([P, PACK, BLOCK], BF16, name="h_rows")
+                    for t in range(PACK):
+                        h_ps = banks["mm"].tile([P, BLOCK], F32, tag="mm")
+                        nc.tensor.matmul(out=h_ps[:], lhsT=w1_by_t[:, t, :], rhs=cond_ts[blk][:], start=True, stop=True)
+                        nc.scalar.activation(
+                            out=h_rows[blk][:, t, :], in_=h_ps[:], func=ACT.Relu, bias=b1_col[:, t : t + 1], scale=1.0
+                        )
+
+            def group_words(blk):
+                if blk < BLOCKS:
+                    h_groups[blk] = prep.tile([P, BLOCK, PACK], BF16, align_bytes=64, name="h_grouped")
+                    nc.vector.tensor_copy(
+                        out=h_groups[blk][:].rearrange("p (c i) t -> p c t i", i=4),
+                        in_=h_rows[blk][:].rearrange("p t (c i) -> p c t i", i=4),
                     )
-                h_grouped = prep.tile([P, BLOCK, PACK], BF16, align_bytes=64)
-                nc.vector.tensor_copy(
-                    out=h_grouped[:].rearrange("p (c i) t -> p c t i", i=4),
-                    in_=h_rows[:].rearrange("p t (c i) -> p c t i", i=4),
+
+            def quantise(blk):
+                if blk < BLOCKS:
+                    codes_of[blk] = kept.tile([P, BLOCK], U32, align_bytes=64, name="h_codes")
+                    scales_of[blk] = kept.tile([P, BLOCK], U8, align_bytes=64, name="h_scales")
+                    nc.vector.quantize_mx(
+                        out=codes_of[blk][:].bitcast(FP8X4),
+                        scales=scales_of[blk][:],
+                        in_=h_groups[blk][:].rearrange("p b t -> p (b t)"),
+                    )
+
+            def mat2_of(blk, l):
+                mat2_ps = subnet(MAT2 + l, codes_of[blk], scales_of[blk])
+                nc.scalar.activation(
+                    out=mat2s[blk][:, l, :], in_=mat2_ps[:], func=ACT.Identity, bias=bias_of(MAT2 + l), scale=1.0
                 )
-                h_codes = kept.tile([P, BLOCK], U32, align_bytes=64)
-                h_scales = kept.tile([P, BLOCK], U8, align_bytes=64)
-                nc.vector.quantize_mx(
-                    out=h_codes[:].bitcast(FP8X4),
-                    scales=h_scales[:],
-                    in_=h_grouped[:].rearrange("p b t -> p (b t)"),
+
+            def times_x(blk, l, mat1_ps):
+                nc.vector.scalar_tensor_tensor(
+                    out=z1s[blk][:, l, :], in0=mat1_ps[:], scalar=bias_of(MAT1 + l), in1=x_ts[blk][:], op0=ALU.add, op1=ALU.mult
                 )
-                x_t = kept.tile([P, BLOCK], BF16)
-                transpose_rows(x_rows, x_t[:])
-                return x_t, h_codes, h_scales
 
-            def products(prepared):
-                x_t, h_codes, h_scales = prepared
-                mat2 = kept.tile([P, LS, BLOCK], F32)
-                z1 = kept.tile([P, LS, BLOCK], F32)
-                relus = work.tile([P, LS, BLOCK], F32)
-                for l in range(LS):
-                    mat2_ps = subnet(MAT2 + l, h_codes, h_scales)
-                    nc.scalar.activation(
-                        out=mat2[:, l, :], in_=mat2_ps[:], func=ACT.Identity, bias=bias_of(MAT2 + l), scale=1.0
-                    )
-                    mat1_ps = subnet(MAT1 + l, h_codes, h_scales)
-                    nc.vector.scalar_tensor_tensor(
-                        out=z1[:, l, :], in0=mat1_ps[:], scalar=bias_of(MAT1 + l), in1=x_t[:], op0=ALU.add, op1=ALU.mult
-                    )
-                    nc.vector.scalar_tensor_tensor(
-                        out=relus[:, l, :], in0=mat1_ps[:], scalar=bias_of(MAT1 + l), in1=mat2[:, l, :], op0=ALU.add, op1=ALU.mult
-                    )
-                for l in range(LS):
-                    bias1_ps = subnet(BIAS1 + l, h_codes, h_scales)
-                    nc.vector.scalar_tensor_tensor(
-                        out=z1[:, l, :], in0=bias1_ps[:], scalar=bias1_plus_1[:, l : l + 1], in1=z1[:, l, :], op0=ALU.add, op1=ALU.add
-                    )
-                return mat2, z1, relus
+            def times_mat2(blk, l, mat1_ps):
+                nc.vector.scalar_tensor_tensor(
+                    out=relus[blk][:, l, :], in0=mat1_ps[:], scalar=bias_of(MAT1 + l), in1=mat2s[blk][:, l, :], op0=ALU.add, op1=ALU.mult
+                )
 
-            def clamp(relus):
-                nc.scalar.activation(out=relus[:], in_=relus[:], func=ACT.Relu, scale=-1.0)
+            def arguments(blk):
+                if 0 <= blk < BLOCKS:
+                    for l in range(LS):
+                        bias1_ps = subnet(BIAS1 + l, codes_of[blk], scales_of[blk])
+                        nc.vector.scalar_tensor_tensor(
+                            out=z1s[blk][:, l, :], in0=bias1_ps[:], scalar=bias1_plus_1[:, l : l + 1], in1=z1s[blk][:, l, :], op0=ALU.add, op1=ALU.add
+                        )
 
-            def log_denominator(blk, relus):
-                den_t = turned_sum([relus[:, l, :] for l in range(LS)])
+            def clamp(blk):
+                nc.scalar.activation(out=relus[blk][:], in_=relus[blk][:], func=ACT.Relu, scale=-1.0)
+
+            def log_denominator(blk):
+                den_t = turned_sum([relus[blk][:, l, :] for l in range(LS)])
                 nc.scalar.activation(out=ln_den[:, block_cols(blk)], in_=den_t[:], func=ACT.Ln, bias=one_col[:], scale=1.0)
 
-            loaded = [load_block(0)]
+            load_block(0)
             load_weights()
-            loaded.append(load_block(1))
-            loaded.append(load_block(2))
-            prepared = [prepare(loaded[0]), prepare(loaded[1])]
-            made = []
+            for blk in range(1, BLOCKS):
+                load_block(blk)
+            turn_inputs(0)
+            hidden(0)
+            bias_columns()
+            sort_by_l(2)
+            sort_by_l(0)
+            group_words(0)
+            sort_by_l(1)
+            quantise(0)
+            turn_inputs(1)
+            hidden(1)
+            turn_inputs(2)
             for step in range(BLOCKS):
-                if step + 3 < BLOCKS:
-                    loaded.append(load_block(step + 3))
-                made.append(products(prepared[step]))
+                mat2s[step] = kept.tile([P, LS, BLOCK], F32, name="mat2")
+                z1s[step] = kept.tile([P, LS, BLOCK], F32, name="z1")
+                relus[step] = work.tile([P, LS, BLOCK], F32, name="relus")
+                mat2_of(step, 0)
+                mat1_0 = subnet(MAT1, codes_of[step], scales_of[step])
+                times_x(step, 0, mat1_0)
+                mat2_of(step, 1)
+                mat1_1 = subnet(MAT1 + 1, codes_of[step], scales_of[step])
+                times_x(step, 1, mat1_1)
+                times_mat2(step, 0, mat1_0)
+                group_words(step + 1)
+                mat2_of(step, 2)
+                mat1_2 = subnet(MAT1 + 2, codes_of[step], scales_of[step])
+                times_x(step, 2, mat1_2)
+                times_mat2(step, 1, mat1_1)
+                times_mat2(step, 2, mat1_2)
+                quantise(step + 1)
                 if step >= 1:
-                    clamp(made[step - 1][2])
-                if step + 2 < BLOCKS:
-                    prepared.append(prepare(loaded[step + 2]))
-                if step >= 2:
-                    log_denominator(step - 2, made[step - 2][2])
-            clamp(made[BLOCKS - 1][2])
-            log_denominator(BLOCKS - 2, made[BLOCKS - 2][2])
-            log_denominator(BLOCKS - 1, made[BLOCKS - 1][2])
+                    clamp(step - 1)
+                hidden(step + 2)
+                arguments(step - 2)
+                turn_inputs(step + 3)
+                if step >= 1:
+                    log_denominator(step - 1)
+            clamp(BLOCKS - 1)
+            arguments(BLOCKS - 2)
+            arguments(BLOCKS - 1)
+            log_denominator(BLOCKS - 1)
 
         wide = ctx.enter_context(tc.tile_pool(name="wide", bufs=3))
         side = ctx.enter_context(tc.tile_pool(name="side", bufs=2))
+        late = ctx.enter_context(tc.tile_pool(name="late", bufs=3))
         fin = ctx.enter_context(tc.tile_pool(name="fin", bufs=2))
+        banks["mm"] = ctx.enter_context(tc.psum_pool(name="mm2", bufs=4))
+        banks["tr"] = ctx.enter_context(tc.psum_pool(name="tr2", bufs=4))
+        terms, gates, gains, shifts, gated_gains, gain_xs, factors, turned = {}, {}, {}, {}, {}, {}, {}, {}
+
+        def exponentials(blk):
+            if blk < BLOCKS:
+                terms[blk] = wide.tile([P, LS, BLOCK], F32, name="terms")
+                nc.scalar.activation(out=terms[blk][:], in_=z1s[blk][:], func=ACT.Exp, bias=minus_one_col[:], scale=1.0)
 
         def side_sections(blk):
-            x_t, h_codes, h_scales = prepared[blk]
-            gate = side.tile([P, BLOCK], F32)
-            eps_ps = subnet(EPS, h_codes, h_scales)
-            nc.scalar.activation(out=gate[:], in_=eps_ps[:], func=ACT.Tanh, bias=half_eps_bias[:], scale=0.05)
-            gain = side.tile([P, BLOCK], F32)
-            alpha_ps = subnet(ALPHA, h_codes, h_scales)
-            nc.scalar.activation(out=gain[:], in_=alpha_ps[:], func=ACT.Exp, bias=alpha_bias[:], scale=0.1)
-            shift = side.tile([P, BLOCK], F32)
-            bias2_ps = subnet(BIAS2, h_codes, h_scales)
-            nc.scalar.activation(out=shift[:], in_=bias2_ps[:], func=ACT.Identity, bias=bias_of(BIAS2), scale=1.0)
-            nc.scalar.activation(
-                out=ln_den[:, block_cols(blk)], in_=ln_den[:, block_cols(blk)], func=ACT.Exp, bias=ln_04_col[:], scale=-1.0
-            )
-            gated_gain = side.tile([P, BLOCK], F32)
-            nc.vector.scalar_tensor_tensor(
-                out=gated_gain[:], in0=gate[:], scalar=1.0, in1=gain[:], op0=ALU.add, op1=ALU.mult
-            )
-            gain_x = side.tile([P, BLOCK], F32)
-            nc.gpsimd.tensor_tensor(out=gain_x[:], in0=gain[:], in1=x_t[:], op=ALU.mult)
-            return gated_gain, shift, gain_x
+            if blk < BLOCKS:
+                gates[blk] = side.tile([P, BLOCK], F32, name="gate")
+                eps_ps = subnet(EPS, codes_of[blk], scales_of[blk])
+                nc.scalar.activation(out=gates[blk][:], in_=eps_ps[:], func=ACT.Tanh, bias=half_eps_bias[:], scale=0.05)
+                gains[blk] = side.tile([P, BLOCK], F32, name="gain")
+                alpha_ps = subnet(ALPHA, codes_of[blk], scales_of[blk])
+                nc.scalar.activation(out=gains[blk][:], in_=alpha_ps[:], func=ACT.Exp, bias=alpha_bias[:], scale=0.1)
+                shifts[blk] = late.tile([P, BLOCK], F32, name="shift")
+                bias2_ps = subnet(BIAS2, codes_of[blk], scales_of[blk])
+                nc.scalar.activation(out=shifts[blk][:], in_=bias2_ps[:], func=ACT.Identity, bias=bias_of(BIAS2), scale=1.0)
+                nc.scalar.activation(
+                    out=ln_den[:, block_cols(blk)], in_=ln_den[:, block_cols(blk)], func=ACT.Exp, bias=ln_04_col[:], scale=-1.0
+                )
+                gain_xs[blk] = late.tile([P, BLOCK], F32, name="gain_x")
+                nc.gpsimd.tensor_tensor(out=gain_xs[blk][:], in0=gains[blk][:], in1=x_ts[blk][:], op=ALU.mult)
 
-        def elu_terms(blk):
-            mat2, z1, relus = made[blk]
-            terms = wide.tile([P, LS, BLOCK], F32)
-            nc.scalar.activation(out=terms[:], in_=z1[:], func=ACT.Exp, bias=minus_one_col[:], scale=1.0)
-            nc.vector.scalar_tensor_tensor(out=terms[:], in0=z1[:], scalar=1.0, in1=terms[:], op0=ALU.max, op1=ALU.min)
-            nc.vector.scalar_tensor_tensor(out=terms[:], in0=terms[:], scalar=-1.0, in1=mat2[:], op0=ALU.add, op1=ALU.mult)
-            return terms
+        def gate_gain(blk):
+            if blk < BLOCKS:
+                gated_gains[blk] = late.tile([P, BLOCK], F32, name="gated_gain")
+                nc.vector.scalar_tensor_tensor(
+                    out=gated_gains[blk][:], in0=gates[blk][:], scalar=1.0, in1=gains[blk][:], op0=ALU.add, op1=ALU.mult
+                )
 
-        def finish(blk, terms, sides):
-            gated_gain, shift, gain_x = sides
-            factor = fin.tile([P, BLOCK], F32)
-            gated_t = turned_sum([gated_gain[:]])
-            nc.vector.tensor_tensor(out=factor[:], in0=gated_t[:], in1=ln_den[:, block_cols(blk)], op=ALU.mult)
-            num_t = turned_sum([terms[:, l, :] for l in range(LS)])
-            nc.vector.tensor_tensor(out=factor[:], in0=num_t[:], in1=factor[:], op=ALU.mult)
-            offset_t = turned_sum([shift[:], gain_x[:]])
-            result = fin.tile([P, SUBS, DIM], F32)
-            nc.vector.tensor_tensor(
-                out=result[:].rearrange("p s d -> p (s d)"), in0=offset_t[:], in1=factor[:], op=ALU.add
-            )
-            nc.sync.dma_start(out=out_view[:, blk * SUBS : (blk + 1) * SUBS, :], in_=result[:])
+        def elu_plus_1(blk):
+            if blk < BLOCKS:
+                nc.vector.scalar_tensor_tensor(
+                    out=terms[blk][:], in0=z1s[blk][:], scalar=1.0, in1=terms[blk][:], op0=ALU.max, op1=ALU.min
+                )
 
-        done = []
+        def times_mat2_again(blk):
+            if blk < BLOCKS:
+                nc.vector.scalar_tensor_tensor(
+                    out=terms[blk][:], in0=terms[blk][:], scalar=-1.0, in1=mat2s[blk][:], op0=ALU.add, op1=ALU.mult
+                )
+
+        def turn_all(blk):
+            if blk >= 0:
+                turned[blk] = (
+                    turned_sum([gated_gains[blk][:]]),
+                    turned_sum([terms[blk][:, l, :] for l in range(LS)]),
+                    turned_sum([shifts[blk][:], gain_xs[blk][:]]),
+                )
+
+        def finish(blk, stage):
+            if blk >= 0:
+                if stage == 0:
+                    factors[blk] = fin.tile([P, BLOCK], F32, name="factor")
+                    nc.vector.tensor_tensor(out=factors[blk][:], in0=turned[blk][0][:], in1=ln_den[:, block_cols(blk)], op=ALU.mult)
+                if stage == 1:
+                    nc.vector.tensor_tensor(out=factors[blk][:], in0=turned[blk][1][:], in1=factors[blk][:], op=ALU.mult)
+                if stage == 2:
+                    result = fin.tile([P, SUBS, DIM], F32)
+                    nc.vector.tensor_tensor(
+                        out=result[:].rearrange("p s d -> p (s d)"), in0=turned[blk][2][:], in1=factors[blk][:], op=ALU.add
+                    )
+                    nc.sync.dma_start(out=out_view[:, blk * SUBS : (blk + 1) * SUBS, :], in_=result[:])
+
+        exponentials(0)
+        side_sections(0)
         for step in range(BLOCKS + 1):
-            if step < BLOCKS:
-                sides = side_sections(step)
-                done.append((elu_terms(step), sides))
-            if step >= 1:
-                finish(step - 1, done[step - 1][0], done[step - 1][1])
+            turn_all(step - 1)
+            side_sections(step + 1)
+            exponentials(step + 1)
+            elu_plus_1(step)
+            if step == 0:
+                gate_gain(0)
+            finish(step - 1, 0)
+            times_mat2_again(step)
+            finish(step - 1, 1)
+            gate_gain(step + 1)
+            finish(step - 1, 2)

@@ -127,8 +127,8 @@ def tile_cn_pa_t_kernel(tc, x, cond, W1, b1, W2_words, W2_scales, b2, out):
         def bias_of(col_tile):
             return b2_col[:, col_tile : col_tile + 1]
 
-        def turned_sum(addends):
-            turned = banks["tr"].tile([P, BLOCK], F32, tag="tr")
+        def turned_sum(addends, pool="tr"):
+            turned = banks[pool].tile([P, BLOCK], F32, tag=pool)
             for s in range(SUBS):
                 sub = slice(s * P, (s + 1) * P)
                 for n, rows in enumerate(addends):
@@ -283,10 +283,10 @@ def tile_cn_pa_t_kernel(tc, x, cond, W1, b1, W2_words, W2_scales, b2, out):
         wide = ctx.enter_context(tc.tile_pool(name="wide", bufs=3))
         side = ctx.enter_context(tc.tile_pool(name="side", bufs=2))
         late = ctx.enter_context(tc.tile_pool(name="late", bufs=3))
-        fin = ctx.enter_context(tc.tile_pool(name="fin", bufs=2))
+        fin = ctx.enter_context(tc.tile_pool(name="fin", bufs=3))
         banks["mm"] = ctx.enter_context(tc.psum_pool(name="mm2", bufs=4))
         banks["tr"] = ctx.enter_context(tc.psum_pool(name="tr2", bufs=4))
-        terms, gates, gains, shifts, gated_gains, gain_xs, factors, turned = {}, {}, {}, {}, {}, {}, {}, {}
+        terms, gates, gains, shifts, gated_gains, factors, turned = {}, {}, {}, {}, {}, {}, {}
 
         def exponentials(blk):
             if blk < BLOCKS:
@@ -295,7 +295,7 @@ def tile_cn_pa_t_kernel(tc, x, cond, W1, b1, W2_words, W2_scales, b2, out):
 
         def side_sections(blk):
             if blk < BLOCKS:
-                gates[blk] = side.tile([P, BLOCK], F32, name="gate")
+                gates[blk] = late.tile([P, BLOCK], F32, name="gate")
                 eps_ps = subnet(EPS, codes_of[blk], scales_of[blk])
                 nc.scalar.activation(out=gates[blk][:], in_=eps_ps[:], func=ACT.Tanh, bias=half_eps_bias[:], scale=0.05)
                 gains[blk] = side.tile([P, BLOCK], F32, name="gain")
@@ -307,8 +307,6 @@ def tile_cn_pa_t_kernel(tc, x, cond, W1, b1, W2_words, W2_scales, b2, out):
                 nc.scalar.activation(
                     out=ln_den[:, block_cols(blk)], in_=ln_den[:, block_cols(blk)], func=ACT.Exp, bias=ln_04_col[:], scale=-1.0
                 )
-                gain_xs[blk] = late.tile([P, BLOCK], F32, name="gain_x")
-                nc.gpsimd.tensor_tensor(out=gain_xs[blk][:], in0=gains[blk][:], in1=x_ts[blk][:], op=ALU.mult)
 
         def gate_gain(blk):
             if blk < BLOCKS:
@@ -316,52 +314,57 @@ def tile_cn_pa_t_kernel(tc, x, cond, W1, b1, W2_words, W2_scales, b2, out):
                 nc.vector.scalar_tensor_tensor(
                     out=gated_gains[blk][:], in0=gates[blk][:], scalar=1.0, in1=gains[blk][:], op0=ALU.add, op1=ALU.mult
                 )
+                nc.gpsimd.tensor_tensor(out=gates[blk][:], in0=gains[blk][:], in1=x_ts[blk][:], op=ALU.mult)
 
-        def elu_plus_1(blk):
+        def elu_plus_1(blk, ls):
             if blk < BLOCKS:
                 nc.vector.scalar_tensor_tensor(
-                    out=terms[blk][:], in0=z1s[blk][:], scalar=1.0, in1=terms[blk][:], op0=ALU.max, op1=ALU.min
+                    out=terms[blk][:, ls, :], in0=z1s[blk][:, ls, :], scalar=1.0, in1=terms[blk][:, ls, :], op0=ALU.max, op1=ALU.min
                 )
 
-        def times_mat2_again(blk):
+        def times_mat2_again(blk, ls):
             if blk < BLOCKS:
                 nc.vector.scalar_tensor_tensor(
-                    out=terms[blk][:], in0=terms[blk][:], scalar=-1.0, in1=mat2s[blk][:], op0=ALU.add, op1=ALU.mult
+                    out=terms[blk][:, ls, :], in0=terms[blk][:, ls, :], scalar=-1.0, in1=mat2s[blk][:, ls, :], op0=ALU.add, op1=ALU.mult
                 )
 
-        def turn_all(blk):
+        def turn_factor(blk):
+            if blk < BLOCKS:
+                turned[(blk, 0)] = turned_sum([gated_gains[blk][:]])
+
+        def turn_sums(blk):
             if blk >= 0:
-                turned[blk] = (
-                    turned_sum([gated_gains[blk][:]]),
-                    turned_sum([terms[blk][:, l, :] for l in range(LS)]),
-                    turned_sum([shifts[blk][:], gain_xs[blk][:]]),
-                )
+                turned[(blk, 1)] = turned_sum([terms[blk][:, l, :] for l in range(LS)])
+                turned[(blk, 2)] = turned_sum([shifts[blk][:], gates[blk][:]])
 
         def finish(blk, stage):
-            if blk >= 0:
+            if 0 <= blk < BLOCKS:
                 if stage == 0:
                     factors[blk] = fin.tile([P, BLOCK], F32, name="factor")
-                    nc.vector.tensor_tensor(out=factors[blk][:], in0=turned[blk][0][:], in1=ln_den[:, block_cols(blk)], op=ALU.mult)
+                    nc.vector.tensor_tensor(out=factors[blk][:], in0=turned[(blk, 0)][:], in1=ln_den[:, block_cols(blk)], op=ALU.mult)
                 if stage == 1:
-                    nc.vector.tensor_tensor(out=factors[blk][:], in0=turned[blk][1][:], in1=factors[blk][:], op=ALU.mult)
+                    nc.vector.tensor_tensor(out=factors[blk][:], in0=turned[(blk, 1)][:], in1=factors[blk][:], op=ALU.mult)
                 if stage == 2:
                     result = fin.tile([P, SUBS, DIM], F32)
                     nc.vector.tensor_tensor(
-                        out=result[:].rearrange("p s d -> p (s d)"), in0=turned[blk][2][:], in1=factors[blk][:], op=ALU.add
+                        out=result[:].rearrange("p s d -> p (s d)"), in0=turned[(blk, 2)][:], in1=factors[blk][:], op=ALU.add
                     )
                     nc.sync.dma_start(out=out_view[:, blk * SUBS : (blk + 1) * SUBS, :], in_=result[:])
 
+        first_ls, last_l = slice(0, LS - 1), slice(LS - 1, LS)
         exponentials(0)
         side_sections(0)
+        gate_gain(0)
         for step in range(BLOCKS + 1):
-            turn_all(step - 1)
             side_sections(step + 1)
             exponentials(step + 1)
-            elu_plus_1(step)
-            if step == 0:
-                gate_gain(0)
-            finish(step - 1, 0)
-            times_mat2_again(step)
-            finish(step - 1, 1)
+            turn_sums(step - 1)
+            turn_factor(step)
+            elu_plus_1(step, first_ls)
+            elu_plus_1(step, last_l)
+            times_mat2_again(step, first_ls)
+            times_mat2_again(step, last_l)
             gate_gain(step + 1)
+            finish(step - 1, 1)
+            finish(step, 0)
             finish(step - 1, 2)

@@ -151,6 +151,7 @@ def tile_cn_pa_t_kernel(tc, x, cond, W1, b1, W2_words, W2_scales, b2, out):
             loads = phase.enter_context(tc.tile_pool(name="loads", bufs=BLOCKS))
             prep = phase.enter_context(tc.tile_pool(name="prep", bufs=2))
             work = phase.enter_context(tc.tile_pool(name="work", bufs=3))
+            single = phase.enter_context(tc.tile_pool(name="single", bufs=1))
             banks["mm"] = phase.enter_context(tc.psum_pool(name="mm1", bufs=6))
             banks["tr"] = phase.enter_context(tc.psum_pool(name="tr1", bufs=1))
             psum_tp = phase.enter_context(tc.psum_pool(name="tp1", bufs=1))
@@ -182,17 +183,25 @@ def tile_cn_pa_t_kernel(tc, x, cond, W1, b1, W2_words, W2_scales, b2, out):
                     for t in range(PACK):
                         h_ps = banks["mm"].tile([P, BLOCK], F32, tag="mm")
                         nc.tensor.matmul(out=h_ps[:], lhsT=w1_by_t[:, t, :], rhs=cond_ts[blk][:], start=True, stop=True)
-                        nc.scalar.activation(
-                            out=h_rows[blk][:, t, :], in_=h_ps[:], func=ACT.Relu, bias=b1_col[:, t : t + 1], scale=1.0
-                        )
+                        if t < PACK - 1:
+                            nc.scalar.activation(
+                                out=h_rows[blk][:, t, :], in_=h_ps[:], func=ACT.Relu, bias=b1_col[:, t : t + 1], scale=1.0
+                            )
+                        else:
+                            nc.vector.tensor_scalar(
+                                out=h_rows[blk][:, t, :], in0=h_ps[:], scalar1=b1_col[:, t : t + 1], scalar2=0.0, op0=ALU.add, op1=ALU.max
+                            )
 
             def group_words(blk):
                 if blk < BLOCKS:
-                    h_groups[blk] = prep.tile([P, BLOCK, PACK], BF16, align_bytes=64, name="h_grouped")
-                    nc.vector.tensor_copy(
-                        out=h_groups[blk][:].rearrange("p (c i) t -> p c t i", i=4),
-                        in_=h_rows[blk][:].rearrange("p t (c i) -> p c t i", i=4),
-                    )
+                    h_groups[blk] = single.tile([P, BLOCK, PACK], BF16, align_bytes=64, name="h_grouped")
+                    if blk == 0:
+                        nc.vector.tensor_copy(
+                            out=h_groups[blk][:].rearrange("p (c i) t -> p c t i", i=4),
+                            in_=h_rows[blk][:].rearrange("p t (c i) -> p c t i", i=4),
+                        )
+                    else:
+                        nc.gpsimd.tensor_copy(out=h_groups[blk][:], in_=h_rows[blk][:].rearrange("p t c -> p c t"))
 
             def quantise(blk):
                 if blk < BLOCKS:
@@ -249,6 +258,7 @@ def tile_cn_pa_t_kernel(tc, x, cond, W1, b1, W2_words, W2_scales, b2, out):
             quantise(0)
             turn_inputs(1)
             hidden(1)
+            group_words(1)
             turn_inputs(2)
             for step in range(BLOCKS):
                 mat2s[step] = kept.tile([P, LS, BLOCK], F32, name="mat2")
@@ -261,7 +271,6 @@ def tile_cn_pa_t_kernel(tc, x, cond, W1, b1, W2_words, W2_scales, b2, out):
                 mat1_1 = subnet(MAT1 + 1, codes_of[step], scales_of[step])
                 times_x(step, 1, mat1_1)
                 times_mat2(step, 0, mat1_0)
-                group_words(step + 1)
                 mat2_of(step, 2)
                 mat1_2 = subnet(MAT1 + 2, codes_of[step], scales_of[step])
                 times_x(step, 2, mat1_2)
@@ -271,6 +280,7 @@ def tile_cn_pa_t_kernel(tc, x, cond, W1, b1, W2_words, W2_scales, b2, out):
                 if step >= 1:
                     clamp(step - 1)
                 hidden(step + 2)
+                group_words(step + 2)
                 arguments(step - 2)
                 turn_inputs(step + 3)
                 if step >= 1:

@@ -67,6 +67,7 @@ def tile_cn_pa_t_kernel(tc, x, cond, W1, b1, W2_words, W2_scales, b2, out):
         minus_one_col = const.tile([P, 1], F32)
         ln_04_col = const.tile([P, 1], F32)
         ln_den = const.tile([P, BATCH], F32)
+        last_relus = const.tile([P, LS, BLOCK], F32)
 
         def load_weights():
             nc.vector.memset(w2_scales[:].bitcast(I32), 0)
@@ -164,18 +165,16 @@ def tile_cn_pa_t_kernel(tc, x, cond, W1, b1, W2_words, W2_scales, b2, out):
                 x_rows[blk] = loads.tile([P, SUBS, DIM], BF16, name="x_rows")
                 nc.sync.dma_start(out=x_rows[blk][:], in_=x_view[:, subs, :])
 
-            def transpose_rows(rows, dest):
-                turned = psum_tp.tile([P, BLOCK], BF16, tag="tp")
-                for s in range(SUBS):
-                    nc.tensor.transpose(turned[:, s * P : (s + 1) * P], rows[:, s, :], ident_bf[:])
-                nc.scalar.copy(out=dest, in_=turned[:])
-
             def turn_inputs(blk):
                 if blk < BLOCKS:
+                    turned = psum_tp.tile([P, 2, BLOCK], BF16, tag="tp")
+                    for half, rows in enumerate((cond_rows[blk], x_rows[blk])):
+                        for s in range(SUBS):
+                            nc.tensor.transpose(turned[:, half, s * P : (s + 1) * P], rows[:, s, :], ident_bf[:])
                     cond_ts[blk] = prep.tile([P, BLOCK], BF16, name="cond_t")
-                    transpose_rows(cond_rows[blk], cond_ts[blk][:])
+                    nc.scalar.copy(out=cond_ts[blk][:], in_=turned[:, 0, :])
                     x_ts[blk] = kept.tile([P, BLOCK], BF16, name="x_t")
-                    transpose_rows(x_rows[blk], x_ts[blk][:])
+                    nc.scalar.copy(out=x_ts[blk][:], in_=turned[:, 1, :])
 
             def hidden(blk):
                 if blk < BLOCKS:
@@ -263,7 +262,7 @@ def tile_cn_pa_t_kernel(tc, x, cond, W1, b1, W2_words, W2_scales, b2, out):
             for step in range(BLOCKS):
                 mat2s[step] = kept.tile([P, LS, BLOCK], F32, name="mat2")
                 z1s[step] = kept.tile([P, LS, BLOCK], F32, name="z1")
-                relus[step] = work.tile([P, LS, BLOCK], F32, name="relus")
+                relus[step] = work.tile([P, LS, BLOCK], F32, name="relus") if step < BLOCKS - 1 else last_relus
                 mat2_of(step, 0)
                 mat1_0 = subnet(MAT1, codes_of[step], scales_of[step])
                 times_x(step, 0, mat1_0)
@@ -285,10 +284,8 @@ def tile_cn_pa_t_kernel(tc, x, cond, W1, b1, W2_words, W2_scales, b2, out):
                 turn_inputs(step + 3)
                 if step >= 1:
                     log_denominator(step - 1)
-            clamp(BLOCKS - 1)
             arguments(BLOCKS - 2)
             arguments(BLOCKS - 1)
-            log_denominator(BLOCKS - 1)
 
         wide = ctx.enter_context(tc.tile_pool(name="wide", bufs=3))
         side = ctx.enter_context(tc.tile_pool(name="side", bufs=2))
@@ -364,16 +361,23 @@ def tile_cn_pa_t_kernel(tc, x, cond, W1, b1, W2_words, W2_scales, b2, out):
         first_ls, last_l = slice(0, LS - 1), slice(LS - 1, LS)
         exponentials(0)
         side_sections(0)
-        gate_gain(0)
         for step in range(BLOCKS + 1):
             side_sections(step + 1)
             exponentials(step + 1)
+            if step == BLOCKS - 4:
+                clamp(BLOCKS - 1)
+            if step == BLOCKS - 3:
+                log_denominator(BLOCKS - 1)
             turn_sums(step - 1)
-            turn_factor(step)
+            if step > 0:
+                turn_factor(step)
             elu_plus_1(step, first_ls)
             elu_plus_1(step, last_l)
             times_mat2_again(step, first_ls)
             times_mat2_again(step, last_l)
+            if step == 0:
+                gate_gain(0)
+                turn_factor(0)
             gate_gain(step + 1)
             finish(step - 1, 1)
             finish(step, 0)

@@ -75,8 +75,6 @@ def tile_cn_pa_t_kernel(tc, x, cond, W1, b1, W2_words, W2_scales, b2, out):
             nc.vector.memset(minus_one_col[:], -1.0)
             nc.sync.dma_start(out=w1_rows[:], in_=W1)
             nc.sync.dma_start(out=b1_bf[:], in_=b1.rearrange("(p t) -> p t", t=PACK))
-            nc.sync.dma_start(out=b2_dl[:, :, 0:LS], in_=b2[0 : 3 * DL].rearrange("(s d l) -> d s l", s=3, l=LS))
-            nc.sync.dma_start(out=b2_rows[0:COL_TILES, :], in_=b2.rearrange("(r q) -> r q", q=P))
             for quad in range(4):
                 nc.sync.dma_start(
                     out=w2_scales[32 * quad : 32 * quad + 4, :].bitcast(I32),
@@ -86,6 +84,9 @@ def tile_cn_pa_t_kernel(tc, x, cond, W1, b1, W2_words, W2_scales, b2, out):
                 out=w2_codes[:].bitcast(I32),
                 in_=W2_words[0].rearrange("p n t -> p (n t)").bitcast(I32),
             )
+            load_x(0)
+            nc.sync.dma_start(out=b2_dl[:, :, 0:LS], in_=b2[0 : 3 * DL].rearrange("(s d l) -> d s l", s=3, l=LS))
+            nc.sync.dma_start(out=b2_rows[0:COL_TILES, :], in_=b2.rearrange("(r q) -> r q", q=P))
             nc.vector.tensor_copy(out=w1_by_t[:], in_=w1_rows[:].rearrange("d (p t) -> d t p", t=PACK))
             nc.vector.tensor_copy(out=b1_col[:], in_=b1_bf[:])
 
@@ -158,23 +159,29 @@ def tile_cn_pa_t_kernel(tc, x, cond, W1, b1, W2_words, W2_scales, b2, out):
             psum_tp = phase.enter_context(tc.psum_pool(name="tp1", bufs=1))
             cond_rows, x_rows, cond_ts, h_rows, h_groups, relus = {}, {}, {}, {}, {}, {}
 
-            def load_block(blk):
-                subs = slice(blk * SUBS, (blk + 1) * SUBS)
+            def load_cond(blk):
                 cond_rows[blk] = loads.tile([P, SUBS, DIM], BF16, name="cond_rows")
-                nc.sync.dma_start(out=cond_rows[blk][:], in_=cond_view[:, subs, :])
-                x_rows[blk] = loads.tile([P, SUBS, DIM], BF16, name="x_rows")
-                nc.sync.dma_start(out=x_rows[blk][:], in_=x_view[:, subs, :])
+                nc.sync.dma_start(out=cond_rows[blk][:], in_=cond_view[:, blk * SUBS : (blk + 1) * SUBS, :])
 
-            def turn_inputs(blk):
+            def load_x(blk):
+                x_rows[blk] = loads.tile([P, SUBS, DIM], BF16, name="x_rows")
+                nc.sync.dma_start(out=x_rows[blk][:], in_=x_view[:, blk * SUBS : (blk + 1) * SUBS, :])
+
+            def turn_inputs(blk, with_cond=True, with_x=True):
                 if blk < BLOCKS:
+                    pairs = ()
+                    if with_cond:
+                        cond_ts[blk] = prep.tile([P, BLOCK], BF16, name="cond_t")
+                        pairs = pairs + ((cond_rows[blk], cond_ts[blk]),)
+                    if with_x:
+                        x_ts[blk] = kept.tile([P, BLOCK], BF16, name="x_t")
+                        pairs = pairs + ((x_rows[blk], x_ts[blk]),)
                     turned = psum_tp.tile([P, 2, BLOCK], BF16, tag="tp")
-                    for half, rows in enumerate((cond_rows[blk], x_rows[blk])):
+                    for half, (rows, dest) in enumerate(pairs):
                         for s in range(SUBS):
                             nc.tensor.transpose(turned[:, half, s * P : (s + 1) * P], rows[:, s, :], ident_bf[:])
-                    cond_ts[blk] = prep.tile([P, BLOCK], BF16, name="cond_t")
-                    nc.scalar.copy(out=cond_ts[blk][:], in_=turned[:, 0, :])
-                    x_ts[blk] = kept.tile([P, BLOCK], BF16, name="x_t")
-                    nc.scalar.copy(out=x_ts[blk][:], in_=turned[:, 1, :])
+                    for half, (rows, dest) in enumerate(pairs):
+                        nc.scalar.copy(out=dest[:], in_=turned[:, half, :])
 
             def hidden(blk):
                 if blk < BLOCKS:
@@ -243,17 +250,18 @@ def tile_cn_pa_t_kernel(tc, x, cond, W1, b1, W2_words, W2_scales, b2, out):
                 den_t = turned_sum([relus[blk][:, l, :] for l in range(LS)])
                 nc.scalar.activation(out=ln_den[:, block_cols(blk)], in_=den_t[:], func=ACT.Ln, bias=one_col[:], scale=1.0)
 
-            load_block(0)
+            load_cond(0)
             load_weights()
             for blk in range(1, BLOCKS):
-                load_block(blk)
-            turn_inputs(0)
-            hidden(0)
-            bias_columns()
+                load_cond(blk)
+                load_x(blk)
+            turn_inputs(0, with_x=False)
             sort_by_l(2)
             sort_by_l(0)
+            hidden(0)
+            turn_inputs(0, with_cond=False)
+            bias_columns()
             group_words(0)
-            sort_by_l(1)
             quantise(0)
             turn_inputs(1)
             hidden(1)
@@ -276,6 +284,8 @@ def tile_cn_pa_t_kernel(tc, x, cond, W1, b1, W2_words, W2_scales, b2, out):
                 times_mat2(step, 1, mat1_1)
                 times_mat2(step, 2, mat1_2)
                 quantise(step + 1)
+                if step == 0:
+                    sort_by_l(1)
                 if step >= 1:
                     clamp(step - 1)
                 hidden(step + 2)
@@ -300,7 +310,7 @@ def tile_cn_pa_t_kernel(tc, x, cond, W1, b1, W2_words, W2_scales, b2, out):
                 terms[blk] = wide.tile([P, LS, BLOCK], F32, name="terms")
                 nc.scalar.activation(out=terms[blk][:], in_=z1s[blk][:], func=ACT.Exp, bias=minus_one_col[:], scale=1.0)
 
-        def side_sections(blk):
+        def gate_and_gain(blk):
             if blk < BLOCKS:
                 gates[blk] = late.tile([P, BLOCK], F32, name="gate")
                 eps_ps = subnet(EPS, codes_of[blk], scales_of[blk])
@@ -308,6 +318,9 @@ def tile_cn_pa_t_kernel(tc, x, cond, W1, b1, W2_words, W2_scales, b2, out):
                 gains[blk] = side.tile([P, BLOCK], F32, name="gain")
                 alpha_ps = subnet(ALPHA, codes_of[blk], scales_of[blk])
                 nc.scalar.activation(out=gains[blk][:], in_=alpha_ps[:], func=ACT.Exp, bias=alpha_bias[:], scale=0.1)
+
+        def shift_and_denominator(blk):
+            if blk < BLOCKS:
                 shifts[blk] = late.tile([P, BLOCK], F32, name="shift")
                 bias2_ps = subnet(BIAS2, codes_of[blk], scales_of[blk])
                 nc.scalar.activation(out=shifts[blk][:], in_=bias2_ps[:], func=ACT.Identity, bias=bias_of(BIAS2), scale=1.0)
@@ -323,16 +336,16 @@ def tile_cn_pa_t_kernel(tc, x, cond, W1, b1, W2_words, W2_scales, b2, out):
                 )
                 nc.gpsimd.tensor_tensor(out=gates[blk][:], in0=gains[blk][:], in1=x_ts[blk][:], op=ALU.mult)
 
-        def elu_plus_1(blk, ls):
+        def elu_plus_1(blk, cols):
             if blk < BLOCKS:
                 nc.vector.scalar_tensor_tensor(
-                    out=terms[blk][:, ls, :], in0=z1s[blk][:, ls, :], scalar=1.0, in1=terms[blk][:, ls, :], op0=ALU.max, op1=ALU.min
+                    out=terms[blk][:, :, cols], in0=z1s[blk][:, :, cols], scalar=1.0, in1=terms[blk][:, :, cols], op0=ALU.max, op1=ALU.min
                 )
 
-        def times_mat2_again(blk, ls):
+        def times_mat2_again(blk, cols):
             if blk < BLOCKS:
                 nc.vector.scalar_tensor_tensor(
-                    out=terms[blk][:, ls, :], in0=terms[blk][:, ls, :], scalar=-1.0, in1=mat2s[blk][:, ls, :], op0=ALU.add, op1=ALU.mult
+                    out=terms[blk][:, :, cols], in0=terms[blk][:, :, cols], scalar=-1.0, in1=mat2s[blk][:, :, cols], op0=ALU.add, op1=ALU.mult
                 )
 
         def turn_factor(blk):
@@ -358,12 +371,14 @@ def tile_cn_pa_t_kernel(tc, x, cond, W1, b1, W2_words, W2_scales, b2, out):
                     )
                     nc.sync.dma_start(out=out_view[:, blk * SUBS : (blk + 1) * SUBS, :], in_=result[:])
 
-        first_ls, last_l = slice(0, LS - 1), slice(LS - 1, LS)
+        first_half, second_half = slice(0, BLOCK // 2), slice(BLOCK // 2, BLOCK)
         exponentials(0)
-        side_sections(0)
+        gate_and_gain(0)
+        shift_and_denominator(0)
         for step in range(BLOCKS + 1):
-            side_sections(step + 1)
+            gate_and_gain(step + 1)
             exponentials(step + 1)
+            shift_and_denominator(step + 1)
             if step == BLOCKS - 4:
                 clamp(BLOCKS - 1)
             if step == BLOCKS - 3:
@@ -371,10 +386,10 @@ def tile_cn_pa_t_kernel(tc, x, cond, W1, b1, W2_words, W2_scales, b2, out):
             turn_sums(step - 1)
             if step > 0:
                 turn_factor(step)
-            elu_plus_1(step, first_ls)
-            elu_plus_1(step, last_l)
-            times_mat2_again(step, first_ls)
-            times_mat2_again(step, last_l)
+            elu_plus_1(step, first_half)
+            elu_plus_1(step, second_half)
+            times_mat2_again(step, first_half)
+            times_mat2_again(step, second_half)
             if step == 0:
                 gate_gain(0)
                 turn_factor(0)

@@ -283,6 +283,8 @@ def tile_cn_pa_t_kernel(tc, x, cond, W1, b1, W2_words, W2_scales, b2, out):
                 times_x(step, 2, mat1_2)
                 times_mat2(step, 1, mat1_1)
                 times_mat2(step, 2, mat1_2)
+                if step >= 2:
+                    log_denominator(step - 2)
                 quantise(step + 1)
                 if step == 0:
                     sort_by_l(1)
@@ -292,8 +294,7 @@ def tile_cn_pa_t_kernel(tc, x, cond, W1, b1, W2_words, W2_scales, b2, out):
                 group_words(step + 2)
                 arguments(step - 2)
                 turn_inputs(step + 3)
-                if step >= 1:
-                    log_denominator(step - 1)
+            log_denominator(BLOCKS - 2)
             arguments(BLOCKS - 2)
             arguments(BLOCKS - 1)
 
@@ -334,7 +335,8 @@ def tile_cn_pa_t_kernel(tc, x, cond, W1, b1, W2_words, W2_scales, b2, out):
                 nc.vector.scalar_tensor_tensor(
                     out=gated_gains[blk][:], in0=gates[blk][:], scalar=1.0, in1=gains[blk][:], op0=ALU.add, op1=ALU.mult
                 )
-                nc.gpsimd.tensor_tensor(out=gates[blk][:], in0=gains[blk][:], in1=x_ts[blk][:], op=ALU.mult)
+                engine = nc.vector if blk <= 1 else nc.gpsimd
+                engine.tensor_tensor(out=gates[blk][:], in0=gains[blk][:], in1=x_ts[blk][:], op=ALU.mult)
 
         def elu_plus_1(blk, cols):
             if blk < BLOCKS:

@@ -26,6 +26,10 @@ SUBS = 4
 BLOCK = SUBS * P
 BLOCKS = SUBTILES // SUBS
 
+GW = 256
+LO = 0
+HI = 6
+LAG = 2
 FLOPS = 2 * BATCH * DIM * HID + 2 * BATCH * HID * P_COLS
 
 
@@ -300,8 +304,8 @@ def tile_cn_pa_t_kernel(tc, x, cond, W1, b1, W2_words, W2_scales, b2, out):
 
         wide = ctx.enter_context(tc.tile_pool(name="wide", bufs=3))
         side = ctx.enter_context(tc.tile_pool(name="side", bufs=2))
-        late = ctx.enter_context(tc.tile_pool(name="late", bufs=3))
-        fin = ctx.enter_context(tc.tile_pool(name="fin", bufs=3))
+        late = ctx.enter_context(tc.tile_pool(name="late", bufs=4))
+        fin = ctx.enter_context(tc.tile_pool(name="fin", bufs=4))
         banks["mm"] = ctx.enter_context(tc.psum_pool(name="mm2", bufs=4))
         banks["tr"] = ctx.enter_context(tc.psum_pool(name="tr2", bufs=4))
         terms, gates, gains, shifts, gated_gains, factors, turned = {}, {}, {}, {}, {}, {}, {}
@@ -336,7 +340,12 @@ def tile_cn_pa_t_kernel(tc, x, cond, W1, b1, W2_words, W2_scales, b2, out):
                     out=gated_gains[blk][:], in0=gates[blk][:], scalar=1.0, in1=gains[blk][:], op0=ALU.add, op1=ALU.mult
                 )
                 engine = nc.vector if blk <= 1 else nc.gpsimd
-                engine.tensor_tensor(out=gates[blk][:], in0=gains[blk][:], in1=x_ts[blk][:], op=ALU.mult)
+                w = GW if LO <= blk - 2 < HI else BLOCK
+                engine.tensor_tensor(out=gates[blk][:, 0:w], in0=gains[blk][:, 0:w], in1=x_ts[blk][:, 0:w], op=ALU.mult)
+
+        def gain_x_rest(blk):
+            if blk < BLOCKS and LO <= blk - 2 < HI:
+                nc.vector.tensor_tensor(out=gates[blk][:, GW:BLOCK], in0=gains[blk][:, GW:BLOCK], in1=x_ts[blk][:, GW:BLOCK], op=ALU.mult)
 
         def elu_plus_1(blk, cols):
             if blk < BLOCKS:
@@ -357,7 +366,19 @@ def tile_cn_pa_t_kernel(tc, x, cond, W1, b1, W2_words, W2_scales, b2, out):
         def turn_sums(blk):
             if blk >= 0:
                 turned[(blk, 1)] = turned_sum([terms[blk][:, l, :] for l in range(LS)])
-                turned[(blk, 2)] = turned_sum([shifts[blk][:], gates[blk][:]])
+                if not LO <= blk < HI:
+                    turned[(blk, 2)] = turned_sum([shifts[blk][:], gates[blk][:]])
+
+        def store(blk):
+            total = banks["tr"].tile([P, BLOCK], F32, tag="tr")
+            for s in range(SUBS):
+                sub = slice(s * P, (s + 1) * P)
+                nc.tensor.matmul(out=total[:, sub], lhsT=shifts[blk][:, sub], rhs=ident_f32[:], start=True, stop=False, is_transpose=True)
+                nc.tensor.matmul(out=total[:, sub], lhsT=gates[blk][:, sub], rhs=ident_f32[:], start=False, stop=False, is_transpose=True)
+                nc.tensor.matmul(out=total[:, sub], lhsT=ident_f32[:], rhs=factors[blk][:, sub], start=False, stop=True)
+            result = fin.tile([P, SUBS, DIM], F32, name="result")
+            nc.scalar.copy(out=result[:].rearrange("p s d -> p (s d)"), in_=total[:])
+            nc.sync.dma_start(out=out_view[:, blk * SUBS : (blk + 1) * SUBS, :], in_=result[:])
 
         def finish(blk, stage):
             if 0 <= blk < BLOCKS:
@@ -366,8 +387,8 @@ def tile_cn_pa_t_kernel(tc, x, cond, W1, b1, W2_words, W2_scales, b2, out):
                     nc.vector.tensor_tensor(out=factors[blk][:], in0=turned[(blk, 0)][:], in1=ln_den[:, block_cols(blk)], op=ALU.mult)
                 if stage == 1:
                     nc.vector.tensor_tensor(out=factors[blk][:], in0=turned[(blk, 1)][:], in1=factors[blk][:], op=ALU.mult)
-                if stage == 2:
-                    result = fin.tile([P, SUBS, DIM], F32)
+                if stage == 2 and not LO <= blk < HI:
+                    result = fin.tile([P, SUBS, DIM], F32, name="result")
                     nc.vector.tensor_tensor(
                         out=result[:].rearrange("p s d -> p (s d)"), in0=turned[(blk, 2)][:], in1=factors[blk][:], op=ALU.add
                     )
@@ -378,6 +399,8 @@ def tile_cn_pa_t_kernel(tc, x, cond, W1, b1, W2_words, W2_scales, b2, out):
         gate_and_gain(0)
         shift_and_denominator(0)
         for step in range(BLOCKS + 1):
+            if LO <= step - 1 - LAG < HI:
+                store(step - 1 - LAG)
             gate_and_gain(step + 1)
             exponentials(step + 1)
             shift_and_denominator(step + 1)
@@ -399,3 +422,4 @@ def tile_cn_pa_t_kernel(tc, x, cond, W1, b1, W2_words, W2_scales, b2, out):
             finish(step - 1, 1)
             finish(step, 0)
             finish(step - 1, 2)
+            gain_x_rest(step + 1)

@@ -30,6 +30,14 @@ GW = 256
 LO = 0
 HI = 6
 LAG = 2
+HV = (0,1)
+FV = {b: 1 for b in range(6)}
+ARGS = {1: [0], 2: [1], 3: [2], 4: [3], 5: [4], 6: [5], 7: [6], 8: [7]}
+QE = (0,)
+DEF = 2
+CL = {6: 3, 7: 4}
+LG = {6: 5, 7: 5}
+RC = {6: 5, 7: 6}
 FLOPS = 2 * BATCH * DIM * HID + 2 * BATCH * HID * P_COLS
 
 
@@ -71,7 +79,9 @@ def tile_cn_pa_t_kernel(tc, x, cond, W1, b1, W2_words, W2_scales, b2, out):
         minus_one_col = const.tile([P, 1], F32)
         ln_04_col = const.tile([P, 1], F32)
         ln_den = const.tile([P, BATCH], F32)
-        last_relus = const.tile([P, LS, BLOCK], F32)
+        late_relus = {}
+        for late_blk in range(BLOCKS - DEF, BLOCKS):
+            late_relus[late_blk] = const.tile([P, LS, BLOCK], F32, name="late_relus%d" % late_blk)
 
         def load_weights():
             nc.vector.memset(w2_scales[:].bitcast(I32), 0)
@@ -193,7 +203,7 @@ def tile_cn_pa_t_kernel(tc, x, cond, W1, b1, W2_words, W2_scales, b2, out):
                     for t in range(PACK):
                         h_ps = banks["mm"].tile([P, BLOCK], F32, tag="mm")
                         nc.tensor.matmul(out=h_ps[:], lhsT=w1_by_t[:, t, :], rhs=cond_ts[blk][:], start=True, stop=True)
-                        if t < PACK - 1:
+                        if t < PACK - 1 or blk not in HV:
                             nc.scalar.activation(
                                 out=h_rows[blk][:, t, :], in_=h_ps[:], func=ACT.Relu, bias=b1_col[:, t : t + 1], scale=1.0
                             )
@@ -248,7 +258,16 @@ def tile_cn_pa_t_kernel(tc, x, cond, W1, b1, W2_words, W2_scales, b2, out):
                         )
 
             def clamp(blk):
-                nc.scalar.activation(out=relus[blk][:], in_=relus[blk][:], func=ACT.Relu, scale=-1.0)
+                e = LS - FV.get(blk, 0)
+                if e:
+                    nc.scalar.activation(out=relus[blk][:, 0:e, :], in_=relus[blk][:, 0:e, :], func=ACT.Relu, scale=-1.0)
+
+            def clamp_v(blk):
+                e = LS - FV.get(blk, 0)
+                if e < LS:
+                    nc.vector.tensor_scalar(
+                        out=relus[blk][:, e:LS, :], in0=relus[blk][:, e:LS, :], scalar1=-1.0, scalar2=0.0, op0=ALU.mult, op1=ALU.max
+                    )
 
             def log_denominator(blk):
                 den_t = turned_sum([relus[blk][:, l, :] for l in range(LS)])
@@ -274,7 +293,7 @@ def tile_cn_pa_t_kernel(tc, x, cond, W1, b1, W2_words, W2_scales, b2, out):
             for step in range(BLOCKS):
                 mat2s[step] = kept.tile([P, LS, BLOCK], F32, name="mat2")
                 z1s[step] = kept.tile([P, LS, BLOCK], F32, name="z1")
-                relus[step] = work.tile([P, LS, BLOCK], F32, name="relus") if step < BLOCKS - 1 else last_relus
+                relus[step] = work.tile([P, LS, BLOCK], F32, name="relus") if step < BLOCKS - DEF else late_relus[step]
                 mat2_of(step, 0)
                 mat1_0 = subnet(MAT1, codes_of[step], scales_of[step])
                 times_x(step, 0, mat1_0)
@@ -285,22 +304,31 @@ def tile_cn_pa_t_kernel(tc, x, cond, W1, b1, W2_words, W2_scales, b2, out):
                 mat2_of(step, 2)
                 mat1_2 = subnet(MAT1 + 2, codes_of[step], scales_of[step])
                 times_x(step, 2, mat1_2)
+                if step in QE:
+                    if 0 <= step - 1 < BLOCKS - DEF:
+                        clamp_v(step - 1)
+                    quantise(step + 1)
                 times_mat2(step, 1, mat1_1)
                 times_mat2(step, 2, mat1_2)
-                if step >= 2:
+                if 0 <= step - 2 < BLOCKS - DEF:
                     log_denominator(step - 2)
-                quantise(step + 1)
+                if step not in QE:
+                    if 0 <= step - 1 < BLOCKS - DEF:
+                        clamp_v(step - 1)
+                    quantise(step + 1)
                 if step == 0:
                     sort_by_l(1)
-                if step >= 1:
+                if 0 <= step - 1 < BLOCKS - DEF:
                     clamp(step - 1)
                 hidden(step + 2)
                 group_words(step + 2)
-                arguments(step - 2)
+                for late in ARGS.get(step, []):
+                    arguments(late)
                 turn_inputs(step + 3)
-            log_denominator(BLOCKS - 2)
-            arguments(BLOCKS - 2)
-            arguments(BLOCKS - 1)
+            if DEF < 2:
+                log_denominator(BLOCKS - 2)
+            for late in ARGS.get(BLOCKS, []):
+                arguments(late)
 
         wide = ctx.enter_context(tc.tile_pool(name="wide", bufs=3))
         side = ctx.enter_context(tc.tile_pool(name="side", bufs=2))
@@ -329,9 +357,13 @@ def tile_cn_pa_t_kernel(tc, x, cond, W1, b1, W2_words, W2_scales, b2, out):
                 shifts[blk] = late.tile([P, BLOCK], F32, name="shift")
                 bias2_ps = subnet(BIAS2, codes_of[blk], scales_of[blk])
                 nc.scalar.activation(out=shifts[blk][:], in_=bias2_ps[:], func=ACT.Identity, bias=bias_of(BIAS2), scale=1.0)
-                nc.scalar.activation(
-                    out=ln_den[:, block_cols(blk)], in_=ln_den[:, block_cols(blk)], func=ACT.Exp, bias=ln_04_col[:], scale=-1.0
-                )
+                if blk < BLOCKS - DEF:
+                    scaled_reciprocal(blk)
+
+        def scaled_reciprocal(blk):
+            nc.scalar.activation(
+                out=ln_den[:, block_cols(blk)], in_=ln_den[:, block_cols(blk)], func=ACT.Exp, bias=ln_04_col[:], scale=-1.0
+            )
 
         def gate_gain(blk):
             if blk < BLOCKS:
@@ -404,10 +436,15 @@ def tile_cn_pa_t_kernel(tc, x, cond, W1, b1, W2_words, W2_scales, b2, out):
             gate_and_gain(step + 1)
             exponentials(step + 1)
             shift_and_denominator(step + 1)
-            if step == BLOCKS - 4:
-                clamp(BLOCKS - 1)
-            if step == BLOCKS - 3:
-                log_denominator(BLOCKS - 1)
+            for lb in range(BLOCKS - DEF, BLOCKS):
+                if CL[lb] == step:
+                    clamp(lb)
+            for lb in range(BLOCKS - DEF, BLOCKS):
+                if LG[lb] == step:
+                    log_denominator(lb)
+            for lb in range(BLOCKS - DEF, BLOCKS):
+                if RC[lb] == step:
+                    scaled_reciprocal(lb)
             turn_sums(step - 1)
             if step > 0:
                 turn_factor(step)

@@ -26,25 +26,26 @@ SUBS = 4
 BLOCK = SUBS * P
 BLOCKS = SUBTILES // SUBS
 
-GW = 256
+GW = 384
 LO = 0
 HI = 6
 LAG = 2
-HV = (0,1)
+SG = {5: (0,1,2)}
+HV = (2,)
 FV = {b: 1 for b in range(6)}
 ARGS = {1: [0], 2: [1], 3: [2], 4: [3], 5: [4], 6: [5], 7: [6], 8: [7]}
-QE = (0,)
+QE = (0, 6)
 DEF = 2
-CL = {6: 3, 7: 4}
-LG = {6: 5, 7: 5}
-RC = {6: 5, 7: 6}
+CL = {6:3,7:4}
+LG = {6:5,7:5}
+RC = {6:5,7:6}
 FLOPS = 2 * BATCH * DIM * HID + 2 * BATCH * HID * P_COLS
 
 
 def tile_cn_pa_t_kernel(tc, x, cond, W1, b1, W2_words, W2_scales, b2, out):
     nc = tc.nc
     with ExitStack() as ctx:
-        ctx.enter_context(tc.manual_schedule(engines={mybir.EngineType.Activation, mybir.EngineType.DVE}))
+        ctx.enter_context(tc.manual_schedule())
         const = ctx.enter_context(tc.tile_pool(name="const", bufs=1))
         kept = ctx.enter_context(tc.tile_pool(name="kept", bufs=BLOCKS))
         banks = {}
@@ -58,9 +59,7 @@ def tile_cn_pa_t_kernel(tc, x, cond, W1, b1, W2_words, W2_scales, b2, out):
         warm = const.tile([P, 1], F32)
         nc.scalar.activation(out=warm[:], in_=one_col[:], func=ACT.Ln)
         ident_bf = const.tile([P, P], BF16)
-        make_identity(nc, ident_bf[:])
         ident_f32 = const.tile([P, P], F32)
-        make_identity(nc, ident_f32[:])
 
         w1_rows = const.tile([P, HID], BF16)
         w1_by_t = const.tile([P, PACK, P], BF16)
@@ -114,15 +113,18 @@ def tile_cn_pa_t_kernel(tc, x, cond, W1, b1, W2_words, W2_scales, b2, out):
             nc.vector.tensor_scalar_mul(out=alpha_bias[:], in0=b2_col[:, ALPHA : ALPHA + 1], scalar1=0.1)
             nc.vector.tensor_scalar_mul(out=ln_04_col[:], in0=one_col[:], scalar1=math.log(0.4))
 
+        def sort_scales_by_l(section):
+            cols = slice(section * DL, (section + 1) * DL)
+            nc.gpsimd.tensor_copy(
+                out=scales_by_l[:, cols].rearrange("p (l d) -> p l d", l=LS),
+                in_=w2_scales[:, cols].rearrange("p (d l) -> p l d", l=LS),
+            )
+
         def sort_by_l(section):
             cols = slice(section * DL, (section + 1) * DL)
             nc.vector.tensor_copy(
                 out=codes_by_l[:, cols].bitcast(I32).rearrange("p (l d) -> p l d", l=LS),
                 in_=w2_codes[:, cols].bitcast(I32).rearrange("p (d l) -> p l d", l=LS),
-            )
-            nc.vector.tensor_copy(
-                out=scales_by_l[:, cols].rearrange("p (l d) -> p l d", l=LS),
-                in_=w2_scales[:, cols].rearrange("p (d l) -> p l d", l=LS),
             )
 
         def subnet(col_tile, h_codes, h_scales):
@@ -173,13 +175,13 @@ def tile_cn_pa_t_kernel(tc, x, cond, W1, b1, W2_words, W2_scales, b2, out):
             psum_tp = phase.enter_context(tc.psum_pool(name="tp1", bufs=1))
             cond_rows, x_rows, cond_ts, h_rows, h_groups, relus = {}, {}, {}, {}, {}, {}
 
-            def load_cond(blk):
+            def load_cond(blk, queue=nc.sync):
                 cond_rows[blk] = loads.tile([P, SUBS, DIM], BF16, name="cond_rows")
-                nc.sync.dma_start(out=cond_rows[blk][:], in_=cond_view[:, blk * SUBS : (blk + 1) * SUBS, :])
+                queue.dma_start(out=cond_rows[blk][:], in_=cond_view[:, blk * SUBS : (blk + 1) * SUBS, :])
 
-            def load_x(blk):
+            def load_x(blk, queue=nc.sync):
                 x_rows[blk] = loads.tile([P, SUBS, DIM], BF16, name="x_rows")
-                nc.sync.dma_start(out=x_rows[blk][:], in_=x_view[:, blk * SUBS : (blk + 1) * SUBS, :])
+                queue.dma_start(out=x_rows[blk][:], in_=x_view[:, blk * SUBS : (blk + 1) * SUBS, :])
 
             def turn_inputs(blk, with_cond=True, with_x=True):
                 if blk < BLOCKS:
@@ -203,7 +205,7 @@ def tile_cn_pa_t_kernel(tc, x, cond, W1, b1, W2_words, W2_scales, b2, out):
                     for t in range(PACK):
                         h_ps = banks["mm"].tile([P, BLOCK], F32, tag="mm")
                         nc.tensor.matmul(out=h_ps[:], lhsT=w1_by_t[:, t, :], rhs=cond_ts[blk][:], start=True, stop=True)
-                        if t < PACK - 1 or blk not in HV:
+                        if (t < PACK - 1 or blk not in HV) and (blk > 0 or t % 2 == 0):
                             nc.scalar.activation(
                                 out=h_rows[blk][:, t, :], in_=h_ps[:], func=ACT.Relu, bias=b1_col[:, t : t + 1], scale=1.0
                             )
@@ -253,6 +255,11 @@ def tile_cn_pa_t_kernel(tc, x, cond, W1, b1, W2_words, W2_scales, b2, out):
                 if 0 <= blk < BLOCKS:
                     for l in range(LS):
                         bias1_ps = subnet(BIAS1 + l, codes_of[blk], scales_of[blk])
+                        if l in SG.get(blk, ()):
+                            bias1_sb = work.tile([P, BLOCK], F32, name="bias1_sb")
+                            nc.scalar.activation(out=bias1_sb[:], in_=bias1_ps[:], func=ACT.Identity, bias=bias1_plus_1[:, l : l + 1], scale=1.0)
+                            nc.gpsimd.tensor_tensor(out=z1s[blk][:, l, :], in0=z1s[blk][:, l, :], in1=bias1_sb[:], op=ALU.add)
+                            continue
                         nc.vector.scalar_tensor_tensor(
                             out=z1s[blk][:, l, :], in0=bias1_ps[:], scalar=bias1_plus_1[:, l : l + 1], in1=z1s[blk][:, l, :], op0=ALU.add, op1=ALU.add
                         )
@@ -273,23 +280,28 @@ def tile_cn_pa_t_kernel(tc, x, cond, W1, b1, W2_words, W2_scales, b2, out):
                 den_t = turned_sum([relus[blk][:, l, :] for l in range(LS)])
                 nc.scalar.activation(out=ln_den[:, block_cols(blk)], in_=den_t[:], func=ACT.Ln, bias=one_col[:], scale=1.0)
 
+            load_cond(1, nc.gpsimd)
+            make_identity(nc, ident_bf[:])
+            make_identity(nc, ident_f32[:])
             load_cond(0)
             load_weights()
-            for blk in range(1, BLOCKS):
+            load_x(1)
+            for blk in range(2, BLOCKS):
                 load_cond(blk)
                 load_x(blk)
             turn_inputs(0, with_x=False)
-            sort_by_l(2)
-            sort_by_l(0)
+            for section in (2, 0, 1):
+                sort_scales_by_l(section)
             hidden(0)
-            turn_inputs(0, with_cond=False)
-            bias_columns()
+            turn_inputs(1, with_x=False)
             group_words(0)
+            sort_by_l(2)
             quantise(0)
-            turn_inputs(1)
             hidden(1)
+            bias_columns()
+            turn_inputs(0, with_cond=False)
+            sort_by_l(0)
             group_words(1)
-            turn_inputs(2)
             for step in range(BLOCKS):
                 mat2s[step] = kept.tile([P, LS, BLOCK], F32, name="mat2")
                 z1s[step] = kept.tile([P, LS, BLOCK], F32, name="z1")
@@ -320,6 +332,9 @@ def tile_cn_pa_t_kernel(tc, x, cond, W1, b1, W2_words, W2_scales, b2, out):
                     sort_by_l(1)
                 if 0 <= step - 1 < BLOCKS - DEF:
                     clamp(step - 1)
+                if step == 0:
+                    turn_inputs(1, with_cond=False)
+                    turn_inputs(2)
                 hidden(step + 2)
                 group_words(step + 2)
                 for late in ARGS.get(step, []):
@@ -446,6 +461,8 @@ def tile_cn_pa_t_kernel(tc, x, cond, W1, b1, W2_words, W2_scales, b2, out):
                 if RC[lb] == step:
                     scaled_reciprocal(lb)
             turn_sums(step - 1)
+            if step == BLOCKS and HI == BLOCKS - 1:
+                store(BLOCKS - 2)
             if step > 0:
                 turn_factor(step)
             elu_plus_1(step, first_half)

@@ -26,15 +26,16 @@ SUBS = 4
 BLOCK = SUBS * P
 BLOCKS = SUBTILES // SUBS
 
-GW = 384
+GW = 256
 LO = 0
 HI = 6
 LAG = 2
-SG = {5: (0,1,2)}
+CS = 768
+SG = {}
 HV = (2,)
 FV = {b: 1 for b in range(6)}
 ARGS = {1: [0], 2: [1], 3: [2], 4: [3], 5: [4], 6: [5], 7: [6], 8: [7]}
-QE = (0, 6)
+QE = (0,)
 DEF = 2
 CL = {6:3,7:4}
 LG = {6:5,7:5}
@@ -59,7 +60,9 @@ def tile_cn_pa_t_kernel(tc, x, cond, W1, b1, W2_words, W2_scales, b2, out):
         warm = const.tile([P, 1], F32)
         nc.scalar.activation(out=warm[:], in_=one_col[:], func=ACT.Ln)
         ident_bf = const.tile([P, P], BF16)
+        make_identity(nc, ident_bf[:])
         ident_f32 = const.tile([P, P], F32)
+        make_identity(nc, ident_f32[:])
 
         w1_rows = const.tile([P, HID], BF16)
         w1_by_t = const.tile([P, PACK, P], BF16)
@@ -97,7 +100,7 @@ def tile_cn_pa_t_kernel(tc, x, cond, W1, b1, W2_words, W2_scales, b2, out):
                 out=w2_codes[:].bitcast(I32),
                 in_=W2_words[0].rearrange("p n t -> p (n t)").bitcast(I32),
             )
-            load_x(0)
+            load_pair("x", 0)
             nc.sync.dma_start(out=b2_dl[:, :, 0:LS], in_=b2[0 : 3 * DL].rearrange("(s d l) -> d s l", s=3, l=LS))
             nc.sync.dma_start(out=b2_rows[0:COL_TILES, :], in_=b2.rearrange("(r q) -> r q", q=P))
             nc.vector.tensor_copy(out=w1_by_t[:], in_=w1_rows[:].rearrange("d (p t) -> d t p", t=PACK))
@@ -115,7 +118,7 @@ def tile_cn_pa_t_kernel(tc, x, cond, W1, b1, W2_words, W2_scales, b2, out):
 
         def sort_scales_by_l(section):
             cols = slice(section * DL, (section + 1) * DL)
-            nc.gpsimd.tensor_copy(
+            nc.vector.tensor_copy(
                 out=scales_by_l[:, cols].rearrange("p (l d) -> p l d", l=LS),
                 in_=w2_scales[:, cols].rearrange("p (d l) -> p l d", l=LS),
             )
@@ -166,7 +169,7 @@ def tile_cn_pa_t_kernel(tc, x, cond, W1, b1, W2_words, W2_scales, b2, out):
         x_ts, codes_of, scales_of, mat2s, z1s = {}, {}, {}, {}, {}
 
         with ExitStack() as phase:
-            loads = phase.enter_context(tc.tile_pool(name="loads", bufs=BLOCKS))
+            loads = phase.enter_context(tc.tile_pool(name="loads", bufs=BLOCKS // 2))
             prep = phase.enter_context(tc.tile_pool(name="prep", bufs=2))
             work = phase.enter_context(tc.tile_pool(name="work", bufs=3))
             single = phase.enter_context(tc.tile_pool(name="single", bufs=1))
@@ -175,13 +178,12 @@ def tile_cn_pa_t_kernel(tc, x, cond, W1, b1, W2_words, W2_scales, b2, out):
             psum_tp = phase.enter_context(tc.psum_pool(name="tp1", bufs=1))
             cond_rows, x_rows, cond_ts, h_rows, h_groups, relus = {}, {}, {}, {}, {}, {}
 
-            def load_cond(blk, queue=nc.sync):
-                cond_rows[blk] = loads.tile([P, SUBS, DIM], BF16, name="cond_rows")
-                queue.dma_start(out=cond_rows[blk][:], in_=cond_view[:, blk * SUBS : (blk + 1) * SUBS, :])
-
-            def load_x(blk, queue=nc.sync):
-                x_rows[blk] = loads.tile([P, SUBS, DIM], BF16, name="x_rows")
-                queue.dma_start(out=x_rows[blk][:], in_=x_view[:, blk * SUBS : (blk + 1) * SUBS, :])
+            def load_pair(kind, pair):
+                rows, view = (cond_rows, cond_view) if kind == "cond" else (x_rows, x_view)
+                both = loads.tile([P, 2 * SUBS, DIM], BF16, name=kind + "_rows")
+                nc.sync.dma_start(out=both[:], in_=view[:, 2 * pair * SUBS : 2 * (pair + 1) * SUBS, :])
+                for half in range(2):
+                    rows[2 * pair + half] = both[:, half * SUBS : (half + 1) * SUBS, :]
 
             def turn_inputs(blk, with_cond=True, with_x=True):
                 if blk < BLOCKS:
@@ -265,33 +267,28 @@ def tile_cn_pa_t_kernel(tc, x, cond, W1, b1, W2_words, W2_scales, b2, out):
                         )
 
             def clamp(blk):
-                e = LS - FV.get(blk, 0)
+                flat = relus[blk][:].rearrange("p l b -> p (l b)")
+                e = CS if FV.get(blk, 0) else LS * BLOCK
                 if e:
-                    nc.scalar.activation(out=relus[blk][:, 0:e, :], in_=relus[blk][:, 0:e, :], func=ACT.Relu, scale=-1.0)
+                    nc.scalar.activation(out=flat[:, 0:e], in_=flat[:, 0:e], func=ACT.Relu, scale=-1.0)
 
             def clamp_v(blk):
-                e = LS - FV.get(blk, 0)
-                if e < LS:
-                    nc.vector.tensor_scalar(
-                        out=relus[blk][:, e:LS, :], in0=relus[blk][:, e:LS, :], scalar1=-1.0, scalar2=0.0, op0=ALU.mult, op1=ALU.max
-                    )
+                flat = relus[blk][:].rearrange("p l b -> p (l b)")
+                if FV.get(blk, 0):
+                    nc.vector.tensor_scalar(out=flat[:, CS : LS * BLOCK], in0=flat[:, CS : LS * BLOCK], scalar1=-1.0, scalar2=0.0, op0=ALU.mult, op1=ALU.max)
 
             def log_denominator(blk):
                 den_t = turned_sum([relus[blk][:, l, :] for l in range(LS)])
                 nc.scalar.activation(out=ln_den[:, block_cols(blk)], in_=den_t[:], func=ACT.Ln, bias=one_col[:], scale=1.0)
 
-            load_cond(1, nc.gpsimd)
-            make_identity(nc, ident_bf[:])
-            make_identity(nc, ident_f32[:])
-            load_cond(0)
+            load_pair("cond", 0)
             load_weights()
-            load_x(1)
-            for blk in range(2, BLOCKS):
-                load_cond(blk)
-                load_x(blk)
+            for pair in range(1, BLOCKS // 2):
+                load_pair("cond", pair)
+                load_pair("x", pair)
             turn_inputs(0, with_x=False)
-            for section in (2, 0, 1):
-                sort_scales_by_l(section)
+            sort_scales_by_l(2)
+            sort_scales_by_l(0)
             hidden(0)
             turn_inputs(1, with_x=False)
             group_words(0)
@@ -329,6 +326,7 @@ def tile_cn_pa_t_kernel(tc, x, cond, W1, b1, W2_words, W2_scales, b2, out):
                         clamp_v(step - 1)
                     quantise(step + 1)
                 if step == 0:
+                    sort_scales_by_l(1)
                     sort_by_l(1)
                 if 0 <= step - 1 < BLOCKS - DEF:
                     clamp(step - 1)
@@ -461,8 +459,6 @@ def tile_cn_pa_t_kernel(tc, x, cond, W1, b1, W2_words, W2_scales, b2, out):
                 if RC[lb] == step:
                     scaled_reciprocal(lb)
             turn_sums(step - 1)
-            if step == BLOCKS and HI == BLOCKS - 1:
-                store(BLOCKS - 2)
             if step > 0:
                 turn_factor(step)
             elu_plus_1(step, first_half)

@@ -108,7 +108,7 @@ def tile_cn_pa_t_kernel(tc, x, cond, W1, b1, W2_words, W2_scales, b2, out):
 
         def bias_columns():
             nc.vector.tensor_copy(out=b2_col[:, 0 : 3 * LS].rearrange("p (s l) -> p s l", l=LS), in_=b2_dl[:, :, 0:LS])
-            b2_ps = banks["tr"].tile([P, P], BF16, tag="tr")
+            b2_ps = banks["tr"].tile([P, P], BF16, tag="mm")
             nc.tensor.transpose(b2_ps[:], b2_rows[:], ident_bf[:])
             nc.vector.tensor_copy(out=b2_col[:, BIAS2:COL_TILES], in_=b2_ps[:, BIAS2:COL_TILES])
             nc.vector.tensor_scalar_add(out=bias1_plus_1[:], in0=b2_col[:, BIAS1 : BIAS1 + LS], scalar1=1.0)
@@ -149,7 +149,7 @@ def tile_cn_pa_t_kernel(tc, x, cond, W1, b1, W2_words, W2_scales, b2, out):
             return b2_col[:, col_tile : col_tile + 1]
 
         def turned_sum(addends, pool="tr"):
-            turned = banks[pool].tile([P, BLOCK], F32, tag=pool)
+            turned = banks[pool].tile([P, BLOCK], F32, tag="mm" if banks["mm"] is banks["tr"] else pool)
             for s in range(SUBS):
                 sub = slice(s * P, (s + 1) * P)
                 for n, rows in enumerate(addends):
@@ -173,9 +173,7 @@ def tile_cn_pa_t_kernel(tc, x, cond, W1, b1, W2_words, W2_scales, b2, out):
             prep = phase.enter_context(tc.tile_pool(name="prep", bufs=2))
             work = phase.enter_context(tc.tile_pool(name="work", bufs=3))
             single = phase.enter_context(tc.tile_pool(name="single", bufs=1))
-            banks["mm"] = phase.enter_context(tc.psum_pool(name="mm1", bufs=6))
-            banks["tr"] = phase.enter_context(tc.psum_pool(name="tr1", bufs=1))
-            psum_tp = phase.enter_context(tc.psum_pool(name="tp1", bufs=1))
+            banks["mm"] = banks["tr"] = psum_tp = phase.enter_context(tc.psum_pool(name="psum1", bufs=8))
             cond_rows, x_rows, cond_ts, h_rows, h_groups, relus = {}, {}, {}, {}, {}, {}
 
             def load_pair(kind, pair):
@@ -194,7 +192,7 @@ def tile_cn_pa_t_kernel(tc, x, cond, W1, b1, W2_words, W2_scales, b2, out):
                     if with_x:
                         x_ts[blk] = kept.tile([P, BLOCK], BF16, name="x_t")
                         pairs = pairs + ((x_rows[blk], x_ts[blk]),)
-                    turned = psum_tp.tile([P, 2, BLOCK], BF16, tag="tp")
+                    turned = psum_tp.tile([P, 2, BLOCK], BF16, tag="mm")
                     for half, (rows, dest) in enumerate(pairs):
                         for s in range(SUBS):
                             nc.tensor.transpose(turned[:, half, s * P : (s + 1) * P], rows[:, s, :], ident_bf[:])
@@ -347,8 +345,7 @@ def tile_cn_pa_t_kernel(tc, x, cond, W1, b1, W2_words, W2_scales, b2, out):
         side = ctx.enter_context(tc.tile_pool(name="side", bufs=2))
         late = ctx.enter_context(tc.tile_pool(name="late", bufs=4))
         fin = ctx.enter_context(tc.tile_pool(name="fin", bufs=4))
-        banks["mm"] = ctx.enter_context(tc.psum_pool(name="mm2", bufs=4))
-        banks["tr"] = ctx.enter_context(tc.psum_pool(name="tr2", bufs=4))
+        banks["mm"] = banks["tr"] = ctx.enter_context(tc.psum_pool(name="psum2", bufs=8))
         terms, gates, gains, shifts, gated_gains, factors, turned = {}, {}, {}, {}, {}, {}, {}
 
         def exponentials(blk):
@@ -415,7 +412,7 @@ def tile_cn_pa_t_kernel(tc, x, cond, W1, b1, W2_words, W2_scales, b2, out):
                     turned[(blk, 2)] = turned_sum([shifts[blk][:], gates[blk][:]])
 
         def store(blk):
-            total = banks["tr"].tile([P, BLOCK], F32, tag="tr")
+            total = banks["tr"].tile([P, BLOCK], F32, tag="mm")
             for s in range(SUBS):
                 sub = slice(s * P, (s + 1) * P)
                 nc.tensor.matmul(out=total[:, sub], lhsT=shifts[blk][:, sub], rhs=ident_f32[:], start=True, stop=False, is_transpose=True)

@@ -35,9 +35,9 @@ SG = {}
 HV = (2,)
 FV = {b: 1 for b in range(6)}
 ARGS = {1: [0], 2: [1], 3: [2], 4: [3], 5: [4], 6: [5], 7: [6], 8: [7]}
-QE = (0,)
+QE = ()
 DEF = 2
-CL = {6:3,7:4}
+CL = {6:99,7:4}
 LG = {6:5,7:5}
 RC = {6:5,7:6}
 FLOPS = 2 * BATCH * DIM * HID + 2 * BATCH * HID * P_COLS
@@ -50,13 +50,19 @@ def tile_cn_pa_t_kernel(tc, x, cond, W1, b1, W2_words, W2_scales, b2, out):
         const = ctx.enter_context(tc.tile_pool(name="const", bufs=1))
         kept = ctx.enter_context(tc.tile_pool(name="kept", bufs=BLOCKS))
         banks = {}
+        banks["mm"] = banks["tr"] = ctx.enter_context(tc.psum_pool(name="psum", bufs=8))
 
         cond_view = cond.rearrange("(p i) d -> p i d", i=SUBTILES)
         x_view = x.rearrange("(p i) d -> p i d", i=SUBTILES)
         out_view = out.rearrange("(p i) d -> p i d", i=SUBTILES)
 
+        zeros = const.tile([P, BLOCK // 2], BF16)
+        nc.vector.memset(zeros[:], 0.0)
         one_col = const.tile([P, 1], F32)
         nc.vector.memset(one_col[:], 1.0)
+        unread = banks["mm"].tile([P, BLOCK // 2], F32, tag="mm")
+        for n in range(6):
+            nc.tensor.matmul(out=unread[:], lhsT=zeros[:, 0:P], rhs=zeros[:], start=True, stop=True)
         warm = const.tile([P, 1], F32)
         nc.scalar.activation(out=warm[:], in_=one_col[:], func=ACT.Ln)
         ident_bf = const.tile([P, P], BF16)
@@ -89,6 +95,7 @@ def tile_cn_pa_t_kernel(tc, x, cond, W1, b1, W2_words, W2_scales, b2, out):
             nc.vector.memset(w2_scales[:].bitcast(I32), 0)
             nc.vector.memset(b2_rows[:], 0.0)
             nc.vector.memset(minus_one_col[:], -1.0)
+            nc.vector.tensor_scalar_mul(out=ln_04_col[:], in0=one_col[:], scalar1=math.log(0.4))
             nc.sync.dma_start(out=w1_rows[:], in_=W1)
             nc.sync.dma_start(out=b1_bf[:], in_=b1.rearrange("(p t) -> p t", t=PACK))
             for quad in range(4):
@@ -106,15 +113,16 @@ def tile_cn_pa_t_kernel(tc, x, cond, W1, b1, W2_words, W2_scales, b2, out):
             nc.vector.tensor_copy(out=w1_by_t[:], in_=w1_rows[:].rearrange("d (p t) -> d t p", t=PACK))
             nc.vector.tensor_copy(out=b1_col[:], in_=b1_bf[:])
 
-        def bias_columns():
+        def early_bias_columns():
             nc.vector.tensor_copy(out=b2_col[:, 0 : 3 * LS].rearrange("p (s l) -> p s l", l=LS), in_=b2_dl[:, :, 0:LS])
+            nc.vector.tensor_scalar_add(out=bias1_plus_1[:], in0=b2_col[:, BIAS1 : BIAS1 + LS], scalar1=1.0)
+
+        def bias_columns():
             b2_ps = banks["tr"].tile([P, P], BF16, tag="mm")
             nc.tensor.transpose(b2_ps[:], b2_rows[:], ident_bf[:])
             nc.vector.tensor_copy(out=b2_col[:, BIAS2:COL_TILES], in_=b2_ps[:, BIAS2:COL_TILES])
-            nc.vector.tensor_scalar_add(out=bias1_plus_1[:], in0=b2_col[:, BIAS1 : BIAS1 + LS], scalar1=1.0)
-            nc.vector.tensor_scalar_mul(out=half_eps_bias[:], in0=b2_col[:, EPS : EPS + 1], scalar1=0.05)
-            nc.vector.tensor_scalar_mul(out=alpha_bias[:], in0=b2_col[:, ALPHA : ALPHA + 1], scalar1=0.1)
-            nc.vector.tensor_scalar_mul(out=ln_04_col[:], in0=one_col[:], scalar1=math.log(0.4))
+            nc.gpsimd.tensor_scalar_mul(out=half_eps_bias[:], in0=b2_col[:, EPS : EPS + 1], scalar1=0.05)
+            nc.gpsimd.tensor_scalar_mul(out=alpha_bias[:], in0=b2_col[:, ALPHA : ALPHA + 1], scalar1=0.1)
 
         def sort_scales_by_l(section):
             cols = slice(section * DL, (section + 1) * DL)
@@ -173,7 +181,7 @@ def tile_cn_pa_t_kernel(tc, x, cond, W1, b1, W2_words, W2_scales, b2, out):
             prep = phase.enter_context(tc.tile_pool(name="prep", bufs=2))
             work = phase.enter_context(tc.tile_pool(name="work", bufs=3))
             single = phase.enter_context(tc.tile_pool(name="single", bufs=1))
-            banks["mm"] = banks["tr"] = psum_tp = phase.enter_context(tc.psum_pool(name="psum1", bufs=8))
+            psum_tp = banks["mm"]
             cond_rows, x_rows, cond_ts, h_rows, h_groups, relus = {}, {}, {}, {}, {}, {}
 
             def load_pair(kind, pair):
@@ -199,10 +207,11 @@ def tile_cn_pa_t_kernel(tc, x, cond, W1, b1, W2_words, W2_scales, b2, out):
                     for half, (rows, dest) in enumerate(pairs):
                         nc.scalar.copy(out=dest[:], in_=turned[:, half, :])
 
-            def hidden(blk):
+            def hidden(blk, ts=range(PACK)):
                 if blk < BLOCKS:
-                    h_rows[blk] = prep.tile([P, PACK, BLOCK], BF16, name="h_rows")
-                    for t in range(PACK):
+                    if 0 in ts:
+                        h_rows[blk] = prep.tile([P, PACK, BLOCK], BF16, name="h_rows")
+                    for t in ts:
                         h_ps = banks["mm"].tile([P, BLOCK], F32, tag="mm")
                         nc.tensor.matmul(out=h_ps[:], lhsT=w1_by_t[:, t, :], rhs=cond_ts[blk][:], start=True, stop=True)
                         if (t < PACK - 1 or blk not in HV) and (blk > 0 or t % 2 == 0):
@@ -251,9 +260,9 @@ def tile_cn_pa_t_kernel(tc, x, cond, W1, b1, W2_words, W2_scales, b2, out):
                     out=relus[blk][:, l, :], in0=mat1_ps[:], scalar=bias_of(MAT1 + l), in1=mat2s[blk][:, l, :], op0=ALU.add, op1=ALU.mult
                 )
 
-            def arguments(blk):
+            def arguments(blk, ls=range(LS)):
                 if 0 <= blk < BLOCKS:
-                    for l in range(LS):
+                    for l in ls:
                         bias1_ps = subnet(BIAS1 + l, codes_of[blk], scales_of[blk])
                         if l in SG.get(blk, ()):
                             bias1_sb = work.tile([P, BLOCK], F32, name="bias1_sb")
@@ -292,15 +301,18 @@ def tile_cn_pa_t_kernel(tc, x, cond, W1, b1, W2_words, W2_scales, b2, out):
             group_words(0)
             sort_by_l(2)
             quantise(0)
-            hidden(1)
-            bias_columns()
+            hidden(1, (0, 1))
             turn_inputs(0, with_cond=False)
+            hidden(1, (2, 3))
             sort_by_l(0)
+            early_bias_columns()
             group_words(1)
             for step in range(BLOCKS):
                 mat2s[step] = kept.tile([P, LS, BLOCK], F32, name="mat2")
                 z1s[step] = kept.tile([P, LS, BLOCK], F32, name="z1")
                 relus[step] = work.tile([P, LS, BLOCK], F32, name="relus") if step < BLOCKS - DEF else late_relus[step]
+                if step == BLOCKS - 1:
+                    clamp(step - 1)
                 mat2_of(step, 0)
                 mat1_0 = subnet(MAT1, codes_of[step], scales_of[step])
                 times_x(step, 0, mat1_0)
@@ -317,8 +329,6 @@ def tile_cn_pa_t_kernel(tc, x, cond, W1, b1, W2_words, W2_scales, b2, out):
                     quantise(step + 1)
                 times_mat2(step, 1, mat1_1)
                 times_mat2(step, 2, mat1_2)
-                if 0 <= step - 2 < BLOCKS - DEF:
-                    log_denominator(step - 2)
                 if step not in QE:
                     if 0 <= step - 1 < BLOCKS - DEF:
                         clamp_v(step - 1)
@@ -329,23 +339,23 @@ def tile_cn_pa_t_kernel(tc, x, cond, W1, b1, W2_words, W2_scales, b2, out):
                 if 0 <= step - 1 < BLOCKS - DEF:
                     clamp(step - 1)
                 if step == 0:
+                    bias_columns()
                     turn_inputs(1, with_cond=False)
                     turn_inputs(2)
+                if 0 <= step - 2 < BLOCKS - DEF:
+                    log_denominator(step - 2)
+                turn_inputs(step + 3)
                 hidden(step + 2)
                 group_words(step + 2)
                 for late in ARGS.get(step, []):
                     arguments(late)
-                turn_inputs(step + 3)
             if DEF < 2:
                 log_denominator(BLOCKS - 2)
-            for late in ARGS.get(BLOCKS, []):
-                arguments(late)
 
         wide = ctx.enter_context(tc.tile_pool(name="wide", bufs=3))
         side = ctx.enter_context(tc.tile_pool(name="side", bufs=2))
         late = ctx.enter_context(tc.tile_pool(name="late", bufs=4))
         fin = ctx.enter_context(tc.tile_pool(name="fin", bufs=4))
-        banks["mm"] = banks["tr"] = ctx.enter_context(tc.psum_pool(name="psum2", bufs=8))
         terms, gates, gains, shifts, gated_gains, factors, turned = {}, {}, {}, {}, {}, {}, {}
 
         def exponentials(blk):
@@ -381,7 +391,7 @@ def tile_cn_pa_t_kernel(tc, x, cond, W1, b1, W2_words, W2_scales, b2, out):
                 nc.vector.scalar_tensor_tensor(
                     out=gated_gains[blk][:], in0=gates[blk][:], scalar=1.0, in1=gains[blk][:], op0=ALU.add, op1=ALU.mult
                 )
-                engine = nc.vector if blk <= 1 else nc.gpsimd
+                engine = nc.vector if blk == 1 else nc.gpsimd
                 w = GW if LO <= blk - 2 < HI else BLOCK
                 engine.tensor_tensor(out=gates[blk][:, 0:w], in0=gains[blk][:, 0:w], in1=x_ts[blk][:, 0:w], op=ALU.mult)
 
@@ -430,16 +440,24 @@ def tile_cn_pa_t_kernel(tc, x, cond, W1, b1, W2_words, W2_scales, b2, out):
                 if stage == 1:
                     nc.vector.tensor_tensor(out=factors[blk][:], in0=turned[(blk, 1)][:], in1=factors[blk][:], op=ALU.mult)
                 if stage == 2 and not LO <= blk < HI:
+                    parts = 2 if blk == BLOCKS - 1 else 1
                     result = fin.tile([P, SUBS, DIM], F32, name="result")
-                    nc.vector.tensor_tensor(
-                        out=result[:].rearrange("p s d -> p (s d)"), in0=turned[(blk, 2)][:], in1=factors[blk][:], op=ALU.add
-                    )
-                    nc.sync.dma_start(out=out_view[:, blk * SUBS : (blk + 1) * SUBS, :], in_=result[:])
+                    for part in range(parts):
+                        subs = slice(part * SUBS // parts, (part + 1) * SUBS // parts)
+                        cols = slice(part * BLOCK // parts, (part + 1) * BLOCK // parts)
+                        nc.vector.tensor_tensor(
+                            out=result[:, subs, :].rearrange("p s d -> p (s d)"), in0=turned[(blk, 2)][:, cols], in1=factors[blk][:, cols], op=ALU.add
+                        )
+                        nc.sync.dma_start(out=out_view[:, blk * SUBS + subs.start : blk * SUBS + subs.stop, :], in_=result[:, subs, :])
 
         first_half, second_half = slice(0, BLOCK // 2), slice(BLOCK // 2, BLOCK)
-        exponentials(0)
         gate_and_gain(0)
+        exponentials(0)
         shift_and_denominator(0)
+        arguments(BLOCKS - 1, (0,))
+        gate_gain(0)
+        arguments(BLOCKS - 1, (1, 2))
+        turn_factor(0)
         for step in range(BLOCKS + 1):
             if LO <= step - 1 - LAG < HI:
                 store(step - 1 - LAG)
@@ -462,9 +480,6 @@ def tile_cn_pa_t_kernel(tc, x, cond, W1, b1, W2_words, W2_scales, b2, out):
             elu_plus_1(step, second_half)
             times_mat2_again(step, first_half)
             times_mat2_again(step, second_half)
-            if step == 0:
-                gate_gain(0)
-                turn_factor(0)
             gate_gain(step + 1)
             finish(step - 1, 1)
             finish(step, 0)

import math
from contextlib import ExitStack

import concourse.mybir as mybir
from concourse.masks import make_identity

F32 = mybir.dt.float32
BF16 = mybir.dt.bfloat16
I32 = mybir.dt.int32
U32 = mybir.dt.uint32
U8 = mybir.dt.uint8
FP8X4 = mybir.dt.float8_e4m3fn_x4
ACT = mybir.ActivationFunctionType
ALU = mybir.AluOpType

P = 128
PACK = 4
BATCH, DIM, HID, LS = 4096, 128, 512, 3
DL = DIM * LS
P_COLS = 3 * DL + 3 * DIM
COL_TILES = P_COLS // P
MAT1, BIAS1, MAT2 = 0, LS, 2 * LS
BIAS2, EPS, ALPHA = 3 * LS, 3 * LS + 1, 3 * LS + 2
SUBTILES = BATCH // P
SUBS = 4
BLOCK = SUBS * P
BLOCKS = SUBTILES // SUBS

GW = 256
LO = 0
HI = 6
LAG = 2
CS = 768
SG = {}
HV = (2,)
FV = {b: 1 for b in range(6)}
ARGS = {1: [0], 2: [1], 3: [2], 4: [3], 5: [4], 6: [5], 7: [6], 8: [7]}
QE = ()
DEF = 2
CL = {6:99,7:4}
LG = {6:5,7:5}
RC = {6:5,7:6}
FLOPS = 2 * BATCH * DIM * HID + 2 * BATCH * HID * P_COLS


def tile_cn_pa_t_kernel(tc, x, cond, W1, b1, W2_words, W2_scales, b2, out):
    nc = tc.nc
    with ExitStack() as ctx:
        ctx.enter_context(tc.manual_schedule())
        const = ctx.enter_context(tc.tile_pool(name="const", bufs=1))
        kept = ctx.enter_context(tc.tile_pool(name="kept", bufs=BLOCKS))
        banks = {}
        banks["mm"] = banks["tr"] = ctx.enter_context(tc.psum_pool(name="psum", bufs=8))

        cond_view = cond.rearrange("(p i) d -> p i d", i=SUBTILES)
        x_view = x.rearrange("(p i) d -> p i d", i=SUBTILES)
        out_view = out.rearrange("(p i) d -> p i d", i=SUBTILES)

        zeros = const.tile([P, BLOCK // 2], BF16)
        nc.vector.memset(zeros[:], 0.0)
        one_col = const.tile([P, 1], F32)
        nc.vector.memset(one_col[:], 1.0)
        unread = banks["mm"].tile([P, BLOCK // 2], F32, tag="mm")
        for n in range(6):
            nc.tensor.matmul(out=unread[:], lhsT=zeros[:, 0:P], rhs=zeros[:], start=True, stop=True)
        warm = const.tile([P, 1], F32)
        nc.scalar.activation(out=warm[:], in_=one_col[:], func=ACT.Ln)
        ident_bf = const.tile([P, P], BF16)
        make_identity(nc, ident_bf[:])
        ident_f32 = const.tile([P, P], F32)
        make_identity(nc, ident_f32[:])

        w1_rows = const.tile([P, HID], BF16)
        w1_by_t = const.tile([P, PACK, P], BF16)
        b1_bf = const.tile([P, PACK], BF16)
        b1_col = const.tile([P, PACK], F32)
        w2_scales = const.tile([P, P_COLS], U8, align_bytes=64)
        w2_codes = const.tile([P, P_COLS], U32, align_bytes=64)
        codes_by_l = const.tile([P, 3 * DL], U32, align_bytes=64)
        scales_by_l = const.tile([P, 3 * DL], U8, align_bytes=64)
        b2_col = const.tile([P, COL_TILES], F32)
        b2_dl = const.tile([P, 3, PACK], BF16)
        b2_rows = const.tile([P, P], BF16)
        bias1_plus_1 = const.tile([P, LS], F32)
        half_eps_bias = const.tile([P, 1], F32)
        alpha_bias = const.tile([P, 1], F32)
        minus_one_col = const.tile([P, 1], F32)
        ln_04_col = const.tile([P, 1], F32)
        ln_den = const.tile([P, BATCH], F32)
        late_relus = {}
        for late_blk in range(BLOCKS - DEF, BLOCKS):
            late_relus[late_blk] = const.tile([P, LS, BLOCK], F32, name="late_relus%d" % late_blk)

        def load_weights():
            nc.vector.memset(w2_scales[:].bitcast(I32), 0)
            nc.vector.memset(b2_rows[:], 0.0)
            nc.vector.memset(minus_one_col[:], -1.0)
            nc.vector.tensor_scalar_mul(out=ln_04_col[:], in0=one_col[:], scalar1=math.log(0.4))
            nc.sync.dma_start(out=w1_rows[:], in_=W1)
            nc.sync.dma_start(out=b1_bf[:], in_=b1.rearrange("(p t) -> p t", t=PACK))
            for quad in range(4):
                nc.sync.dma_start(
                    out=w2_scales[32 * quad : 32 * quad + 4, :].bitcast(I32),
                    in_=W2_scales[0, 4 * quad : 4 * quad + 4, :].bitcast(I32),
                )
            nc.sync.dma_start(
                out=w2_codes[:].bitcast(I32),
                in_=W2_words[0].rearrange("p n t -> p (n t)").bitcast(I32),
            )
            load_pair("x", 0)
            nc.sync.dma_start(out=b2_dl[:, :, 0:LS], in_=b2[0 : 3 * DL].rearrange("(s d l) -> d s l", s=3, l=LS))
            nc.sync.dma_start(out=b2_rows[0:COL_TILES, :], in_=b2.rearrange("(r q) -> r q", q=P))
            nc.vector.tensor_copy(out=w1_by_t[:], in_=w1_rows[:].rearrange("d (p t) -> d t p", t=PACK))
            nc.vector.tensor_copy(out=b1_col[:], in_=b1_bf[:])

        def early_bias_columns():
            nc.vector.tensor_copy(out=b2_col[:, 0 : 3 * LS].rearrange("p (s l) -> p s l", l=LS), in_=b2_dl[:, :, 0:LS])
            nc.vector.tensor_scalar_add(out=bias1_plus_1[:], in0=b2_col[:, BIAS1 : BIAS1 + LS], scalar1=1.0)

        def bias_columns():
            b2_ps = banks["tr"].tile([P, P], BF16, tag="mm")
            nc.tensor.transpose(b2_ps[:], b2_rows[:], ident_bf[:])
            nc.vector.tensor_copy(out=b2_col[:, BIAS2:COL_TILES], in_=b2_ps[:, BIAS2:COL_TILES])
            nc.gpsimd.tensor_scalar_mul(out=half_eps_bias[:], in0=b2_col[:, EPS : EPS + 1], scalar1=0.05)
            nc.gpsimd.tensor_scalar_mul(out=alpha_bias[:], in0=b2_col[:, ALPHA : ALPHA + 1], scalar1=0.1)

        def sort_scales_by_l(section):
            cols = slice(section * DL, (section + 1) * DL)
            nc.vector.tensor_copy(
                out=scales_by_l[:, cols].rearrange("p (l d) -> p l d", l=LS),
                in_=w2_scales[:, cols].rearrange("p (d l) -> p l d", l=LS),
            )

        def sort_by_l(section):
            cols = slice(section * DL, (section + 1) * DL)
            nc.vector.tensor_copy(
                out=codes_by_l[:, cols].bitcast(I32).rearrange("p (l d) -> p l d", l=LS),
                in_=w2_codes[:, cols].bitcast(I32).rearrange("p (d l) -> p l d", l=LS),
            )

        def subnet(col_tile, h_codes, h_scales):
            cols = slice(col_tile * P, (col_tile + 1) * P)
            codes, scales = (codes_by_l, scales_by_l) if col_tile < BIAS2 else (w2_codes, w2_scales)
            p_ps = banks["mm"].tile([P, BLOCK], F32, tag="mm")
            nc.tensor.matmul_mx(
                out=p_ps[:],
                lhsT=codes[:, cols].bitcast(FP8X4),
                lhsT_scale=scales[:, cols],
                rhs=h_codes[:].bitcast(FP8X4),
                rhs_scale=h_scales[:],
                start=True,
                stop=True,
            )
            return p_ps

        def bias_of(col_tile):
            return b2_col[:, col_tile : col_tile + 1]

        def turned_sum(addends, pool="tr"):
            turned = banks[pool].tile([P, BLOCK], F32, tag="mm" if banks["mm"] is banks["tr"] else pool)
            for s in range(SUBS):
                sub = slice(s * P, (s + 1) * P)
                for n, rows in enumerate(addends):
                    nc.tensor.matmul(
                        out=turned[:, sub],
                        lhsT=rows[:, sub],
                        rhs=ident_f32[:],
                        start=(n == 0),
                        stop=(n == len(addends) - 1),
                        is_transpose=True,
                    )
            return turned

        def block_cols(blk):
            return slice(blk * BLOCK, (blk + 1) * BLOCK)

        x_ts, codes_of, scales_of, mat2s, z1s = {}, {}, {}, {}, {}

        with ExitStack() as phase:
            loads = phase.enter_context(tc.tile_pool(name="loads", bufs=BLOCKS // 2))
            prep = phase.enter_context(tc.tile_pool(name="prep", bufs=2))
            work = phase.enter_context(tc.tile_pool(name="work", bufs=3))
            single = phase.enter_context(tc.tile_pool(name="single", bufs=1))
            psum_tp = banks["mm"]
            cond_rows, x_rows, cond_ts, h_rows, h_groups, relus = {}, {}, {}, {}, {}, {}

            def load_pair(kind, pair):
                rows, view = (cond_rows, cond_view) if kind == "cond" else (x_rows, x_view)
                both = loads.tile([P, 2 * SUBS, DIM], BF16, name=kind + "_rows")
                nc.sync.dma_start(out=both[:], in_=view[:, 2 * pair * SUBS : 2 * (pair + 1) * SUBS, :])
                for half in range(2):
                    rows[2 * pair + half] = both[:, half * SUBS : (half + 1) * SUBS, :]

            def turn_inputs(blk, with_cond=True, with_x=True):
                if blk < BLOCKS:
                    pairs = ()
                    if with_cond:
                        cond_ts[blk] = prep.tile([P, BLOCK], BF16, name="cond_t")
                        pairs = pairs + ((cond_rows[blk], cond_ts[blk]),)
                    if with_x:
                        x_ts[blk] = kept.tile([P, BLOCK], BF16, name="x_t")
                        pairs = pairs + ((x_rows[blk], x_ts[blk]),)
                    turned = psum_tp.tile([P, 2, BLOCK], BF16, tag="mm")
                    for half, (rows, dest) in enumerate(pairs):
                        for s in range(SUBS):
                            nc.tensor.transpose(turned[:, half, s * P : (s + 1) * P], rows[:, s, :], ident_bf[:])
                    for half, (rows, dest) in enumerate(pairs):
                        nc.scalar.copy(out=dest[:], in_=turned[:, half, :])

            def hidden(blk, ts=range(PACK)):
                if blk < BLOCKS:
                    if 0 in ts:
                        h_rows[blk] = prep.tile([P, PACK, BLOCK], BF16, name="h_rows")
                    for t in ts:
                        h_ps = banks["mm"].tile([P, BLOCK], F32, tag="mm")
                        nc.tensor.matmul(out=h_ps[:], lhsT=w1_by_t[:, t, :], rhs=cond_ts[blk][:], start=True, stop=True)
                        if (t < PACK - 1 or blk not in HV) and (blk > 0 or t % 2 == 0):
                            nc.scalar.activation(
                                out=h_rows[blk][:, t, :], in_=h_ps[:], func=ACT.Relu, bias=b1_col[:, t : t + 1], scale=1.0
                            )
                        else:
                            nc.vector.tensor_scalar(
                                out=h_rows[blk][:, t, :], in0=h_ps[:], scalar1=b1_col[:, t : t + 1], scalar2=0.0, op0=ALU.add, op1=ALU.max
                            )

            def group_words(blk):
                if blk < BLOCKS:
                    h_groups[blk] = single.tile([P, BLOCK, PACK], BF16, align_bytes=64, name="h_grouped")
                    if blk == 0:
                        nc.vector.tensor_copy(
                            out=h_groups[blk][:].rearrange("p (c i) t -> p c t i", i=4),
                            in_=h_rows[blk][:].rearrange("p t (c i) -> p c t i", i=4),
                        )
                    else:
                        nc.gpsimd.tensor_copy(out=h_groups[blk][:], in_=h_rows[blk][:].rearrange("p t c -> p c t"))

            def quantise(blk):
                if blk < BLOCKS:
                    codes_of[blk] = kept.tile([P, BLOCK], U32, align_bytes=64, name="h_codes")
                    scales_of[blk] = kept.tile([P, BLOCK], U8, align_bytes=64, name="h_scales")
                    nc.vector.quantize_mx(
                        out=codes_of[blk][:].bitcast(FP8X4),
                        scales=scales_of[blk][:],
                        in_=h_groups[blk][:].rearrange("p b t -> p (b t)"),
                    )

            def mat2_of(blk, l):
                mat2_ps = subnet(MAT2 + l, codes_of[blk], scales_of[blk])
                nc.scalar.activation(
                    out=mat2s[blk][:, l, :], in_=mat2_ps[:], func=ACT.Identity, bias=bias_of(MAT2 + l), scale=1.0
                )

            def times_x(blk, l, mat1_ps):
                nc.vector.scalar_tensor_tensor(
                    out=z1s[blk][:, l, :], in0=mat1_ps[:], scalar=bias_of(MAT1 + l), in1=x_ts[blk][:], op0=ALU.add, op1=ALU.mult
                )

            def times_mat2(blk, l, mat1_ps):
                nc.vector.scalar_tensor_tensor(
                    out=relus[blk][:, l, :], in0=mat1_ps[:], scalar=bias_of(MAT1 + l), in1=mat2s[blk][:, l, :], op0=ALU.add, op1=ALU.mult
                )

            def arguments(blk, ls=range(LS)):
                if 0 <= blk < BLOCKS:
                    for l in ls:
                        bias1_ps = subnet(BIAS1 + l, codes_of[blk], scales_of[blk])
                        if l in SG.get(blk, ()):
                            bias1_sb = work.tile([P, BLOCK], F32, name="bias1_sb")
                            nc.scalar.activation(out=bias1_sb[:], in_=bias1_ps[:], func=ACT.Identity, bias=bias1_plus_1[:, l : l + 1], scale=1.0)
                            nc.gpsimd.tensor_tensor(out=z1s[blk][:, l, :], in0=z1s[blk][:, l, :], in1=bias1_sb[:], op=ALU.add)
                            continue
                        nc.vector.scalar_tensor_tensor(
                            out=z1s[blk][:, l, :], in0=bias1_ps[:], scalar=bias1_plus_1[:, l : l + 1], in1=z1s[blk][:, l, :], op0=ALU.add, op1=ALU.add
                        )

            def clamp(blk):
                flat = relus[blk][:].rearrange("p l b -> p (l b)")
                e = CS if FV.get(blk, 0) else LS * BLOCK
                if e:
                    nc.scalar.activation(out=flat[:, 0:e], in_=flat[:, 0:e], func=ACT.Relu, scale=-1.0)

            def clamp_v(blk):
                flat = relus[blk][:].rearrange("p l b -> p (l b)")
                if FV.get(blk, 0):
                    nc.vector.tensor_scalar(out=flat[:, CS : LS * BLOCK], in0=flat[:, CS : LS * BLOCK], scalar1=-1.0, scalar2=0.0, op0=ALU.mult, op1=ALU.max)

            def log_denominator(blk):
                den_t = turned_sum([relus[blk][:, l, :] for l in range(LS)])
                nc.scalar.activation(out=ln_den[:, block_cols(blk)], in_=den_t[:], func=ACT.Ln, bias=one_col[:], scale=1.0)

            load_pair("cond", 0)
            load_weights()
            for pair in range(1, BLOCKS // 2):
                load_pair("cond", pair)
                load_pair("x", pair)
            turn_inputs(0, with_x=False)
            sort_scales_by_l(2)
            sort_scales_by_l(0)
            hidden(0)
            turn_inputs(1, with_x=False)
            group_words(0)
            sort_by_l(2)
            quantise(0)
            hidden(1, (0, 1))
            turn_inputs(0, with_cond=False)
            hidden(1, (2, 3))
            sort_by_l(0)
            early_bias_columns()
            group_words(1)
            for step in range(BLOCKS):
                mat2s[step] = kept.tile([P, LS, BLOCK], F32, name="mat2")
                z1s[step] = kept.tile([P, LS, BLOCK], F32, name="z1")
                relus[step] = work.tile([P, LS, BLOCK], F32, name="relus") if step < BLOCKS - DEF else late_relus[step]
                if step == BLOCKS - 1:
                    clamp(step - 1)
                mat2_of(step, 0)
                mat1_0 = subnet(MAT1, codes_of[step], scales_of[step])
                times_x(step, 0, mat1_0)
                mat2_of(step, 1)
                mat1_1 = subnet(MAT1 + 1, codes_of[step], scales_of[step])
                times_x(step, 1, mat1_1)
                times_mat2(step, 0, mat1_0)
                mat2_of(step, 2)
                mat1_2 = subnet(MAT1 + 2, codes_of[step], scales_of[step])
                times_x(step, 2, mat1_2)
                if step in QE:
                    if 0 <= step - 1 < BLOCKS - DEF:
                        clamp_v(step - 1)
                    quantise(step + 1)
                times_mat2(step, 1, mat1_1)
                times_mat2(step, 2, mat1_2)
                if step not in QE:
                    if 0 <= step - 1 < BLOCKS - DEF:
                        clamp_v(step - 1)
                    quantise(step + 1)
                if step == 0:
                    sort_scales_by_l(1)
                    sort_by_l(1)
                if 0 <= step - 1 < BLOCKS - DEF:
                    clamp(step - 1)
                if step == 0:
                    bias_columns()
                    turn_inputs(1, with_cond=False)
                    turn_inputs(2)
                if 0 <= step - 2 < BLOCKS - DEF:
                    log_denominator(step - 2)
                turn_inputs(step + 3)
                hidden(step + 2)
                group_words(step + 2)
                for late in ARGS.get(step, []):
                    arguments(late)
            if DEF < 2:
                log_denominator(BLOCKS - 2)

        wide = ctx.enter_context(tc.tile_pool(name="wide", bufs=3))
        side = ctx.enter_context(tc.tile_pool(name="side", bufs=2))
        late = ctx.enter_context(tc.tile_pool(name="late", bufs=4))
        fin = ctx.enter_context(tc.tile_pool(name="fin", bufs=4))
        terms, gates, gains, shifts, gated_gains, factors, turned = {}, {}, {}, {}, {}, {}, {}

        def exponentials(blk):
            if blk < BLOCKS:
                terms[blk] = wide.tile([P, LS, BLOCK], F32, name="terms")
                nc.scalar.activation(out=terms[blk][:], in_=z1s[blk][:], func=ACT.Exp, bias=minus_one_col[:], scale=1.0)

        def gate_and_gain(blk):
            if blk < BLOCKS:
                gates[blk] = late.tile([P, BLOCK], F32, name="gate")
                eps_ps = subnet(EPS, codes_of[blk], scales_of[blk])
                nc.scalar.activation(out=gates[blk][:], in_=eps_ps[:], func=ACT.Tanh, bias=half_eps_bias[:], scale=0.05)
                gains[blk] = side.tile([P, BLOCK], F32, name="gain")
                alpha_ps = subnet(ALPHA, codes_of[blk], scales_of[blk])
                nc.scalar.activation(out=gains[blk][:], in_=alpha_ps[:], func=ACT.Exp, bias=alpha_bias[:], scale=0.1)

        def shift_and_denominator(blk):
            if blk < BLOCKS:
                shifts[blk] = late.tile([P, BLOCK], F32, name="shift")
                bias2_ps = subnet(BIAS2, codes_of[blk], scales_of[blk])
                nc.scalar.activation(out=shifts[blk][:], in_=bias2_ps[:], func=ACT.Identity, bias=bias_of(BIAS2), scale=1.0)
                if blk < BLOCKS - DEF:
                    scaled_reciprocal(blk)

        def scaled_reciprocal(blk):
            nc.scalar.activation(
                out=ln_den[:, block_cols(blk)], in_=ln_den[:, block_cols(blk)], func=ACT.Exp, bias=ln_04_col[:], scale=-1.0
            )

        def gate_gain(blk):
            if blk < BLOCKS:
                gated_gains[blk] = late.tile([P, BLOCK], F32, name="gated_gain")
                nc.vector.scalar_tensor_tensor(
                    out=gated_gains[blk][:], in0=gates[blk][:], scalar=1.0, in1=gains[blk][:], op0=ALU.add, op1=ALU.mult
                )
                engine = nc.vector if blk == 1 else nc.gpsimd
                w = GW if LO <= blk - 2 < HI else BLOCK
                engine.tensor_tensor(out=gates[blk][:, 0:w], in0=gains[blk][:, 0:w], in1=x_ts[blk][:, 0:w], op=ALU.mult)

        def gain_x_rest(blk):
            if blk < BLOCKS and LO <= blk - 2 < HI:
                nc.vector.tensor_tensor(out=gates[blk][:, GW:BLOCK], in0=gains[blk][:, GW:BLOCK], in1=x_ts[blk][:, GW:BLOCK], op=ALU.mult)

        def elu_plus_1(blk, cols):
            if blk < BLOCKS:
                nc.vector.scalar_tensor_tensor(
                    out=terms[blk][:, :, cols], in0=z1s[blk][:, :, cols], scalar=1.0, in1=terms[blk][:, :, cols], op0=ALU.max, op1=ALU.min
                )

        def times_mat2_again(blk, cols):
            if blk < BLOCKS:
                nc.vector.scalar_tensor_tensor(
                    out=terms[blk][:, :, cols], in0=terms[blk][:, :, cols], scalar=-1.0, in1=mat2s[blk][:, :, cols], op0=ALU.add, op1=ALU.mult
                )

        def turn_factor(blk):
            if blk < BLOCKS:
                turned[(blk, 0)] = turned_sum([gated_gains[blk][:]])

        def turn_sums(blk):
            if blk >= 0:
                turned[(blk, 1)] = turned_sum([terms[blk][:, l, :] for l in range(LS)])
                if not LO <= blk < HI:
                    turned[(blk, 2)] = turned_sum([shifts[blk][:], gates[blk][:]])

        def store(blk):
            total = banks["tr"].tile([P, BLOCK], F32, tag="mm")
            for s in range(SUBS):
                sub = slice(s * P, (s + 1) * P)
                nc.tensor.matmul(out=total[:, sub], lhsT=shifts[blk][:, sub], rhs=ident_f32[:], start=True, stop=False, is_transpose=True)
                nc.tensor.matmul(out=total[:, sub], lhsT=gates[blk][:, sub], rhs=ident_f32[:], start=False, stop=False, is_transpose=True)
                nc.tensor.matmul(out=total[:, sub], lhsT=ident_f32[:], rhs=factors[blk][:, sub], start=False, stop=True)
            result = fin.tile([P, SUBS, DIM], F32, name="result")
            nc.scalar.copy(out=result[:].rearrange("p s d -> p (s d)"), in_=total[:])
            nc.sync.dma_start(out=out_view[:, blk * SUBS : (blk + 1) * SUBS, :], in_=result[:])

        def finish(blk, stage):
            if 0 <= blk < BLOCKS:
                if stage == 0:
                    factors[blk] = fin.tile([P, BLOCK], F32, name="factor")
                    nc.vector.tensor_tensor(out=factors[blk][:], in0=turned[(blk, 0)][:], in1=ln_den[:, block_cols(blk)], op=ALU.mult)
                if stage == 1:
                    nc.vector.tensor_tensor(out=factors[blk][:], in0=turned[(blk, 1)][:], in1=factors[blk][:], op=ALU.mult)
                if stage == 2 and not LO <= blk < HI:
                    parts = 2 if blk == BLOCKS - 1 else 1
                    result = fin.tile([P, SUBS, DIM], F32, name="result")
                    for part in range(parts):
                        subs = slice(part * SUBS // parts, (part + 1) * SUBS // parts)
                        cols = slice(part * BLOCK // parts, (part + 1) * BLOCK // parts)
                        nc.vector.tensor_tensor(
                            out=result[:, subs, :].rearrange("p s d -> p (s d)"), in0=turned[(blk, 2)][:, cols], in1=factors[blk][:, cols], op=ALU.add
                        )
                        nc.sync.dma_start(out=out_view[:, blk * SUBS + subs.start : blk * SUBS + subs.stop, :], in_=result[:, subs, :])

        first_half, second_half = slice(0, BLOCK // 2), slice(BLOCK // 2, BLOCK)
        gate_and_gain(0)
        exponentials(0)
        shift_and_denominator(0)
        arguments(BLOCKS - 1, (0,))
        gate_gain(0)
        arguments(BLOCKS - 1, (1, 2))
        turn_factor(0)
        for step in range(BLOCKS + 1):
            if LO <= step - 1 - LAG < HI:
                store(step - 1 - LAG)
            gate_and_gain(step + 1)
            exponentials(step + 1)
            shift_and_denominator(step + 1)
            for lb in range(BLOCKS - DEF, BLOCKS):
                if CL[lb] == step:
                    clamp(lb)
            for lb in range(BLOCKS - DEF, BLOCKS):
                if LG[lb] == step:
                    log_denominator(lb)
            for lb in range(BLOCKS - DEF, BLOCKS):
                if RC[lb] == step:
                    scaled_reciprocal(lb)
            turn_sums(step - 1)
            if step > 0:
                turn_factor(step)
            elu_plus_1(step, first_half)
            elu_plus_1(step, second_half)
            times_mat2_again(step, first_half)
            times_mat2_again(step, second_half)
            gate_gain(step + 1)
            finish(step - 1, 1)
            finish(step, 0)
            finish(step - 1, 2)
            gain_x_rest(step + 1)
